import numpy as np
import ml_dtypes


def mxq(x, axis, fmt="e4m3"):
    dtype, down = {"e4m3": (ml_dtypes.float8_e4m3fn, 7), "e5m2": (ml_dtypes.float8_e5m2, 14)}[fmt]
    v = np.moveaxis(np.asarray(x, np.float32).astype(ml_dtypes.bfloat16).astype(np.float64), axis, -1)
    blocks = v.reshape(v.shape[:-1] + (-1, 32))
    amax = np.abs(blocks).max(-1, keepdims=True)
    byte = np.maximum(np.where(amax > 0, np.frexp(amax)[1] - 1 + 127, 0) - down, 1)
    scale = np.exp2(byte - 127.0)
    codes = (blocks / scale).astype(np.float32).astype(dtype).astype(np.float64)
    return np.moveaxis((codes * scale).reshape(v.shape), -1, axis)


WIDE = False


def mx_kscale(k):
    if not WIDE:
        return np.ones(k)
    levels = np.array([10, -10, 5, -5, 0])
    a = np.random.permutation(np.resize(levels, k // 512 * 4)).reshape(k // 512, 4)
    idx = np.arange(k)
    return np.exp2(a[idx // 512, idx % 128 // 32])


BF16 = ml_dtypes.bfloat16


def bf(x):
    return np.asarray(x, np.float32).astype(BF16)


def f64(x):
    return np.asarray(x).astype(np.float64)


B, N, C, H, D = 1, 2048, 512, 16, 32
EPS = 1e-12
SCALE = float(D) ** 0.25
VG = 4.0


def normalize(t):
    n = np.sqrt((t * t).sum(-1, keepdims=True))
    return t / np.maximum(n, EPS)


def heads(t):
    return t.reshape(B, N, H, D).transpose(0, 2, 1, 3)


def setup_inputs():
    s = mx_kscale(C)
    return {'x': bf(np.random.standard_normal((B, N, C)) * s),
            'Wk': bf(np.random.standard_normal((H * D, C)) / np.sqrt(C) / s),
            'bk': bf(np.random.standard_normal(H * D) * 0.1),
            'Wv': bf(np.random.standard_normal((H * D, C)) * VG / np.sqrt(C) / s),
            'bv': bf(np.random.standard_normal(H * D) * 0.1)}


def reference(x, Wk, bk, Wv, bv):
    xq = mxq(f64(x), 2, 'e4m3')
    k = heads((xq @ mxq(f64(Wk), 1, 'e4m3').T) + f64(bk))
    v = heads((xq @ mxq(f64(Wv), 1, 'e4m3').T) + f64(bv))
    kn = normalize(k) * SCALE
    vN = v / N
    kk = (kn[..., :, None] * kn[..., None, :]).reshape(B, H, N, D * D)
    vq = mxq(vN, 2, 'e4m3')
    mod_v = mxq(kk, 2, 'e4m3').transpose(0, 1, 3, 2) @ vq
    mod_n = kk.sum(2) / N
    kv_mod = np.concatenate([mod_n[..., None], mod_v], axis=-1).reshape(B, H, D, D, D + 1)
    kv_v = mxq(kn, 2, 'e4m3').transpose(0, 1, 3, 2) @ vq
    kv_n = kn.sum(2) / N
    kv = np.concatenate([kv_n[..., None], kv_v], axis=-1)
    vsum = np.concatenate([np.ones((B, H, 1)), vN.sum(2)], axis=-1)[:, :, None, :]
    return kv_mod, kv, vsum

@@ -1,0 +1,358 @@
+from contextlib import ExitStack
+
+import concourse.masks as masks
+import concourse.mybir as mybir
+
+F32 = mybir.dt.float32
+BF16 = mybir.dt.bfloat16
+U32 = mybir.dt.uint32
+U8 = mybir.dt.uint8
+FP8X4 = mybir.dt.float8_e4m3fn_x4
+ACT = mybir.ActivationFunctionType
+ALU = mybir.AluOpType
+
+P = 128
+PACK = 4
+K_PASS = P * PACK
+TOKENS = 2048
+CHANNELS = 512
+HEADS = 16
+DIM = 32
+OUT_DIM = DIM + 1
+EPS = 1e-12
+SCALE = float(DIM) ** 0.25
+
+GROUP_HEADS = P // DIM
+GROUPS = HEADS // GROUP_HEADS
+BLOCKS = TOKENS // K_PASS
+STEPS = GROUPS * BLOCKS
+SHIFTS = DIM // 2
+CHUNK = 4
+CHUNKS = SHIFTS // CHUNK
+WRAPPED = DIM + SHIFTS
+GRAM_COLS = P + 2
+BAND = 2 * DIM + 1
+
+FLOPS = 2 * TOKENS * CHANNELS * 2 * HEADS * DIM + 2 * TOKENS * HEADS * (DIM * DIM * DIM + DIM * DIM)
+
+
+def tile_taylorsoftmaxattention_pa_kernel(tc, x, Wk, bk, Wv, bv, out_0, out_1, out_2):
+    nc = tc.nc
+
+    x_rows = x.rearrange("b (j p) c -> p (b j) c", p=P)
+    wk_rows = Wk.rearrange("(g p) c -> p g c", p=P)
+    wv_rows = Wv.rearrange("(g p) c -> p g c", p=P)
+    kv_mod_rows = out_0.rearrange("b (g h) a w e -> (b g) (h a) (w e)", g=GROUPS)
+    kv_rows = out_1.rearrange("b (g h) d e -> (h d) (b g) e", g=GROUPS)
+    vsum_rows = out_2.rearrange("b (g h) o e -> (h o) (b g) e", g=GROUPS)
+
+    with ExitStack() as ctx:
+        keep = ctx.enter_context(tc.tile_pool(name="keep", bufs=1))
+        prep = ctx.enter_context(tc.tile_pool(name="prep", bufs=2))
+        prod = ctx.enter_context(tc.tile_pool(name="prod", bufs=3))
+        done = ctx.enter_context(tc.tile_pool(name="done", bufs=2))
+        psum_acc = ctx.enter_context(tc.psum_pool(name="psum_acc", bufs=1))
+        psum_gram = ctx.enter_context(tc.psum_pool(name="psum_gram", bufs=1))
+        psum_work = ctx.enter_context(tc.psum_pool(name="psum_work", bufs=2))
+
+        bias_rows = keep.tile([2 * GROUPS, P], BF16)
+        nc.sync.dma_start(out=bias_rows[0:GROUPS, :], in_=bk.rearrange("(g f) -> g f", g=GROUPS))
+        nc.sync.dma_start(out=bias_rows[GROUPS : 2 * GROUPS, :], in_=bv.rearrange("(g f) -> g f", g=GROUPS))
+        w_raw = keep.tile([P, GROUPS, 2, CHANNELS], BF16)
+        x_raw = keep.tile([P, TOKENS // P, CHANNELS], BF16)
+        nc.sync.dma_start(out=w_raw[:, 0, 0, :], in_=wk_rows[:, 0, :])
+        nc.sync.dma_start(out=w_raw[:, 0, 1, :], in_=wv_rows[:, 0, :])
+        for c in range(BLOCKS):
+            nc.sync.dma_start(out=x_raw[:, PACK * c : PACK * (c + 1), :], in_=x_rows[:, PACK * c : PACK * (c + 1), :])
+        nc.sync.dma_start(out=w_raw[:, 1:GROUPS, 0, :], in_=wk_rows[:, 1:GROUPS, :])
+        nc.sync.dma_start(out=w_raw[:, 1:GROUPS, 1, :], in_=wv_rows[:, 1:GROUPS, :])
+        w_words = w_raw[:].bitcast(F32)
+        x_words = x_raw[:].bitcast(F32)
+
+        ident = keep.tile([P, P], F32)
+        masks.make_identity(nc, ident[:])
+        one = keep.tile([P, 1], F32)
+        nc.vector.memset(one[:], 1.0)
+        table_warm = keep.tile([P, 1], F32)
+        nc.scalar.activation(out=table_warm[:], in_=one[:], func=ACT.Sqrt)
+
+        x_codes = keep.tile([P, TOKENS], U32, align_bytes=64)
+        x_scales = keep.tile([P, TOKENS], U8, align_bytes=64)
+        w_codes = keep.tile([P, GROUPS, 2 * P], U32, align_bytes=64)
+        w_scales = keep.tile([P, GROUPS, 2 * P], U8, align_bytes=64)
+
+        kn_rows = keep.tile([P, PACK, GRAM_COLS], F32)
+        nc.vector.memset(kn_rows[:], 1.0)
+        band = keep.tile([P, DIM * BAND], F32)
+        nc.vector.memset(band[:], 0.0)
+        by_shift = band[:].rearrange("p (a w) -> p a w", w=BAND)
+        square = band[:, 0 : DIM * 2 * DIM].rearrange("p (a w) -> p a w", w=2 * DIM)
+        small = keep.tile([P, GROUPS, 2, DIM], F32, align_bytes=64)
+        nc.vector.memset(small[:], 0.0)
+        small_turned = keep.tile([P, GROUPS, 2, DIM], F32, align_bytes=64)
+        kv_stage = keep.tile([P, GROUPS, OUT_DIM], F32)
+        vsum_stage = keep.tile([P, GROUPS, OUT_DIM], F32)
+        nc.vector.memset(vsum_stage[:], 1.0)
+
+        bias_square = keep.tile([P, P], F32)
+        nc.vector.memset(bias_square[:], 0.0)
+        nc.vector.tensor_copy(out=bias_square[0 : 2 * GROUPS, :], in_=bias_rows[:])
+        bias_turned = psum_work.tile([P, P], F32, tag="work")
+        nc.tensor.transpose(out=bias_turned[:], in_=bias_square[:], identity=ident[:])
+        bias_cols = keep.tile([P, 2 * GROUPS], F32)
+        nc.scalar.copy(out=bias_cols[:, 0:GROUPS], in_=bias_turned[:, 0:GROUPS])
+        nc.scalar.mul(out=bias_cols[:, GROUPS : 2 * GROUPS], in_=bias_turned[:, GROUPS : 2 * GROUPS], mul=1.0 / TOKENS)
+
+        w_grouped = {}
+        k_tok, v_tok, norm = {}, {}, {}
+        kn_wrapped, first_bf, v_bf, v_codes, v_scales = {}, {}, {}, {}, {}
+        products = {}
+        acc, gram, v_sums, stage = {}, {}, {}, {}
+
+        def turn_weights(g):
+            turned = psum_work.tile([P, 2, 2, P], F32, tag="work")
+            for m in range(2):
+                for u in range(2):
+                    nc.tensor.transpose(out=turned[:, m, u, :], in_=w_words[:, g, m, u * P : (u + 1) * P], identity=ident[:])
+            w_grouped[g] = prep.tile([P, 2, P, PACK], BF16, name="w_grouped", align_bytes=64)
+            nc.scalar.copy(out=w_grouped[g][:].bitcast(F32), in_=turned[:].rearrange("p m u o -> p m o u"))
+
+        def quantise_weights(g):
+            nc.vector.quantize_mx(
+                out=w_codes[:, g, :].bitcast(FP8X4),
+                scales=w_scales[:, g, :],
+                in_=w_grouped[g][:].rearrange("p m o k -> p (m o k)"),
+            )
+
+        def prepare_tokens(c):
+            x_grouped = prep.tile([P, K_PASS, PACK], BF16, align_bytes=64)
+            pairs = x_grouped[:].bitcast(F32).rearrange("p (j n) u -> p j n u", j=PACK)
+            for half in range(2):
+                turned = psum_acc.tile([P, 2, 2, P], F32, name="x_turned", tag="acc%d" % ((2 * c + half) % CHUNKS))
+                for j in range(2):
+                    for u in range(2):
+                        nc.tensor.transpose(
+                            out=turned[:, j, u, :],
+                            in_=x_words[:, PACK * c + 2 * half + j, u * P : (u + 1) * P],
+                            identity=ident[:],
+                        )
+                nc.vector.tensor_copy(out=pairs[:, 2 * half : 2 * half + 2, :, :], in_=turned[:].rearrange("p j u n -> p j n u"))
+            block = slice(c * K_PASS, (c + 1) * K_PASS)
+            nc.vector.quantize_mx(
+                out=x_codes[:, block].bitcast(FP8X4),
+                scales=x_scales[:, block],
+                in_=x_grouped[:].rearrange("p n k -> p (n k)"),
+            )
+
+        def project(step):
+            g, c = divmod(step, BLOCKS)
+            block = slice(c * K_PASS, (c + 1) * K_PASS)
+            if c == 0:
+                v_sums[g] = prep.tile([P, BLOCKS], F32, name="v_sums")
+            feat = []
+            for m in range(2):
+                sums = psum_work.tile([P, K_PASS], F32, name="proj", tag="work")
+                nc.tensor.matmul_mx(
+                    out=sums[:],
+                    lhsT=w_codes[:, g, m * P : (m + 1) * P].bitcast(FP8X4),
+                    lhsT_scale=w_scales[:, g, m * P : (m + 1) * P],
+                    rhs=x_codes[:, block].bitcast(FP8X4),
+                    rhs_scale=x_scales[:, block],
+                    start=True,
+                    stop=True,
+                )
+                feat.append(sums)
+            k_feat = prep.tile([P, K_PASS], F32)
+            nc.scalar.activation(out=k_feat[:], in_=feat[0][:], func=ACT.Identity, bias=bias_cols[:, g : g + 1], scale=1.0)
+            v_feat = prep.tile([P, K_PASS], F32)
+            nc.scalar.activation(
+                out=v_feat[:],
+                in_=feat[1][:],
+                func=ACT.Identity,
+                bias=bias_cols[:, GROUPS + g : GROUPS + g + 1],
+                scale=1.0 / TOKENS,
+                accum_out=v_sums[g][:, c : c + 1],
+            )
+            k_tok[step] = psum_work.tile([P, PACK, P], F32, name="k_tok", tag="work")
+            v_tok[step] = psum_work.tile([P, PACK, P], F32, name="v_tok", tag="work")
+            for t in range(PACK):
+                nc.tensor.transpose(out=k_tok[step][:, t, :], in_=k_feat[:, t * P : (t + 1) * P], identity=ident[:])
+            for t in range(PACK):
+                nc.tensor.transpose(out=v_tok[step][:, t, :], in_=v_feat[:, t * P : (t + 1) * P], identity=ident[:])
+            squares = prep.tile([P, DIM], F32)
+            square_sums = prep.tile([P, PACK * GROUP_HEADS], F32)
+            for t in range(PACK):
+                for h in range(GROUP_HEADS):
+                    nc.scalar.activation(
+                        out=squares[:],
+                        in_=k_tok[step][:, t, h * DIM : (h + 1) * DIM],
+                        func=ACT.Square,
+                        accum_out=square_sums[:, t * GROUP_HEADS + h : t * GROUP_HEADS + h + 1],
+                    )
+            norm[step] = prep.tile([P, PACK * GROUP_HEADS], F32, name="norm")
+            nc.scalar.activation(out=norm[step][:], in_=square_sums[:], func=ACT.Sqrt)
+
+        def normalise(step):
+            g, c = divmod(step, BLOCKS)
+            divisor = prep.tile([P, PACK * GROUP_HEADS], F32)
+            nc.vector.tensor_scalar(out=divisor[:], in0=norm[step][:], scalar1=EPS, scalar2=1.0 / SCALE, op0=ALU.max, op1=ALU.mult)
+            factor = prep.tile([P, PACK * GROUP_HEADS], F32)
+            nc.vector.reciprocal(out=factor[:], in_=divisor[:])
+            v_bf[step] = prep.tile([P, P, PACK], BF16, name="v_bf", align_bytes=64)
+            nc.scalar.copy(out=v_bf[step][:], in_=v_tok[step][:].rearrange("p t f -> p f t"))
+            for t in range(PACK):
+                for h in range(GROUP_HEADS):
+                    nc.scalar.activation(
+                        out=kn_rows[:, t, h * DIM : (h + 1) * DIM],
+                        in_=k_tok[step][:, t, h * DIM : (h + 1) * DIM],
+                        func=ACT.Copy,
+                        scale=factor[:, t * GROUP_HEADS + h : t * GROUP_HEADS + h + 1],
+                    )
+            if c == 0:
+                gram[g] = psum_gram.tile([P, GRAM_COLS], F32, name="gram")
+            for t in range(PACK):
+                nc.tensor.matmul(
+                    out=gram[g][:],
+                    lhsT=kn_rows[:, t, 0:P],
+                    rhs=kn_rows[:, t, :],
+                    start=(c == 0 and t == 0),
+                    stop=(c == BLOCKS - 1 and t == PACK - 1),
+                )
+            wrapped = prep.tile([P, GROUP_HEADS, WRAPPED, PACK], F32, name="kn_wrapped")
+            kn_wrapped[step] = wrapped
+            nc.scalar.copy(out=wrapped[:, :, 0:DIM, :], in_=kn_rows[:, :, 0:P].rearrange("p t (h d) -> p h d t", h=GROUP_HEADS))
+            nc.scalar.copy(out=wrapped[:, :, DIM:WRAPPED, :], in_=wrapped[:, :, 0:SHIFTS, :])
+            first_bf[step] = prep.tile([P, 2, P, PACK], BF16, name="first_bf", align_bytes=64)
+            nc.scalar.copy(
+                out=first_bf[step][:, 0, :, :].rearrange("p (h d) t -> p h d t", h=GROUP_HEADS), in_=wrapped[:, :, 0:DIM, :]
+            )
+            nc.scalar.activation(
+                out=first_bf[step][:, 1, :, :].rearrange("p (h d) t -> p h d t", h=GROUP_HEADS),
+                in_=wrapped[:, :, 0:DIM, :],
+                func=ACT.Square,
+            )
+            if c == BLOCKS - 1:
+                stage[g] = done.tile([P, DIM, OUT_DIM], F32, name="stage")
+                for h in range(GROUP_HEADS):
+                    rows = slice(h * DIM, (h + 1) * DIM)
+                    nc.scalar.mul(out=stage[g][rows, :, 0], in_=gram[g][rows, h * DIM : (h + 1) * DIM], mul=1.0 / TOKENS)
+                nc.scalar.mul(out=kv_stage[:, g, 0:1], in_=gram[g][:, P : P + 1], mul=1.0 / TOKENS)
+
+        def accumulate(step, name, bank_tag, codes, scales, width):
+            g, c = divmod(step, BLOCKS)
+            if c == 0:
+                acc[name] = psum_acc.tile([P, width], F32, name="acc", tag=bank_tag)
+            nc.tensor.matmul_mx(
+                out=acc[name][:],
+                lhsT=v_codes[step][:].bitcast(FP8X4),
+                lhsT_scale=v_scales[step][:],
+                rhs=codes[:].bitcast(FP8X4),
+                rhs_scale=scales[:],
+                start=(c == 0),
+                stop=(c == BLOCKS - 1),
+            )
+
+        def first_columns(step):
+            v_codes[step] = prod.tile([P, P], U32, name="v_codes", align_bytes=64)
+            v_scales[step] = prod.tile([P, P], U8, name="v_scales", align_bytes=64)
+            nc.vector.quantize_mx(
+                out=v_codes[step][:].bitcast(FP8X4), scales=v_scales[step][:], in_=v_bf[step][:].rearrange("p f t -> p (f t)")
+            )
+            codes = prod.tile([P, 2 * P], U32, name="first_codes", align_bytes=64)
+            scales = prod.tile([P, 2 * P], U8, name="first_scales", align_bytes=64)
+            nc.vector.quantize_mx(
+                out=codes[:].bitcast(FP8X4), scales=scales[:], in_=first_bf[step][:].rearrange("p s f t -> p (s f t)")
+            )
+            accumulate(step, CHUNKS, "acc%d" % CHUNKS, codes, scales, 2 * P)
+
+        def multiply(step, chunk):
+            kn = kn_wrapped[step]
+            kk = prod.tile([P, CHUNK, P, PACK], BF16, name="kk", align_bytes=64)
+            products[(step, chunk)] = kk
+            for q in range(CHUNK):
+                shift = chunk * CHUNK + q + 1
+                nc.vector.tensor_tensor(
+                    out=kk[:, q, :, :].rearrange("p (h i) t -> p h i t", h=GROUP_HEADS),
+                    in0=kn[:, :, 0:DIM, :],
+                    in1=kn[:, :, shift : shift + DIM, :],
+                    op=ALU.mult,
+                )
+
+        def contract(step, chunk):
+            codes = prod.tile([P, CHUNK * P], U32, name="kk_codes", align_bytes=64)
+            scales = prod.tile([P, CHUNK * P], U8, name="kk_scales", align_bytes=64)
+            nc.vector.quantize_mx(
+                out=codes[:].bitcast(FP8X4), scales=scales[:], in_=products[(step, chunk)][:].rearrange("p s f t -> p (s f t)")
+            )
+            accumulate(step, chunk, "acc%d" % chunk, codes, scales, CHUNK * P)
+
+        def collect(g):
+            by_pair = done.tile([P, SHIFTS + 1, DIM], F32)
+            first = acc[CHUNKS][:].rearrange("p (s m i) -> p s m i", s=2, m=GROUP_HEADS)
+            for h in range(GROUP_HEADS):
+                rows = slice(h * DIM, (h + 1) * DIM)
+                nc.scalar.copy(out=small[rows, g, 0, :], in_=first[rows, 0, h, :])
+                nc.scalar.mul(out=by_pair[rows, 0, :], in_=first[rows, 1, h, :], mul=0.5)
+                for chunk in range(CHUNKS):
+                    sums = acc[chunk][:].rearrange("p (s m i) -> p s m i", s=CHUNK, m=GROUP_HEADS)
+                    nc.scalar.copy(out=by_pair[rows, chunk * CHUNK + 1 : (chunk + 1) * CHUNK + 1, :], in_=sums[rows, :, h, :])
+            nc.scalar.copy(out=by_shift[:, :, 0 : SHIFTS + 1], in_=by_pair[:].rearrange("p s a -> p a s"))
+            nc.scalar.copy(
+                out=by_shift[:, SHIFTS - 1 : DIM - 1, DIM + 2 : DIM + 1 + SHIFTS],
+                in_=by_pair[:, 1:SHIFTS, SHIFTS:DIM].rearrange("p s a -> p a s"),
+            )
+            total = done.tile([P, BLOCKS], F32)
+            nc.scalar.activation(out=total[:], in_=v_sums[g][:], func=ACT.Copy, accum_out=small[:, g, 1, 0:1])
+
+        def finish(g):
+            full = done.tile([P, DIM, DIM], F32, align_bytes=64)
+            nc.vector.tensor_tensor(
+                out=full[:], in0=square[:, :, 0:DIM], in1=square[:, :, 0:DIM].rearrange("p a b -> p b a"), op=ALU.add
+            )
+            turned = done.tile([P, DIM, DIM], F32, align_bytes=64)
+            nc.vector.transpose(out=turned[:].rearrange("p b e -> p (b e)"), in_=full[:].rearrange("p b a -> p (b a)"))
+            nc.scalar.copy(out=stage[g][:, :, 1:OUT_DIM], in_=turned[:])
+            nc.sync.dma_start(out=kv_mod_rows[g], in_=stage[g][:].rearrange("p w e -> p (w e)"))
+
+        turn_weights(0)
+        quantise_weights(0)
+        prepare_tokens(0)
+        project(0)
+        prepare_tokens(1)
+        normalise(0)
+        prepare_tokens(2)
+        prepare_tokens(3)
+        project(1)
+
+        waiting = []
+        for step in range(STEPS):
+            g, c = divmod(step, BLOCKS)
+            for chunk in range(CHUNKS):
+                multiply(step, chunk)
+                if waiting:
+                    contract(waiting[0], waiting[1])
+                waiting = [step, chunk]
+                if chunk == 0:
+                    if c == 0 and g > 0:
+                        collect(g - 1)
+                    first_columns(step)
+                    if step + 1 < STEPS:
+                        normalise(step + 1)
+                    if c == 1 and g + 1 < GROUPS:
+                        turn_weights(g + 1)
+                    if step + 2 < STEPS:
+                        project(step + 2)
+                if chunk == 2:
+                    if c == 0 and g > 0:
+                        finish(g - 1)
+                    if c == 1 and g + 1 < GROUPS:
+                        quantise_weights(g + 1)
+        contract(waiting[0], waiting[1])
+        collect(GROUPS - 1)
+        finish(GROUPS - 1)
+
+        nc.vector.transpose(out=small_turned[:].rearrange("p g s e -> p (g s e)"), in_=small[:].rearrange("p g s d -> p (g s d)"))
+        nc.scalar.copy(out=kv_stage[:, :, 1:OUT_DIM], in_=small_turned[:, :, 0, :])
+        nc.scalar.copy(out=vsum_stage[:, :, 1:OUT_DIM], in_=small_turned[:, :, 1, :])
+        nc.sync.dma_start(out=kv_rows, in_=kv_stage[:])
+        nc.sync.dma_start(out=vsum_rows, in_=vsum_stage[0:P:DIM, :, :])

@@ -54,6 +54,7 @@ def tile_taylorsoftmaxattention_pa_kernel(tc, x, Wk, bk, Wv, bv, out_0, out_1, o
         psum_acc = ctx.enter_context(tc.psum_pool(name="psum_acc", bufs=1))
         psum_gram = ctx.enter_context(tc.psum_pool(name="psum_gram", bufs=1))
         psum_work = ctx.enter_context(tc.psum_pool(name="psum_work", bufs=2))
+        ctx.enter_context(tc.manual_schedule())
 
         bias_rows = keep.tile([2 * GROUPS, P], BF16)
         nc.sync.dma_start(out=bias_rows[0:GROUPS, :], in_=bk.rearrange("(g f) -> g f", g=GROUPS))
@@ -74,7 +75,11 @@ def tile_taylorsoftmaxattention_pa_kernel(tc, x, Wk, bk, Wv, bv, out_0, out_1, o
         one = keep.tile([P, 1], F32)
         nc.vector.memset(one[:], 1.0)
         table_warm = keep.tile([P, 1], F32)
-        nc.scalar.activation(out=table_warm[:], in_=one[:], func=ACT.Sqrt)
+        nc.scalar.activation(out=table_warm[:], in_=one[:], func=ACT.Abs_reciprocal_sqrt)
+        minus_floor = keep.tile([P, 1], F32)
+        nc.vector.memset(minus_floor[:], -EPS * EPS)
+        scaled_floor = keep.tile([P, 1], F32)
+        nc.vector.memset(scaled_floor[:], EPS * EPS / (SCALE * SCALE))
 
         x_codes = keep.tile([P, TOKENS], U32, align_bytes=64)
         x_scales = keep.tile([P, TOKENS], U8, align_bytes=64)
@@ -104,10 +109,10 @@ def tile_taylorsoftmaxattention_pa_kernel(tc, x, Wk, bk, Wv, bv, out_0, out_1, o
         nc.scalar.mul(out=bias_cols[:, GROUPS : 2 * GROUPS], in_=bias_turned[:, GROUPS : 2 * GROUPS], mul=1.0 / TOKENS)
 
         w_grouped = {}
-        k_tok, v_tok, norm = {}, {}, {}
+        k_tok, v_tok, factor = {}, {}, {}
         kn_wrapped, first_bf, v_bf, v_codes, v_scales = {}, {}, {}, {}, {}
         products = {}
-        acc, gram, v_sums, stage = {}, {}, {}, {}
+        acc, gram, v_sums, stage, by_pair = {}, {}, {}, {}, {}
 
         def turn_weights(g):
             turned = psum_work.tile([P, 2, 2, P], F32, tag="work")
@@ -189,15 +194,19 @@ def tile_taylorsoftmaxattention_pa_kernel(tc, x, Wk, bk, Wv, bv, out_0, out_1, o
                         func=ACT.Square,
                         accum_out=square_sums[:, t * GROUP_HEADS + h : t * GROUP_HEADS + h + 1],
                     )
-            norm[step] = prep.tile([P, PACK * GROUP_HEADS], F32, name="norm")
-            nc.scalar.activation(out=norm[step][:], in_=square_sums[:], func=ACT.Sqrt)
+            above_floor = prep.tile([P, PACK * GROUP_HEADS], F32)
+            nc.scalar.activation(out=above_floor[:], in_=square_sums[:], func=ACT.Relu, bias=minus_floor[:], scale=1.0)
+            factor[step] = prep.tile([P, PACK * GROUP_HEADS], F32, name="factor")
+            nc.scalar.activation(
+                out=factor[step][:],
+                in_=above_floor[:],
+                func=ACT.Abs_reciprocal_sqrt,
+                bias=scaled_floor[:],
+                scale=1.0 / (SCALE * SCALE),
+            )
 
         def normalise(step):
             g, c = divmod(step, BLOCKS)
-            divisor = prep.tile([P, PACK * GROUP_HEADS], F32)
-            nc.vector.tensor_scalar(out=divisor[:], in0=norm[step][:], scalar1=EPS, scalar2=1.0 / SCALE, op0=ALU.max, op1=ALU.mult)
-            factor = prep.tile([P, PACK * GROUP_HEADS], F32)
-            nc.vector.reciprocal(out=factor[:], in_=divisor[:])
             v_bf[step] = prep.tile([P, P, PACK], BF16, name="v_bf", align_bytes=64)
             nc.scalar.copy(out=v_bf[step][:], in_=v_tok[step][:].rearrange("p t f -> p f t"))
             for t in range(PACK):
@@ -206,7 +215,7 @@ def tile_taylorsoftmaxattention_pa_kernel(tc, x, Wk, bk, Wv, bv, out_0, out_1, o
                         out=kn_rows[:, t, h * DIM : (h + 1) * DIM],
                         in_=k_tok[step][:, t, h * DIM : (h + 1) * DIM],
                         func=ACT.Copy,
-                        scale=factor[:, t * GROUP_HEADS + h : t * GROUP_HEADS + h + 1],
+                        scale=factor[step][:, t * GROUP_HEADS + h : t * GROUP_HEADS + h + 1],
                     )
             if c == 0:
                 gram[g] = psum_gram.tile([P, GRAM_COLS], F32, name="gram")
@@ -264,6 +273,16 @@ def tile_taylorsoftmaxattention_pa_kernel(tc, x, Wk, bk, Wv, bv, out_0, out_1, o
                 out=codes[:].bitcast(FP8X4), scales=scales[:], in_=first_bf[step][:].rearrange("p s f t -> p (s f t)")
             )
             accumulate(step, CHUNKS, "acc%d" % CHUNKS, codes, scales, 2 * P)
+            g, c = divmod(step, BLOCKS)
+            if c == BLOCKS - 1:
+                by_pair[g] = done.tile([P, SHIFTS + 1, DIM], F32, name="by_pair")
+                sums = acc[CHUNKS][:].rearrange("p (s m i) -> p s m i", s=2, m=GROUP_HEADS)
+                for h in range(GROUP_HEADS):
+                    rows = slice(h * DIM, (h + 1) * DIM)
+                    nc.scalar.copy(out=small[rows, g, 0, :], in_=sums[rows, 0, h, :])
+                    nc.scalar.mul(out=by_pair[g][rows, 0, :], in_=sums[rows, 1, h, :], mul=0.5)
+                total = done.tile([P, BLOCKS], F32)
+                nc.scalar.activation(out=total[:], in_=v_sums[g][:], func=ACT.Copy, accum_out=small[:, g, 1, 0:1])
 
         def multiply(step, chunk):
             kn = kn_wrapped[step]
@@ -285,24 +304,21 @@ def tile_taylorsoftmaxattention_pa_kernel(tc, x, Wk, bk, Wv, bv, out_0, out_1, o
                 out=codes[:].bitcast(FP8X4), scales=scales[:], in_=products[(step, chunk)][:].rearrange("p s f t -> p (s f t)")
             )
             accumulate(step, chunk, "acc%d" % chunk, codes, scales, CHUNK * P)
+            g, c = divmod(step, BLOCKS)
+            if c == BLOCKS - 1:
+                sums = acc[chunk][:].rearrange("p (s m i) -> p s m i", s=CHUNK, m=GROUP_HEADS)
+                for h in range(GROUP_HEADS):
+                    rows = slice(h * DIM, (h + 1) * DIM)
+                    nc.scalar.copy(out=by_pair[g][rows, chunk * CHUNK + 1 : (chunk + 1) * CHUNK + 1, :], in_=sums[rows, :, h, :])
+                if chunk == CHUNKS - 1:
+                    spread(g)
 
-        def collect(g):
-            by_pair = done.tile([P, SHIFTS + 1, DIM], F32)
-            first = acc[CHUNKS][:].rearrange("p (s m i) -> p s m i", s=2, m=GROUP_HEADS)
-            for h in range(GROUP_HEADS):
-                rows = slice(h * DIM, (h + 1) * DIM)
-                nc.scalar.copy(out=small[rows, g, 0, :], in_=first[rows, 0, h, :])
-                nc.scalar.mul(out=by_pair[rows, 0, :], in_=first[rows, 1, h, :], mul=0.5)
-                for chunk in range(CHUNKS):
-                    sums = acc[chunk][:].rearrange("p (s m i) -> p s m i", s=CHUNK, m=GROUP_HEADS)
-                    nc.scalar.copy(out=by_pair[rows, chunk * CHUNK + 1 : (chunk + 1) * CHUNK + 1, :], in_=sums[rows, :, h, :])
-            nc.scalar.copy(out=by_shift[:, :, 0 : SHIFTS + 1], in_=by_pair[:].rearrange("p s a -> p a s"))
+        def spread(g):
+            nc.scalar.copy(out=by_shift[:, :, 0 : SHIFTS + 1], in_=by_pair[g][:].rearrange("p s a -> p a s"))
             nc.scalar.copy(
                 out=by_shift[:, SHIFTS - 1 : DIM - 1, DIM + 2 : DIM + 1 + SHIFTS],
-                in_=by_pair[:, 1:SHIFTS, SHIFTS:DIM].rearrange("p s a -> p a s"),
+                in_=by_pair[g][:, 1:SHIFTS, SHIFTS:DIM].rearrange("p s a -> p a s"),
             )
-            total = done.tile([P, BLOCKS], F32)
-            nc.scalar.activation(out=total[:], in_=v_sums[g][:], func=ACT.Copy, accum_out=small[:, g, 1, 0:1])
 
         def finish(g):
             full = done.tile([P, DIM, DIM], F32, align_bytes=64)
@@ -318,10 +334,9 @@ def tile_taylorsoftmaxattention_pa_kernel(tc, x, Wk, bk, Wv, bv, out_0, out_1, o
         quantise_weights(0)
         prepare_tokens(0)
         project(0)
-        prepare_tokens(1)
+        for c in range(1, BLOCKS):
+            prepare_tokens(c)
         normalise(0)
-        prepare_tokens(2)
-        prepare_tokens(3)
         project(1)
 
         waiting = []
@@ -333,8 +348,6 @@ def tile_taylorsoftmaxattention_pa_kernel(tc, x, Wk, bk, Wv, bv, out_0, out_1, o
                     contract(waiting[0], waiting[1])
                 waiting = [step, chunk]
                 if chunk == 0:
-                    if c == 0 and g > 0:
-                        collect(g - 1)
                     first_columns(step)
                     if step + 1 < STEPS:
                         normalise(step + 1)
@@ -347,12 +360,11 @@ def tile_taylorsoftmaxattention_pa_kernel(tc, x, Wk, bk, Wv, bv, out_0, out_1, o
                         finish(g - 1)
                     if c == 1 and g + 1 < GROUPS:
                         quantise_weights(g + 1)
-        contract(waiting[0], waiting[1])
-        collect(GROUPS - 1)
-        finish(GROUPS - 1)
 
         nc.vector.transpose(out=small_turned[:].rearrange("p g s e -> p (g s e)"), in_=small[:].rearrange("p g s d -> p (g s d)"))
         nc.scalar.copy(out=kv_stage[:, :, 1:OUT_DIM], in_=small_turned[:, :, 0, :])
         nc.scalar.copy(out=vsum_stage[:, :, 1:OUT_DIM], in_=small_turned[:, :, 1, :])
         nc.sync.dma_start(out=kv_rows, in_=kv_stage[:])
         nc.sync.dma_start(out=vsum_rows, in_=vsum_stage[0:P:DIM, :, :])
+        contract(waiting[0], waiting[1])
+        finish(GROUPS - 1)

@@ -29,6 +29,7 @@ STEPS = GROUPS * BLOCKS
 SHIFTS = DIM // 2
 CHUNK = 4
 CHUNKS = SHIFTS // CHUNK
+WIDE = 8
 WRAPPED = DIM + SHIFTS
 GRAM_COLS = P + 2
 BAND = 2 * DIM + 1
@@ -49,7 +50,7 @@ def tile_taylorsoftmaxattention_pa_kernel(tc, x, Wk, bk, Wv, bv, out_0, out_1, o
     with ExitStack() as ctx:
         keep = ctx.enter_context(tc.tile_pool(name="keep", bufs=1))
         prep = ctx.enter_context(tc.tile_pool(name="prep", bufs=2))
-        prod = ctx.enter_context(tc.tile_pool(name="prod", bufs=3))
+        prod = ctx.enter_context(tc.tile_pool(name="prod", bufs=2))
         done = ctx.enter_context(tc.tile_pool(name="done", bufs=2))
         psum_acc = ctx.enter_context(tc.psum_pool(name="psum_acc", bufs=1))
         psum_gram = ctx.enter_context(tc.psum_pool(name="psum_gram", bufs=1))
@@ -110,8 +111,8 @@ def tile_taylorsoftmaxattention_pa_kernel(tc, x, Wk, bk, Wv, bv, out_0, out_1, o
 
         w_grouped = {}
         k_tok, v_tok, factor = {}, {}, {}
-        kn_wrapped, first_bf, v_bf, v_codes, v_scales = {}, {}, {}, {}, {}
-        products = {}
+        kn_wrapped, first_bf, v_bf, kk_bf = {}, {}, {}, {}
+        v_codes, v_scales, first_codes, first_scales, kk_codes, kk_scales = {}, {}, {}, {}, {}, {}
         acc, gram, v_sums, stage, by_pair = {}, {}, {}, {}, {}
 
         def turn_weights(g):
@@ -247,34 +248,58 @@ def tile_taylorsoftmaxattention_pa_kernel(tc, x, Wk, bk, Wv, bv, out_0, out_1, o
                     nc.scalar.mul(out=stage[g][rows, :, 0], in_=gram[g][rows, h * DIM : (h + 1) * DIM], mul=1.0 / TOKENS)
                 nc.scalar.mul(out=kv_stage[:, g, 0:1], in_=gram[g][:, P : P + 1], mul=1.0 / TOKENS)
 
-        def accumulate(step, name, bank_tag, codes, scales, width):
-            g, c = divmod(step, BLOCKS)
-            if c == 0:
-                acc[name] = psum_acc.tile([P, width], F32, name="acc", tag=bank_tag)
-            nc.tensor.matmul_mx(
-                out=acc[name][:],
-                lhsT=v_codes[step][:].bitcast(FP8X4),
-                lhsT_scale=v_scales[step][:],
-                rhs=codes[:].bitcast(FP8X4),
-                rhs_scale=scales[:],
-                start=(c == 0),
-                stop=(c == BLOCKS - 1),
-            )
+        def multiply(step):
+            kn = kn_wrapped[step]
+            kk_bf[step] = prod.tile([P, SHIFTS, P, PACK], BF16, name="kk_bf", align_bytes=64)
+            for shift in range(1, SHIFTS + 1):
+                nc.vector.tensor_tensor(
+                    out=kk_bf[step][:, shift - 1, :, :].rearrange("p (h i) t -> p h i t", h=GROUP_HEADS),
+                    in0=kn[:, :, 0:DIM, :],
+                    in1=kn[:, :, shift : shift + DIM, :],
+                    op=ALU.mult,
+                )
 
-        def first_columns(step):
+        def quantise(step):
             v_codes[step] = prod.tile([P, P], U32, name="v_codes", align_bytes=64)
             v_scales[step] = prod.tile([P, P], U8, name="v_scales", align_bytes=64)
             nc.vector.quantize_mx(
                 out=v_codes[step][:].bitcast(FP8X4), scales=v_scales[step][:], in_=v_bf[step][:].rearrange("p f t -> p (f t)")
             )
-            codes = prod.tile([P, 2 * P], U32, name="first_codes", align_bytes=64)
-            scales = prod.tile([P, 2 * P], U8, name="first_scales", align_bytes=64)
+            first_codes[step] = prod.tile([P, 2 * P], U32, name="first_codes", align_bytes=64)
+            first_scales[step] = prod.tile([P, 2 * P], U8, name="first_scales", align_bytes=64)
             nc.vector.quantize_mx(
-                out=codes[:].bitcast(FP8X4), scales=scales[:], in_=first_bf[step][:].rearrange("p s f t -> p (s f t)")
+                out=first_codes[step][:].bitcast(FP8X4),
+                scales=first_scales[step][:],
+                in_=first_bf[step][:].rearrange("p s f t -> p (s f t)"),
             )
-            accumulate(step, CHUNKS, "acc%d" % CHUNKS, codes, scales, 2 * P)
+            kk_codes[step] = prod.tile([P, SHIFTS * P], U32, name="kk_codes", align_bytes=64)
+            kk_scales[step] = prod.tile([P, SHIFTS * P], U8, name="kk_scales", align_bytes=64)
+            for w in range(SHIFTS // WIDE):
+                nc.vector.quantize_mx(
+                    out=kk_codes[step][:, w * WIDE * P : (w + 1) * WIDE * P].bitcast(FP8X4),
+                    scales=kk_scales[step][:, w * WIDE * P : (w + 1) * WIDE * P],
+                    in_=kk_bf[step][:, w * WIDE : (w + 1) * WIDE, :, :].rearrange("p s f t -> p (s f t)"),
+                )
+
+        def accumulate(step, bank, codes, scales, width):
             g, c = divmod(step, BLOCKS)
-            if c == BLOCKS - 1:
+            if c == 0:
+                acc[bank] = psum_acc.tile([P, width], F32, name="acc", tag="acc%d" % bank)
+            nc.tensor.matmul_mx(
+                out=acc[bank][:],
+                lhsT=v_codes[step][:].bitcast(FP8X4),
+                lhsT_scale=v_scales[step][:],
+                rhs=codes.bitcast(FP8X4),
+                rhs_scale=scales,
+                start=(c == 0),
+                stop=(c == BLOCKS - 1),
+            )
+
+        def contract(step):
+            g, c = divmod(step, BLOCKS)
+            last = c == BLOCKS - 1
+            accumulate(step, CHUNKS, first_codes[step][:], first_scales[step][:], 2 * P)
+            if last:
                 by_pair[g] = done.tile([P, SHIFTS + 1, DIM], F32, name="by_pair")
                 sums = acc[CHUNKS][:].rearrange("p (s m i) -> p s m i", s=2, m=GROUP_HEADS)
                 for h in range(GROUP_HEADS):
@@ -283,35 +308,16 @@ def tile_taylorsoftmaxattention_pa_kernel(tc, x, Wk, bk, Wv, bv, out_0, out_1, o
                     nc.scalar.mul(out=by_pair[g][rows, 0, :], in_=sums[rows, 1, h, :], mul=0.5)
                 total = done.tile([P, BLOCKS], F32)
                 nc.scalar.activation(out=total[:], in_=v_sums[g][:], func=ACT.Copy, accum_out=small[:, g, 1, 0:1])
-
-        def multiply(step, chunk):
-            kn = kn_wrapped[step]
-            kk = prod.tile([P, CHUNK, P, PACK], BF16, name="kk", align_bytes=64)
-            products[(step, chunk)] = kk
-            for q in range(CHUNK):
-                shift = chunk * CHUNK + q + 1
-                nc.vector.tensor_tensor(
-                    out=kk[:, q, :, :].rearrange("p (h i) t -> p h i t", h=GROUP_HEADS),
-                    in0=kn[:, :, 0:DIM, :],
-                    in1=kn[:, :, shift : shift + DIM, :],
-                    op=ALU.mult,
-                )
-
-        def contract(step, chunk):
-            codes = prod.tile([P, CHUNK * P], U32, name="kk_codes", align_bytes=64)
-            scales = prod.tile([P, CHUNK * P], U8, name="kk_scales", align_bytes=64)
-            nc.vector.quantize_mx(
-                out=codes[:].bitcast(FP8X4), scales=scales[:], in_=products[(step, chunk)][:].rearrange("p s f t -> p (s f t)")
-            )
-            accumulate(step, chunk, "acc%d" % chunk, codes, scales, CHUNK * P)
-            g, c = divmod(step, BLOCKS)
-            if c == BLOCKS - 1:
-                sums = acc[chunk][:].rearrange("p (s m i) -> p s m i", s=CHUNK, m=GROUP_HEADS)
-                for h in range(GROUP_HEADS):
-                    rows = slice(h * DIM, (h + 1) * DIM)
-                    nc.scalar.copy(out=by_pair[g][rows, chunk * CHUNK + 1 : (chunk + 1) * CHUNK + 1, :], in_=sums[rows, :, h, :])
-                if chunk == CHUNKS - 1:
-                    spread(g)
+            for chunk in range(CHUNKS):
+                columns = slice(chunk * CHUNK * P, (chunk + 1) * CHUNK * P)
+                accumulate(step, chunk, kk_codes[step][:, columns], kk_scales[step][:, columns], CHUNK * P)
+                if last:
+                    sums = acc[chunk][:].rearrange("p (s m i) -> p s m i", s=CHUNK, m=GROUP_HEADS)
+                    for h in range(GROUP_HEADS):
+                        rows = slice(h * DIM, (h + 1) * DIM)
+                        nc.scalar.copy(out=by_pair[g][rows, chunk * CHUNK + 1 : (chunk + 1) * CHUNK + 1, :], in_=sums[rows, :, h, :])
+            if last:
+                spread(g)
 
         def spread(g):
             nc.scalar.copy(out=by_shift[:, :, 0 : SHIFTS + 1], in_=by_pair[g][:].rearrange("p s a -> p a s"))
@@ -339,32 +345,25 @@ def tile_taylorsoftmaxattention_pa_kernel(tc, x, Wk, bk, Wv, bv, out_0, out_1, o
         normalise(0)
         project(1)
 
-        waiting = []
         for step in range(STEPS):
             g, c = divmod(step, BLOCKS)
-            for chunk in range(CHUNKS):
-                multiply(step, chunk)
-                if waiting:
-                    contract(waiting[0], waiting[1])
-                waiting = [step, chunk]
-                if chunk == 0:
-                    first_columns(step)
-                    if step + 1 < STEPS:
-                        normalise(step + 1)
-                    if c == 1 and g + 1 < GROUPS:
-                        turn_weights(g + 1)
-                    if step + 2 < STEPS:
-                        project(step + 2)
-                if chunk == 2:
-                    if c == 0 and g > 0:
-                        finish(g - 1)
-                    if c == 1 and g + 1 < GROUPS:
-                        quantise_weights(g + 1)
+            if step + 1 < STEPS:
+                normalise(step + 1)
+            if c == 1 and g + 1 < GROUPS:
+                turn_weights(g + 1)
+            if step + 2 < STEPS:
+                project(step + 2)
+            multiply(step)
+            quantise(step)
+            if c == 0 and g > 0:
+                finish(g - 1)
+            if c == 1 and g + 1 < GROUPS:
+                quantise_weights(g + 1)
+            contract(step)
+        finish(GROUPS - 1)
 
         nc.vector.transpose(out=small_turned[:].rearrange("p g s e -> p (g s e)"), in_=small[:].rearrange("p g s d -> p (g s d)"))
         nc.scalar.copy(out=kv_stage[:, :, 1:OUT_DIM], in_=small_turned[:, :, 0, :])
         nc.scalar.copy(out=vsum_stage[:, :, 1:OUT_DIM], in_=small_turned[:, :, 1, :])
         nc.sync.dma_start(out=kv_rows, in_=kv_stage[:])
         nc.sync.dma_start(out=vsum_rows, in_=vsum_stage[0:P:DIM, :, :])
-        contract(waiting[0], waiting[1])
-        finish(GROUPS - 1)

@@ -185,12 +185,12 @@ def tile_taylorsoftmaxattention_pa_kernel(tc, x, Wk, bk, Wv, bv, out_0, out_1, o
                 nc.tensor.transpose(out=k_tok[step][:, t, :], in_=k_feat[:, t * P : (t + 1) * P], identity=ident[:])
             for t in range(PACK):
                 nc.tensor.transpose(out=v_tok[step][:, t, :], in_=v_feat[:, t * P : (t + 1) * P], identity=ident[:])
-            squares = prep.tile([P, DIM], F32)
+            squares = prep.tile([P, PACK, P], F32)
             square_sums = prep.tile([P, PACK * GROUP_HEADS], F32)
             for t in range(PACK):
                 for h in range(GROUP_HEADS):
                     nc.scalar.activation(
-                        out=squares[:],
+                        out=squares[:, t, h * DIM : (h + 1) * DIM],
                         in_=k_tok[step][:, t, h * DIM : (h + 1) * DIM],
                         func=ACT.Square,
                         accum_out=square_sums[:, t * GROUP_HEADS + h : t * GROUP_HEADS + h + 1],

@@ -30,7 +30,8 @@ SHIFTS = DIM // 2
 CHUNK = 4
 CHUNKS = SHIFTS // CHUNK
 WIDE = 8
-WRAPPED = DIM + SHIFTS
+WRAPPED = DIM + SHIFTS - 1
+VECTOR_SHIFTS = 12
 GRAM_COLS = P + 2
 BAND = 2 * DIM + 1
 
@@ -54,7 +55,8 @@ def tile_taylorsoftmaxattention_pa_kernel(tc, x, Wk, bk, Wv, bv, out_0, out_1, o
         done = ctx.enter_context(tc.tile_pool(name="done", bufs=2))
         psum_acc = ctx.enter_context(tc.psum_pool(name="psum_acc", bufs=1))
         psum_gram = ctx.enter_context(tc.psum_pool(name="psum_gram", bufs=1))
-        psum_work = ctx.enter_context(tc.psum_pool(name="psum_work", bufs=2))
+        psum_k = ctx.enter_context(tc.psum_pool(name="psum_k", bufs=2))
+        psum_work = ctx.enter_context(tc.psum_pool(name="psum_work", bufs=1))
         ctx.enter_context(tc.manual_schedule())
 
         bias_rows = keep.tile([2 * GROUPS, P], BF16)
@@ -89,6 +91,10 @@ def tile_taylorsoftmaxattention_pa_kernel(tc, x, Wk, bk, Wv, bv, out_0, out_1, o
 
         kn_rows = keep.tile([P, PACK, GRAM_COLS], F32)
         nc.vector.memset(kn_rows[:], 1.0)
+        kk_bf = []
+        for parity in range(2):
+            kk_bf.append(keep.tile([P, SHIFTS, P, PACK], BF16, name="kk_bf%d" % parity, align_bytes=64))
+            nc.vector.memset(kk_bf[parity][:, SHIFTS - 1, :, :], 0.0)
         band = keep.tile([P, DIM * BAND], F32)
         nc.vector.memset(band[:], 0.0)
         by_shift = band[:].rearrange("p (a w) -> p a w", w=BAND)
@@ -110,8 +116,8 @@ def tile_taylorsoftmaxattention_pa_kernel(tc, x, Wk, bk, Wv, bv, out_0, out_1, o
         nc.scalar.mul(out=bias_cols[:, GROUPS : 2 * GROUPS], in_=bias_turned[:, GROUPS : 2 * GROUPS], mul=1.0 / TOKENS)
 
         w_grouped = {}
-        k_tok, v_tok, factor = {}, {}, {}
-        kn_wrapped, first_bf, v_bf, kk_bf = {}, {}, {}, {}
+        k_tok, factor, factor_squared = {}, {}, {}
+        k_packed, w_wrapped, first_bf, v_bf = {}, {}, {}, {}
         v_codes, v_scales, first_codes, first_scales, kk_codes, kk_scales = {}, {}, {}, {}, {}, {}
         acc, gram, v_sums, stage, by_pair = {}, {}, {}, {}, {}
 
@@ -150,14 +156,20 @@ def tile_taylorsoftmaxattention_pa_kernel(tc, x, Wk, bk, Wv, bv, out_0, out_1, o
                 in_=x_grouped[:].rearrange("p n k -> p (n k)"),
             )
 
+        def by_head(ap):
+            return ap.rearrange("p (h d) t -> p h d t", h=GROUP_HEADS)
+
+        def planes_by_head(ap):
+            return ap.rearrange("p t (h d) -> p h d t", h=GROUP_HEADS)
+
         def project(step):
             g, c = divmod(step, BLOCKS)
             block = slice(c * K_PASS, (c + 1) * K_PASS)
             if c == 0:
                 v_sums[g] = prep.tile([P, BLOCKS], F32, name="v_sums")
-            feat = []
-            for m in range(2):
-                sums = psum_work.tile([P, K_PASS], F32, name="proj", tag="work")
+            k_sums = psum_k.tile([P, K_PASS], F32, name="k_sums", tag="k")
+            v_sum_bank = psum_work.tile([P, K_PASS], F32, name="v_sum_bank", tag="work")
+            for m, sums in enumerate([k_sums, v_sum_bank]):
                 nc.tensor.matmul_mx(
                     out=sums[:],
                     lhsT=w_codes[:, g, m * P : (m + 1) * P].bitcast(FP8X4),
@@ -167,24 +179,23 @@ def tile_taylorsoftmaxattention_pa_kernel(tc, x, Wk, bk, Wv, bv, out_0, out_1, o
                     start=True,
                     stop=True,
                 )
-                feat.append(sums)
             k_feat = prep.tile([P, K_PASS], F32)
-            nc.scalar.activation(out=k_feat[:], in_=feat[0][:], func=ACT.Identity, bias=bias_cols[:, g : g + 1], scale=1.0)
+            nc.scalar.activation(out=k_feat[:], in_=k_sums[:], func=ACT.Identity, bias=bias_cols[:, g : g + 1], scale=1.0)
             v_feat = prep.tile([P, K_PASS], F32)
             nc.scalar.activation(
                 out=v_feat[:],
-                in_=feat[1][:],
+                in_=v_sum_bank[:],
                 func=ACT.Identity,
                 bias=bias_cols[:, GROUPS + g : GROUPS + g + 1],
                 scale=1.0 / TOKENS,
                 accum_out=v_sums[g][:, c : c + 1],
             )
-            k_tok[step] = psum_work.tile([P, PACK, P], F32, name="k_tok", tag="work")
-            v_tok[step] = psum_work.tile([P, PACK, P], F32, name="v_tok", tag="work")
+            k_tok[step] = psum_k.tile([P, PACK, P], F32, name="k_tok", tag="k")
+            v_tok = psum_work.tile([P, PACK, P], F32, name="v_tok", tag="work")
             for t in range(PACK):
                 nc.tensor.transpose(out=k_tok[step][:, t, :], in_=k_feat[:, t * P : (t + 1) * P], identity=ident[:])
             for t in range(PACK):
-                nc.tensor.transpose(out=v_tok[step][:, t, :], in_=v_feat[:, t * P : (t + 1) * P], identity=ident[:])
+                nc.tensor.transpose(out=v_tok[:, t, :], in_=v_feat[:, t * P : (t + 1) * P], identity=ident[:])
             squares = prep.tile([P, PACK, P], F32)
             square_sums = prep.tile([P, PACK * GROUP_HEADS], F32)
             for t in range(PACK):
@@ -197,6 +208,8 @@ def tile_taylorsoftmaxattention_pa_kernel(tc, x, Wk, bk, Wv, bv, out_0, out_1, o
                     )
             above_floor = prep.tile([P, PACK * GROUP_HEADS], F32)
             nc.scalar.activation(out=above_floor[:], in_=square_sums[:], func=ACT.Relu, bias=minus_floor[:], scale=1.0)
+            v_bf[step] = prep.tile([P, P, PACK], BF16, name="v_bf", align_bytes=64)
+            nc.scalar.copy(out=v_bf[step][:], in_=v_tok[:].rearrange("p t f -> p f t"))
             factor[step] = prep.tile([P, PACK * GROUP_HEADS], F32, name="factor")
             nc.scalar.activation(
                 out=factor[step][:],
@@ -205,11 +218,11 @@ def tile_taylorsoftmaxattention_pa_kernel(tc, x, Wk, bk, Wv, bv, out_0, out_1, o
                 bias=scaled_floor[:],
                 scale=1.0 / (SCALE * SCALE),
             )
+            factor_squared[step] = prep.tile([P, PACK * GROUP_HEADS], F32, name="factor_squared")
+            nc.scalar.activation(out=factor_squared[step][:], in_=factor[step][:], func=ACT.Square)
 
         def normalise(step):
             g, c = divmod(step, BLOCKS)
-            v_bf[step] = prep.tile([P, P, PACK], BF16, name="v_bf", align_bytes=64)
-            nc.scalar.copy(out=v_bf[step][:], in_=v_tok[step][:].rearrange("p t f -> p f t"))
             for t in range(PACK):
                 for h in range(GROUP_HEADS):
                     nc.scalar.activation(
@@ -228,18 +241,24 @@ def tile_taylorsoftmaxattention_pa_kernel(tc, x, Wk, bk, Wv, bv, out_0, out_1, o
                     start=(c == 0 and t == 0),
                     stop=(c == BLOCKS - 1 and t == PACK - 1),
                 )
-            wrapped = prep.tile([P, GROUP_HEADS, WRAPPED, PACK], F32, name="kn_wrapped")
-            kn_wrapped[step] = wrapped
-            nc.scalar.copy(out=wrapped[:, :, 0:DIM, :], in_=kn_rows[:, :, 0:P].rearrange("p t (h d) -> p h d t", h=GROUP_HEADS))
-            nc.scalar.copy(out=wrapped[:, :, DIM:WRAPPED, :], in_=wrapped[:, :, 0:SHIFTS, :])
+            k_packed[step] = prep.tile([P, GROUP_HEADS, DIM, PACK], F32, name="k_packed")
+            nc.scalar.copy(out=k_packed[step][:], in_=planes_by_head(k_tok[step][:]))
             first_bf[step] = prep.tile([P, 2, P, PACK], BF16, name="first_bf", align_bytes=64)
-            nc.scalar.copy(
-                out=first_bf[step][:, 0, :, :].rearrange("p (h d) t -> p h d t", h=GROUP_HEADS), in_=wrapped[:, :, 0:DIM, :]
+            nc.scalar.copy(out=by_head(first_bf[step][:, 0, :, :]), in_=planes_by_head(kn_rows[:, :, 0:P]))
+            per_head = factor_squared[step][:].rearrange("p (t h) -> p h t", h=GROUP_HEADS).unsqueeze(2)
+            w = prep.tile([P, GROUP_HEADS, WRAPPED, PACK], F32, name="w_wrapped")
+            w_wrapped[step] = w
+            nc.gpsimd.tensor_tensor(
+                out=w[:, :, 0:DIM, :],
+                in0=k_packed[step][:],
+                in1=per_head.to_broadcast([P, GROUP_HEADS, DIM, PACK]),
+                op=ALU.mult,
             )
-            nc.scalar.activation(
-                out=first_bf[step][:, 1, :, :].rearrange("p (h d) t -> p h d t", h=GROUP_HEADS),
-                in_=wrapped[:, :, 0:DIM, :],
-                func=ACT.Square,
+            nc.gpsimd.tensor_tensor(
+                out=w[:, :, DIM:WRAPPED, :],
+                in0=k_packed[step][:, :, 0 : WRAPPED - DIM, :],
+                in1=per_head.to_broadcast([P, GROUP_HEADS, WRAPPED - DIM, PACK]),
+                op=ALU.mult,
             )
             if c == BLOCKS - 1:
                 stage[g] = done.tile([P, DIM, OUT_DIM], F32, name="stage")
@@ -249,74 +268,87 @@ def tile_taylorsoftmaxattention_pa_kernel(tc, x, Wk, bk, Wv, bv, out_0, out_1, o
                 nc.scalar.mul(out=kv_stage[:, g, 0:1], in_=gram[g][:, P : P + 1], mul=1.0 / TOKENS)
 
         def multiply(step):
-            kn = kn_wrapped[step]
-            kk_bf[step] = prod.tile([P, SHIFTS, P, PACK], BF16, name="kk_bf", align_bytes=64)
+            w = w_wrapped[step]
             for shift in range(1, SHIFTS + 1):
-                nc.vector.tensor_tensor(
-                    out=kk_bf[step][:, shift - 1, :, :].rearrange("p (h i) t -> p h i t", h=GROUP_HEADS),
-                    in0=kn[:, :, 0:DIM, :],
-                    in1=kn[:, :, shift : shift + DIM, :],
-                    op=ALU.mult,
-                )
+                count = DIM if shift < SHIFTS else DIM - SHIFTS
+                out = by_head(kk_bf[step % 2][:, shift - 1, :, :])[:, :, 0:count, :]
+                if shift <= VECTOR_SHIFTS:
+                    nc.vector.tensor_tensor(
+                        out=out, in0=planes_by_head(k_tok[step][:])[:, :, 0:count, :], in1=w[:, :, shift : shift + count, :], op=ALU.mult
+                    )
+                else:
+                    nc.gpsimd.tensor_tensor(
+                        out=out, in0=k_packed[step][:, :, 0:count, :], in1=w[:, :, shift : shift + count, :], op=ALU.mult
+                    )
+            nc.gpsimd.tensor_tensor(out=by_head(first_bf[step][:, 1, :, :]), in0=k_packed[step][:], in1=w[:, :, 0:DIM, :], op=ALU.mult)
 
         def quantise(step):
-            v_codes[step] = prod.tile([P, P], U32, name="v_codes", align_bytes=64)
-            v_scales[step] = prod.tile([P, P], U8, name="v_scales", align_bytes=64)
+            g, c = divmod(step, BLOCKS)
+            if c == 0:
+                v_codes[g] = prod.tile([P, BLOCKS, P], U32, name="v_codes", align_bytes=64)
+                v_scales[g] = prod.tile([P, BLOCKS, P], U8, name="v_scales", align_bytes=64)
+                first_codes[g] = prod.tile([P, BLOCKS, 2 * P], U32, name="first_codes", align_bytes=64)
+                first_scales[g] = prod.tile([P, BLOCKS, 2 * P], U8, name="first_scales", align_bytes=64)
             nc.vector.quantize_mx(
-                out=v_codes[step][:].bitcast(FP8X4), scales=v_scales[step][:], in_=v_bf[step][:].rearrange("p f t -> p (f t)")
-            )
-            first_codes[step] = prod.tile([P, 2 * P], U32, name="first_codes", align_bytes=64)
-            first_scales[step] = prod.tile([P, 2 * P], U8, name="first_scales", align_bytes=64)
-            nc.vector.quantize_mx(
-                out=first_codes[step][:].bitcast(FP8X4),
-                scales=first_scales[step][:],
-                in_=first_bf[step][:].rearrange("p s f t -> p (s f t)"),
+                out=v_codes[g][:, c, :].bitcast(FP8X4), scales=v_scales[g][:, c, :], in_=v_bf[step][:].rearrange("p f t -> p (f t)")
             )
             kk_codes[step] = prod.tile([P, SHIFTS * P], U32, name="kk_codes", align_bytes=64)
             kk_scales[step] = prod.tile([P, SHIFTS * P], U8, name="kk_scales", align_bytes=64)
-            for w in range(SHIFTS // WIDE):
+            for half in range(SHIFTS // WIDE):
+                columns = slice(half * WIDE * P, (half + 1) * WIDE * P)
                 nc.vector.quantize_mx(
-                    out=kk_codes[step][:, w * WIDE * P : (w + 1) * WIDE * P].bitcast(FP8X4),
-                    scales=kk_scales[step][:, w * WIDE * P : (w + 1) * WIDE * P],
-                    in_=kk_bf[step][:, w * WIDE : (w + 1) * WIDE, :, :].rearrange("p s f t -> p (s f t)"),
+                    out=kk_codes[step][:, columns].bitcast(FP8X4),
+                    scales=kk_scales[step][:, columns],
+                    in_=kk_bf[step % 2][:, half * WIDE : (half + 1) * WIDE, :, :].rearrange("p s f t -> p (s f t)"),
                 )
-
-        def accumulate(step, bank, codes, scales, width):
-            g, c = divmod(step, BLOCKS)
-            if c == 0:
-                acc[bank] = psum_acc.tile([P, width], F32, name="acc", tag="acc%d" % bank)
-            nc.tensor.matmul_mx(
-                out=acc[bank][:],
-                lhsT=v_codes[step][:].bitcast(FP8X4),
-                lhsT_scale=v_scales[step][:],
-                rhs=codes.bitcast(FP8X4),
-                rhs_scale=scales,
-                start=(c == 0),
-                stop=(c == BLOCKS - 1),
+            nc.vector.quantize_mx(
+                out=first_codes[g][:, c, :].bitcast(FP8X4),
+                scales=first_scales[g][:, c, :],
+                in_=first_bf[step][:].rearrange("p s f t -> p (s f t)"),
             )
 
         def contract(step):
             g, c = divmod(step, BLOCKS)
             last = c == BLOCKS - 1
-            accumulate(step, CHUNKS, first_codes[step][:], first_scales[step][:], 2 * P)
             if last:
                 by_pair[g] = done.tile([P, SHIFTS + 1, DIM], F32, name="by_pair")
-                sums = acc[CHUNKS][:].rearrange("p (s m i) -> p s m i", s=2, m=GROUP_HEADS)
-                for h in range(GROUP_HEADS):
-                    rows = slice(h * DIM, (h + 1) * DIM)
-                    nc.scalar.copy(out=small[rows, g, 0, :], in_=sums[rows, 0, h, :])
-                    nc.scalar.mul(out=by_pair[g][rows, 0, :], in_=sums[rows, 1, h, :], mul=0.5)
-                total = done.tile([P, BLOCKS], F32)
-                nc.scalar.activation(out=total[:], in_=v_sums[g][:], func=ACT.Copy, accum_out=small[:, g, 1, 0:1])
             for chunk in range(CHUNKS):
                 columns = slice(chunk * CHUNK * P, (chunk + 1) * CHUNK * P)
-                accumulate(step, chunk, kk_codes[step][:, columns], kk_scales[step][:, columns], CHUNK * P)
+                if c == 0:
+                    acc[chunk] = psum_acc.tile([P, CHUNK * P], F32, name="acc", tag="acc%d" % chunk)
+                nc.tensor.matmul_mx(
+                    out=acc[chunk][:],
+                    lhsT=v_codes[g][:, c, :].bitcast(FP8X4),
+                    lhsT_scale=v_scales[g][:, c, :],
+                    rhs=kk_codes[step][:, columns].bitcast(FP8X4),
+                    rhs_scale=kk_scales[step][:, columns],
+                    start=(c == 0),
+                    stop=last,
+                )
                 if last:
                     sums = acc[chunk][:].rearrange("p (s m i) -> p s m i", s=CHUNK, m=GROUP_HEADS)
                     for h in range(GROUP_HEADS):
                         rows = slice(h * DIM, (h + 1) * DIM)
                         nc.scalar.copy(out=by_pair[g][rows, chunk * CHUNK + 1 : (chunk + 1) * CHUNK + 1, :], in_=sums[rows, :, h, :])
             if last:
+                first = psum_work.tile([P, 2 * P], F32, name="first", tag="work")
+                for b in range(BLOCKS):
+                    nc.tensor.matmul_mx(
+                        out=first[:],
+                        lhsT=v_codes[g][:, b, :].bitcast(FP8X4),
+                        lhsT_scale=v_scales[g][:, b, :],
+                        rhs=first_codes[g][:, b, :].bitcast(FP8X4),
+                        rhs_scale=first_scales[g][:, b, :],
+                        start=(b == 0),
+                        stop=(b == BLOCKS - 1),
+                    )
+                sums = first[:].rearrange("p (s m i) -> p s m i", s=2, m=GROUP_HEADS)
+                for h in range(GROUP_HEADS):
+                    rows = slice(h * DIM, (h + 1) * DIM)
+                    nc.scalar.copy(out=small[rows, g, 0, :], in_=sums[rows, 0, h, :])
+                    nc.scalar.mul(out=by_pair[g][rows, 0, :], in_=sums[rows, 1, h, :], mul=0.5)
+                total = done.tile([P, BLOCKS], F32)
+                nc.scalar.activation(out=total[:], in_=v_sums[g][:], func=ACT.Copy, accum_out=small[:, g, 1, 0:1])
                 spread(g)
 
         def spread(g):
@@ -347,23 +379,23 @@ def tile_taylorsoftmaxattention_pa_kernel(tc, x, Wk, bk, Wv, bv, out_0, out_1, o
 
         for step in range(STEPS):
             g, c = divmod(step, BLOCKS)
+            multiply(step)
             if step + 1 < STEPS:
                 normalise(step + 1)
             if c == 1 and g + 1 < GROUPS:
                 turn_weights(g + 1)
-            if step + 2 < STEPS:
-                project(step + 2)
-            multiply(step)
             quantise(step)
-            if c == 0 and g > 0:
-                finish(g - 1)
             if c == 1 and g + 1 < GROUPS:
                 quantise_weights(g + 1)
+            if step + 2 < STEPS:
+                project(step + 2)
+            if c == 0 and g > 0:
+                finish(g - 1)
             contract(step)
-        finish(GROUPS - 1)
 
         nc.vector.transpose(out=small_turned[:].rearrange("p g s e -> p (g s e)"), in_=small[:].rearrange("p g s d -> p (g s d)"))
         nc.scalar.copy(out=kv_stage[:, :, 1:OUT_DIM], in_=small_turned[:, :, 0, :])
         nc.scalar.copy(out=vsum_stage[:, :, 1:OUT_DIM], in_=small_turned[:, :, 1, :])
         nc.sync.dma_start(out=kv_rows, in_=kv_stage[:])
         nc.sync.dma_start(out=vsum_rows, in_=vsum_stage[0:P:DIM, :, :])
+        finish(GROUPS - 1)

@@ -248,15 +248,15 @@ def tile_taylorsoftmaxattention_pa_kernel(tc, x, Wk, bk, Wv, bv, out_0, out_1, o
             per_head = factor_squared[step][:].rearrange("p (t h) -> p h t", h=GROUP_HEADS).unsqueeze(2)
             w = prep.tile([P, GROUP_HEADS, WRAPPED, PACK], F32, name="w_wrapped")
             w_wrapped[step] = w
-            nc.gpsimd.tensor_tensor(
+            nc.vector.tensor_tensor(
                 out=w[:, :, 0:DIM, :],
-                in0=k_packed[step][:],
+                in0=planes_by_head(k_tok[step][:]),
                 in1=per_head.to_broadcast([P, GROUP_HEADS, DIM, PACK]),
                 op=ALU.mult,
             )
-            nc.gpsimd.tensor_tensor(
+            nc.vector.tensor_tensor(
                 out=w[:, :, DIM:WRAPPED, :],
-                in0=k_packed[step][:, :, 0 : WRAPPED - DIM, :],
+                in0=planes_by_head(k_tok[step][:])[:, :, 0 : WRAPPED - DIM, :],
                 in1=per_head.to_broadcast([P, GROUP_HEADS, WRAPPED - DIM, PACK]),
                 op=ALU.mult,
             )

@@ -245,18 +245,19 @@ def tile_taylorsoftmaxattention_pa_kernel(tc, x, Wk, bk, Wv, bv, out_0, out_1, o
             nc.scalar.copy(out=k_packed[step][:], in_=planes_by_head(k_tok[step][:]))
             first_bf[step] = prep.tile([P, 2, P, PACK], BF16, name="first_bf", align_bytes=64)
             nc.scalar.copy(out=by_head(first_bf[step][:, 0, :, :]), in_=planes_by_head(kn_rows[:, :, 0:P]))
+            nc.scalar.activation(out=by_head(first_bf[step][:, 1, :, :]), in_=planes_by_head(kn_rows[:, :, 0:P]), func=ACT.Square)
             per_head = factor_squared[step][:].rearrange("p (t h) -> p h t", h=GROUP_HEADS).unsqueeze(2)
             w = prep.tile([P, GROUP_HEADS, WRAPPED, PACK], F32, name="w_wrapped")
             w_wrapped[step] = w
-            nc.vector.tensor_tensor(
+            nc.gpsimd.tensor_tensor(
                 out=w[:, :, 0:DIM, :],
-                in0=planes_by_head(k_tok[step][:]),
+                in0=k_packed[step][:],
                 in1=per_head.to_broadcast([P, GROUP_HEADS, DIM, PACK]),
                 op=ALU.mult,
             )
-            nc.vector.tensor_tensor(
+            nc.gpsimd.tensor_tensor(
                 out=w[:, :, DIM:WRAPPED, :],
-                in0=planes_by_head(k_tok[step][:])[:, :, 0 : WRAPPED - DIM, :],
+                in0=k_packed[step][:, :, 0 : WRAPPED - DIM, :],
                 in1=per_head.to_broadcast([P, GROUP_HEADS, WRAPPED - DIM, PACK]),
                 op=ALU.mult,
             )
@@ -280,7 +281,6 @@ def tile_taylorsoftmaxattention_pa_kernel(tc, x, Wk, bk, Wv, bv, out_0, out_1, o
                     nc.gpsimd.tensor_tensor(
                         out=out, in0=k_packed[step][:, :, 0:count, :], in1=w[:, :, shift : shift + count, :], op=ALU.mult
                     )
-            nc.gpsimd.tensor_tensor(out=by_head(first_bf[step][:, 1, :, :]), in0=k_packed[step][:], in1=w[:, :, 0:DIM, :], op=ALU.mult)
 
         def quantise(step):
             g, c = divmod(step, BLOCKS)
@@ -292,6 +292,11 @@ def tile_taylorsoftmaxattention_pa_kernel(tc, x, Wk, bk, Wv, bv, out_0, out_1, o
             nc.vector.quantize_mx(
                 out=v_codes[g][:, c, :].bitcast(FP8X4), scales=v_scales[g][:, c, :], in_=v_bf[step][:].rearrange("p f t -> p (f t)")
             )
+            nc.vector.quantize_mx(
+                out=first_codes[g][:, c, :].bitcast(FP8X4),
+                scales=first_scales[g][:, c, :],
+                in_=first_bf[step][:].rearrange("p s f t -> p (s f t)"),
+            )
             kk_codes[step] = prod.tile([P, SHIFTS * P], U32, name="kk_codes", align_bytes=64)
             kk_scales[step] = prod.tile([P, SHIFTS * P], U8, name="kk_scales", align_bytes=64)
             for half in range(SHIFTS // WIDE):
@@ -301,17 +306,30 @@ def tile_taylorsoftmaxattention_pa_kernel(tc, x, Wk, bk, Wv, bv, out_0, out_1, o
                     scales=kk_scales[step][:, columns],
                     in_=kk_bf[step % 2][:, half * WIDE : (half + 1) * WIDE, :, :].rearrange("p s f t -> p (s f t)"),
                 )
-            nc.vector.quantize_mx(
-                out=first_codes[g][:, c, :].bitcast(FP8X4),
-                scales=first_scales[g][:, c, :],
-                in_=first_bf[step][:].rearrange("p s f t -> p (s f t)"),
-            )
 
         def contract(step):
             g, c = divmod(step, BLOCKS)
             last = c == BLOCKS - 1
             if last:
                 by_pair[g] = done.tile([P, SHIFTS + 1, DIM], F32, name="by_pair")
+                first = psum_work.tile([P, 2 * P], F32, name="first", tag="work")
+                for b in range(BLOCKS):
+                    nc.tensor.matmul_mx(
+                        out=first[:],
+                        lhsT=v_codes[g][:, b, :].bitcast(FP8X4),
+                        lhsT_scale=v_scales[g][:, b, :],
+                        rhs=first_codes[g][:, b, :].bitcast(FP8X4),
+                        rhs_scale=first_scales[g][:, b, :],
+                        start=(b == 0),
+                        stop=(b == BLOCKS - 1),
+                    )
+                sums = first[:].rearrange("p (s m i) -> p s m i", s=2, m=GROUP_HEADS)
+                for h in range(GROUP_HEADS):
+                    rows = slice(h * DIM, (h + 1) * DIM)
+                    nc.scalar.copy(out=small[rows, g, 0, :], in_=sums[rows, 0, h, :])
+                    nc.scalar.mul(out=by_pair[g][rows, 0, :], in_=sums[rows, 1, h, :], mul=0.5)
+                total = done.tile([P, BLOCKS], F32)
+                nc.scalar.activation(out=total[:], in_=v_sums[g][:], func=ACT.Copy, accum_out=small[:, g, 1, 0:1])
             for chunk in range(CHUNKS):
                 columns = slice(chunk * CHUNK * P, (chunk + 1) * CHUNK * P)
                 if c == 0:
@@ -331,24 +349,6 @@ def tile_taylorsoftmaxattention_pa_kernel(tc, x, Wk, bk, Wv, bv, out_0, out_1, o
                         rows = slice(h * DIM, (h + 1) * DIM)
                         nc.scalar.copy(out=by_pair[g][rows, chunk * CHUNK + 1 : (chunk + 1) * CHUNK + 1, :], in_=sums[rows, :, h, :])
             if last:
-                first = psum_work.tile([P, 2 * P], F32, name="first", tag="work")
-                for b in range(BLOCKS):
-                    nc.tensor.matmul_mx(
-                        out=first[:],
-                        lhsT=v_codes[g][:, b, :].bitcast(FP8X4),
-                        lhsT_scale=v_scales[g][:, b, :],
-                        rhs=first_codes[g][:, b, :].bitcast(FP8X4),
-                        rhs_scale=first_scales[g][:, b, :],
-                        start=(b == 0),
-                        stop=(b == BLOCKS - 1),
-                    )
-                sums = first[:].rearrange("p (s m i) -> p s m i", s=2, m=GROUP_HEADS)
-                for h in range(GROUP_HEADS):
-                    rows = slice(h * DIM, (h + 1) * DIM)
-                    nc.scalar.copy(out=small[rows, g, 0, :], in_=sums[rows, 0, h, :])
-                    nc.scalar.mul(out=by_pair[g][rows, 0, :], in_=sums[rows, 1, h, :], mul=0.5)
-                total = done.tile([P, BLOCKS], F32)
-                nc.scalar.activation(out=total[:], in_=v_sums[g][:], func=ACT.Copy, accum_out=small[:, g, 1, 0:1])
                 spread(g)
 
         def spread(g):

@@ -31,7 +31,7 @@ CHUNK = 4
 CHUNKS = SHIFTS // CHUNK
 WIDE = 8
 WRAPPED = DIM + SHIFTS - 1
-VECTOR_SHIFTS = 12
+VECTOR_SHIFTS = 16
 GRAM_COLS = P + 2
 BAND = 2 * DIM + 1
 

@@ -10,6 +10,7 @@ U8 = mybir.dt.uint8
 FP8X4 = mybir.dt.float8_e4m3fn_x4
 ACT = mybir.ActivationFunctionType
 ALU = mybir.AluOpType
+AXIS = mybir.AxisListType
 
 P = 128
 PACK = 4
@@ -26,14 +27,18 @@ GROUP_HEADS = P // DIM
 GROUPS = HEADS // GROUP_HEADS
 BLOCKS = TOKENS // K_PASS
 STEPS = GROUPS * BLOCKS
-SHIFTS = DIM // 2
-CHUNK = 4
-CHUNKS = SHIFTS // CHUNK
-WIDE = 8
-WRAPPED = DIM + SHIFTS - 1
-VECTOR_SHIFTS = 16
+CELL = GROUP_HEADS * PACK
+SPANS = [16, 8, 4, 2, 1]
+FIRST_PAIR = {16: 0, 8: 256, 4: 384, 2: 448, 1: 480}
+PAIRS = DIM * (DIM - 1) // 2
+PAIR_SLOTS = 512
+CHUNK = 128
+CHUNKS = PAIR_SLOTS // CHUNK
+HALF = PAIR_SLOTS // 2
+VECTOR_PARTS = [(16, 0), (4, 1), (4, 2), (4, 3), (2, 0), (2, 1), (1, 0)]
+GPSIMD_PARTS = [(8, 0), (8, 1), (4, 0)]
 GRAM_COLS = P + 2
-BAND = 2 * DIM + 1
+DIAG = DIM + 1
 
 FLOPS = 2 * TOKENS * CHANNELS * 2 * HEADS * DIM + 2 * TOKENS * HEADS * (DIM * DIM * DIM + DIM * DIM)
 
@@ -59,14 +64,15 @@ def tile_taylorsoftmaxattention_pa_kernel(tc, x, Wk, bk, Wv, bv, out_0, out_1, o
         psum_work = ctx.enter_context(tc.psum_pool(name="psum_work", bufs=1))
         ctx.enter_context(tc.manual_schedule())
 
-        bias_rows = keep.tile([2 * GROUPS, P], BF16)
-        nc.sync.dma_start(out=bias_rows[0:GROUPS, :], in_=bk.rearrange("(g f) -> g f", g=GROUPS))
-        nc.sync.dma_start(out=bias_rows[GROUPS : 2 * GROUPS, :], in_=bv.rearrange("(g f) -> g f", g=GROUPS))
         w_raw = keep.tile([P, GROUPS, 2, CHANNELS], BF16)
         x_raw = keep.tile([P, TOKENS // P, CHANNELS], BF16)
+        bias_rows = keep.tile([2 * GROUPS, P], BF16)
+        nc.scalar.dma_start(out=bias_rows[0:GROUPS, :], in_=bk.rearrange("(g f) -> g f", g=GROUPS))
+        nc.scalar.dma_start(out=bias_rows[GROUPS : 2 * GROUPS, :], in_=bv.rearrange("(g f) -> g f", g=GROUPS))
         nc.sync.dma_start(out=w_raw[:, 0, 0, :], in_=wk_rows[:, 0, :])
         nc.sync.dma_start(out=w_raw[:, 0, 1, :], in_=wv_rows[:, 0, :])
-        for c in range(BLOCKS):
+        nc.sync.dma_start(out=x_raw[:, 0:PACK, :], in_=x_rows[:, 0:PACK, :])
+        for c in range(1, BLOCKS):
             nc.sync.dma_start(out=x_raw[:, PACK * c : PACK * (c + 1), :], in_=x_rows[:, PACK * c : PACK * (c + 1), :])
         nc.sync.dma_start(out=w_raw[:, 1:GROUPS, 0, :], in_=wk_rows[:, 1:GROUPS, :])
         nc.sync.dma_start(out=w_raw[:, 1:GROUPS, 1, :], in_=wv_rows[:, 1:GROUPS, :])
@@ -83,6 +89,16 @@ def tile_taylorsoftmaxattention_pa_kernel(tc, x, Wk, bk, Wv, bv, out_0, out_1, o
         nc.vector.memset(minus_floor[:], -EPS * EPS)
         scaled_floor = keep.tile([P, 1], F32)
         nc.vector.memset(scaled_floor[:], EPS * EPS / (SCALE * SCALE))
+        bias_square = keep.tile([P, P], F32)
+        nc.vector.memset(bias_square[:], 0.0)
+        ident_by_feature = keep.tile([P, P], F32)
+        nc.vector.tensor_copy(
+            out=ident_by_feature[:].rearrange("p (d h) -> p d h", h=GROUP_HEADS), in_=ident[:].rearrange("p (h d) -> p d h", h=GROUP_HEADS)
+        )
+        head_ones = keep.tile([P, GROUP_HEADS], F32)
+        nc.vector.tensor_reduce(
+            out=head_ones[:], in_=ident[:].rearrange("p (h d) -> p h d", h=GROUP_HEADS), op=ALU.add, axis=AXIS.X
+        )
 
         x_codes = keep.tile([P, TOKENS], U32, align_bytes=64)
         x_scales = keep.tile([P, TOKENS], U8, align_bytes=64)
@@ -90,36 +106,22 @@ def tile_taylorsoftmaxattention_pa_kernel(tc, x, Wk, bk, Wv, bv, out_0, out_1, o
         w_scales = keep.tile([P, GROUPS, 2 * P], U8, align_bytes=64)
 
         kn_rows = keep.tile([P, PACK, GRAM_COLS], F32)
-        nc.vector.memset(kn_rows[:], 1.0)
-        kk_bf = []
-        for parity in range(2):
-            kk_bf.append(keep.tile([P, SHIFTS, P, PACK], BF16, name="kk_bf%d" % parity, align_bytes=64))
-            nc.vector.memset(kk_bf[parity][:, SHIFTS - 1, :, :], 0.0)
-        band = keep.tile([P, DIM * BAND], F32)
-        nc.vector.memset(band[:], 0.0)
-        by_shift = band[:].rearrange("p (a w) -> p a w", w=BAND)
-        square = band[:, 0 : DIM * 2 * DIM].rearrange("p (a w) -> p a w", w=2 * DIM)
+        nc.gpsimd.memset(kn_rows[:], 1.0)
+        kk_bf = keep.tile([P, PAIR_SLOTS, CELL], BF16, align_bytes=64)
+        nc.gpsimd.memset(kk_bf[:, PAIRS:PAIR_SLOTS, :], 0.0)
         small = keep.tile([P, GROUPS, 2, DIM], F32, align_bytes=64)
-        nc.vector.memset(small[:], 0.0)
+        nc.gpsimd.memset(small[:], 0.0)
         small_turned = keep.tile([P, GROUPS, 2, DIM], F32, align_bytes=64)
         kv_stage = keep.tile([P, GROUPS, OUT_DIM], F32)
         vsum_stage = keep.tile([P, GROUPS, OUT_DIM], F32)
-        nc.vector.memset(vsum_stage[:], 1.0)
-
-        bias_square = keep.tile([P, P], F32)
-        nc.vector.memset(bias_square[:], 0.0)
-        nc.vector.tensor_copy(out=bias_square[0 : 2 * GROUPS, :], in_=bias_rows[:])
-        bias_turned = psum_work.tile([P, P], F32, tag="work")
-        nc.tensor.transpose(out=bias_turned[:], in_=bias_square[:], identity=ident[:])
+        nc.gpsimd.memset(vsum_stage[:], 1.0)
         bias_cols = keep.tile([P, 2 * GROUPS], F32)
-        nc.scalar.copy(out=bias_cols[:, 0:GROUPS], in_=bias_turned[:, 0:GROUPS])
-        nc.scalar.mul(out=bias_cols[:, GROUPS : 2 * GROUPS], in_=bias_turned[:, GROUPS : 2 * GROUPS], mul=1.0 / TOKENS)
 
         w_grouped = {}
-        k_tok, factor, factor_squared = {}, {}, {}
-        k_packed, w_wrapped, first_bf, v_bf = {}, {}, {}, {}
+        k_feat, squares, k_tok, factor, factor_squared = {}, {}, {}, {}, {}
+        k_packed, w_packed, first_bf, v_bf = {}, {}, {}, {}
         v_codes, v_scales, first_codes, first_scales, kk_codes, kk_scales = {}, {}, {}, {}, {}, {}
-        acc, gram, v_sums, stage, by_pair = {}, {}, {}, {}, {}
+        acc, gram, v_sums, stage, by_pair, by_square, square, turned_square = {}, {}, {}, {}, {}, {}, {}, {}
 
         def turn_weights(g):
             turned = psum_work.tile([P, 2, 2, P], F32, tag="work")
@@ -136,6 +138,13 @@ def tile_taylorsoftmaxattention_pa_kernel(tc, x, Wk, bk, Wv, bv, out_0, out_1, o
                 in_=w_grouped[g][:].rearrange("p m o k -> p (m o k)"),
             )
 
+        def turn_biases():
+            nc.vector.tensor_copy(out=bias_square[0 : 2 * GROUPS, :], in_=bias_rows[:])
+            bias_turned = psum_k.tile([P, P], F32, name="bias_turned", tag="k")
+            nc.tensor.transpose(out=bias_turned[:], in_=bias_square[:], identity=ident[:])
+            nc.scalar.copy(out=bias_cols[:, 0:GROUPS], in_=bias_turned[:, 0:GROUPS])
+            nc.scalar.mul(out=bias_cols[:, GROUPS : 2 * GROUPS], in_=bias_turned[:, GROUPS : 2 * GROUPS], mul=1.0 / TOKENS)
+
         def prepare_tokens(c):
             x_grouped = prep.tile([P, K_PASS, PACK], BF16, align_bytes=64)
             pairs = x_grouped[:].bitcast(F32).rearrange("p (j n) u -> p j n u", j=PACK)
@@ -148,7 +157,8 @@ def tile_taylorsoftmaxattention_pa_kernel(tc, x, Wk, bk, Wv, bv, out_0, out_1, o
                             in_=x_words[:, PACK * c + 2 * half + j, u * P : (u + 1) * P],
                             identity=ident[:],
                         )
-                nc.vector.tensor_copy(out=pairs[:, 2 * half : 2 * half + 2, :, :], in_=turned[:].rearrange("p j u n -> p j n u"))
+                copy = nc.scalar.copy if c == 0 and half == 0 else nc.vector.tensor_copy
+                copy(out=pairs[:, 2 * half : 2 * half + 2, :, :], in_=turned[:].rearrange("p j u n -> p j n u"))
             block = slice(c * K_PASS, (c + 1) * K_PASS)
             nc.vector.quantize_mx(
                 out=x_codes[:, block].bitcast(FP8X4),
@@ -156,31 +166,89 @@ def tile_taylorsoftmaxattention_pa_kernel(tc, x, Wk, bk, Wv, bv, out_0, out_1, o
                 in_=x_grouped[:].rearrange("p n k -> p (n k)"),
             )
 
-        def by_head(ap):
-            return ap.rearrange("p (h d) t -> p h d t", h=GROUP_HEADS)
-
-        def planes_by_head(ap):
-            return ap.rearrange("p t (h d) -> p h d t", h=GROUP_HEADS)
-
-        def project(step):
+        def project(sums, m, step):
             g, c = divmod(step, BLOCKS)
             block = slice(c * K_PASS, (c + 1) * K_PASS)
-            if c == 0:
-                v_sums[g] = prep.tile([P, BLOCKS], F32, name="v_sums")
+            nc.tensor.matmul_mx(
+                out=sums,
+                lhsT=w_codes[:, g, m * P : (m + 1) * P].bitcast(FP8X4),
+                lhsT_scale=w_scales[:, g, m * P : (m + 1) * P],
+                rhs=x_codes[:, block].bitcast(FP8X4),
+                rhs_scale=x_scales[:, block],
+                start=True,
+                stop=True,
+            )
+
+        def start_k(step):
+            g = step // BLOCKS
             k_sums = psum_k.tile([P, K_PASS], F32, name="k_sums", tag="k")
+            project(k_sums[:], 0, step)
+            bias = bias_cols[:, g : g + 1]
+            k_feat[step] = prep.tile([P, K_PASS], F32, name="k_feat")
+            nc.scalar.activation(out=k_feat[step][:], in_=k_sums[:], func=ACT.Identity, bias=bias, scale=1.0)
+            squares[step] = prep.tile([P, K_PASS], F32, name="squares")
+            nc.scalar.activation(out=squares[step][:], in_=k_sums[:], func=ACT.Square, bias=bias, scale=1.0)
+
+        def finish_k(step):
+            k_tok[step] = psum_k.tile([P, P, PACK], F32, name="k_tok", tag="k")
+            for t in range(PACK):
+                nc.tensor.transpose(out=k_tok[step][:, :, t], in_=k_feat[step][:, t * P : (t + 1) * P], identity=ident_by_feature[:])
+            norms = psum_work.tile([P, PACK, GROUP_HEADS], F32, tag="work")
+            for t in range(PACK):
+                nc.tensor.matmul(out=norms[:, t, :], lhsT=squares[step][:, t * P : (t + 1) * P], rhs=head_ones[:], start=True, stop=True)
+            k_packed[step] = prep.tile([P, DIM, CELL], F32, name="k_packed")
+            nc.scalar.copy(out=k_packed[step][:], in_=by_cell(k_tok[step]))
+            above_floor = prep.tile([P, GROUP_HEADS, PACK], F32)
+            nc.scalar.activation(
+                out=above_floor[:], in_=norms[:].rearrange("p t h -> p h t"), func=ACT.Relu, bias=minus_floor[:], scale=1.0
+            )
+            factor[step] = prep.tile([P, CELL], F32, name="factor")
+            nc.scalar.activation(
+                out=factor[step][:],
+                in_=above_floor[:].rearrange("p h t -> p (h t)"),
+                func=ACT.Abs_reciprocal_sqrt,
+                bias=scaled_floor[:],
+                scale=1.0 / (SCALE * SCALE),
+            )
+            factor_squared[step] = prep.tile([P, CELL], F32, name="factor_squared")
+            nc.scalar.activation(out=factor_squared[step][:], in_=factor[step][:], func=ACT.Square)
+
+        def by_cell(tile):
+            return tile[:].rearrange("p (d h) t -> p d (h t)", h=GROUP_HEADS)
+
+        def make_w(step):
+            w_packed[step] = prep.tile([P, DIM, CELL], F32, name="w_packed")
+            nc.gpsimd.tensor_tensor(
+                out=w_packed[step][:],
+                in0=k_packed[step][:],
+                in1=factor_squared[step][:].unsqueeze(1).to_broadcast([P, DIM, CELL]),
+                op=ALU.mult,
+            )
+
+        def make_kn_and_v(step):
+            g, c = divmod(step, BLOCKS)
+            k_cells = k_tok[step][:].rearrange("p (d h) t -> p h d t", h=GROUP_HEADS)
+            for t in range(PACK):
+                for h in range(GROUP_HEADS):
+                    nc.scalar.activation(
+                        out=kn_rows[:, t, h * DIM : (h + 1) * DIM],
+                        in_=k_cells[:, h, :, t],
+                        func=ACT.Copy,
+                        scale=factor[step][:, h * PACK + t : h * PACK + t + 1],
+                    )
+            if c == 0:
+                gram[g] = psum_gram.tile([P, GRAM_COLS], F32, name="gram")
+                v_sums[g] = prep.tile([P, BLOCKS], F32, name="v_sums")
             v_sum_bank = psum_work.tile([P, K_PASS], F32, name="v_sum_bank", tag="work")
-            for m, sums in enumerate([k_sums, v_sum_bank]):
-                nc.tensor.matmul_mx(
-                    out=sums[:],
-                    lhsT=w_codes[:, g, m * P : (m + 1) * P].bitcast(FP8X4),
-                    lhsT_scale=w_scales[:, g, m * P : (m + 1) * P],
-                    rhs=x_codes[:, block].bitcast(FP8X4),
-                    rhs_scale=x_scales[:, block],
-                    start=True,
-                    stop=True,
+            project(v_sum_bank[:], 1, step)
+            for t in range(PACK):
+                nc.tensor.matmul(
+                    out=gram[g][:],
+                    lhsT=kn_rows[:, t, 0:P],
+                    rhs=kn_rows[:, t, :],
+                    start=(c == 0 and t == 0),
+                    stop=(c == BLOCKS - 1 and t == PACK - 1),
                 )
-            k_feat = prep.tile([P, K_PASS], F32)
-            nc.scalar.activation(out=k_feat[:], in_=k_sums[:], func=ACT.Identity, bias=bias_cols[:, g : g + 1], scale=1.0)
             v_feat = prep.tile([P, K_PASS], F32)
             nc.scalar.activation(
                 out=v_feat[:],
@@ -190,77 +258,15 @@ def tile_taylorsoftmaxattention_pa_kernel(tc, x, Wk, bk, Wv, bv, out_0, out_1, o
                 scale=1.0 / TOKENS,
                 accum_out=v_sums[g][:, c : c + 1],
             )
-            k_tok[step] = psum_k.tile([P, PACK, P], F32, name="k_tok", tag="k")
             v_tok = psum_work.tile([P, PACK, P], F32, name="v_tok", tag="work")
             for t in range(PACK):
-                nc.tensor.transpose(out=k_tok[step][:, t, :], in_=k_feat[:, t * P : (t + 1) * P], identity=ident[:])
-            for t in range(PACK):
                 nc.tensor.transpose(out=v_tok[:, t, :], in_=v_feat[:, t * P : (t + 1) * P], identity=ident[:])
-            squares = prep.tile([P, PACK, P], F32)
-            square_sums = prep.tile([P, PACK * GROUP_HEADS], F32)
-            for t in range(PACK):
-                for h in range(GROUP_HEADS):
-                    nc.scalar.activation(
-                        out=squares[:, t, h * DIM : (h + 1) * DIM],
-                        in_=k_tok[step][:, t, h * DIM : (h + 1) * DIM],
-                        func=ACT.Square,
-                        accum_out=square_sums[:, t * GROUP_HEADS + h : t * GROUP_HEADS + h + 1],
-                    )
-            above_floor = prep.tile([P, PACK * GROUP_HEADS], F32)
-            nc.scalar.activation(out=above_floor[:], in_=square_sums[:], func=ACT.Relu, bias=minus_floor[:], scale=1.0)
+            first_bf[step] = prep.tile([P, 2, P, PACK], BF16, name="first_bf", align_bytes=64)
+            kn_words = kn_rows[:, :, 0:P].rearrange("p t f -> p f t")
+            nc.scalar.copy(out=first_bf[step][:, 0, :, :], in_=kn_words)
+            nc.scalar.activation(out=first_bf[step][:, 1, :, :], in_=kn_words, func=ACT.Square)
             v_bf[step] = prep.tile([P, P, PACK], BF16, name="v_bf", align_bytes=64)
             nc.scalar.copy(out=v_bf[step][:], in_=v_tok[:].rearrange("p t f -> p f t"))
-            factor[step] = prep.tile([P, PACK * GROUP_HEADS], F32, name="factor")
-            nc.scalar.activation(
-                out=factor[step][:],
-                in_=above_floor[:],
-                func=ACT.Abs_reciprocal_sqrt,
-                bias=scaled_floor[:],
-                scale=1.0 / (SCALE * SCALE),
-            )
-            factor_squared[step] = prep.tile([P, PACK * GROUP_HEADS], F32, name="factor_squared")
-            nc.scalar.activation(out=factor_squared[step][:], in_=factor[step][:], func=ACT.Square)
-
-        def normalise(step):
-            g, c = divmod(step, BLOCKS)
-            for t in range(PACK):
-                for h in range(GROUP_HEADS):
-                    nc.scalar.activation(
-                        out=kn_rows[:, t, h * DIM : (h + 1) * DIM],
-                        in_=k_tok[step][:, t, h * DIM : (h + 1) * DIM],
-                        func=ACT.Copy,
-                        scale=factor[step][:, t * GROUP_HEADS + h : t * GROUP_HEADS + h + 1],
-                    )
-            if c == 0:
-                gram[g] = psum_gram.tile([P, GRAM_COLS], F32, name="gram")
-            for t in range(PACK):
-                nc.tensor.matmul(
-                    out=gram[g][:],
-                    lhsT=kn_rows[:, t, 0:P],
-                    rhs=kn_rows[:, t, :],
-                    start=(c == 0 and t == 0),
-                    stop=(c == BLOCKS - 1 and t == PACK - 1),
-                )
-            k_packed[step] = prep.tile([P, GROUP_HEADS, DIM, PACK], F32, name="k_packed")
-            nc.scalar.copy(out=k_packed[step][:], in_=planes_by_head(k_tok[step][:]))
-            first_bf[step] = prep.tile([P, 2, P, PACK], BF16, name="first_bf", align_bytes=64)
-            nc.scalar.copy(out=by_head(first_bf[step][:, 0, :, :]), in_=planes_by_head(kn_rows[:, :, 0:P]))
-            nc.scalar.activation(out=by_head(first_bf[step][:, 1, :, :]), in_=planes_by_head(kn_rows[:, :, 0:P]), func=ACT.Square)
-            per_head = factor_squared[step][:].rearrange("p (t h) -> p h t", h=GROUP_HEADS).unsqueeze(2)
-            w = prep.tile([P, GROUP_HEADS, WRAPPED, PACK], F32, name="w_wrapped")
-            w_wrapped[step] = w
-            nc.gpsimd.tensor_tensor(
-                out=w[:, :, 0:DIM, :],
-                in0=k_packed[step][:],
-                in1=per_head.to_broadcast([P, GROUP_HEADS, DIM, PACK]),
-                op=ALU.mult,
-            )
-            nc.gpsimd.tensor_tensor(
-                out=w[:, :, DIM:WRAPPED, :],
-                in0=k_packed[step][:, :, 0 : WRAPPED - DIM, :],
-                in1=per_head.to_broadcast([P, GROUP_HEADS, WRAPPED - DIM, PACK]),
-                op=ALU.mult,
-            )
             if c == BLOCKS - 1:
                 stage[g] = done.tile([P, DIM, OUT_DIM], F32, name="stage")
                 for h in range(GROUP_HEADS):
@@ -269,18 +275,25 @@ def tile_taylorsoftmaxattention_pa_kernel(tc, x, Wk, bk, Wv, bv, out_0, out_1, o
                 nc.scalar.mul(out=kv_stage[:, g, 0:1], in_=gram[g][:, P : P + 1], mul=1.0 / TOKENS)
 
         def multiply(step):
-            w = w_wrapped[step]
-            for shift in range(1, SHIFTS + 1):
-                count = DIM if shift < SHIFTS else DIM - SHIFTS
-                out = by_head(kk_bf[step % 2][:, shift - 1, :, :])[:, :, 0:count, :]
-                if shift <= VECTOR_SHIFTS:
-                    nc.vector.tensor_tensor(
-                        out=out, in0=planes_by_head(k_tok[step][:])[:, :, 0:count, :], in1=w[:, :, shift : shift + count, :], op=ALU.mult
-                    )
-                else:
-                    nc.gpsimd.tensor_tensor(
-                        out=out, in0=k_packed[step][:, :, 0:count, :], in1=w[:, :, shift : shift + count, :], op=ALU.mult
-                    )
+            w = w_packed[step][:]
+            for engine, k, parts in [
+                (nc.vector, by_cell(k_tok[step]), VECTOR_PARTS),
+                (nc.gpsimd, k_packed[step][:], GPSIMD_PARTS),
+            ]:
+                for span, part in parts:
+                    if span >= 8:
+                        shape = [P, span, span, CELL]
+                        start = FIRST_PAIR[span] + part * span * span
+                        low = part * 2 * span
+                        left = k[:, low : low + span, :].unsqueeze(2)
+                        right = w[:, low + span : low + 2 * span, :].unsqueeze(1)
+                    else:
+                        shape = [P, DIM // (2 * span), span, CELL]
+                        start = FIRST_PAIR[span] + part * (DIM // 2)
+                        left = k.rearrange("p (b r) x -> p b r x", r=2 * span)[:, :, part, :].unsqueeze(2)
+                        right = w.rearrange("p (b r) x -> p b r x", r=2 * span)[:, :, span : 2 * span, :]
+                    out = kk_bf[:, start : start + shape[1] * span, :].rearrange("p (a j) x -> p a j x", j=span)
+                    engine.tensor_tensor(out=out, in0=left.to_broadcast(shape), in1=right.to_broadcast(shape), op=ALU.mult)
 
         def quantise(step):
             g, c = divmod(step, BLOCKS)
@@ -297,21 +310,22 @@ def tile_taylorsoftmaxattention_pa_kernel(tc, x, Wk, bk, Wv, bv, out_0, out_1, o
                 scales=first_scales[g][:, c, :],
                 in_=first_bf[step][:].rearrange("p s f t -> p (s f t)"),
             )
-            kk_codes[step] = prod.tile([P, SHIFTS * P], U32, name="kk_codes", align_bytes=64)
-            kk_scales[step] = prod.tile([P, SHIFTS * P], U8, name="kk_scales", align_bytes=64)
-            for half in range(SHIFTS // WIDE):
-                columns = slice(half * WIDE * P, (half + 1) * WIDE * P)
+            kk_codes[step] = prod.tile([P, PAIR_SLOTS * GROUP_HEADS], U32, name="kk_codes", align_bytes=64)
+            kk_scales[step] = prod.tile([P, PAIR_SLOTS * GROUP_HEADS], U8, name="kk_scales", align_bytes=64)
+            for half in range(PAIR_SLOTS // HALF):
+                columns = slice(half * HALF * GROUP_HEADS, (half + 1) * HALF * GROUP_HEADS)
                 nc.vector.quantize_mx(
                     out=kk_codes[step][:, columns].bitcast(FP8X4),
                     scales=kk_scales[step][:, columns],
-                    in_=kk_bf[step % 2][:, half * WIDE : (half + 1) * WIDE, :, :].rearrange("p s f t -> p (s f t)"),
+                    in_=kk_bf[:, half * HALF : (half + 1) * HALF, :].rearrange("p q x -> p (q x)"),
                 )
 
         def contract(step):
             g, c = divmod(step, BLOCKS)
             last = c == BLOCKS - 1
             if last:
-                by_pair[g] = done.tile([P, SHIFTS + 1, DIM], F32, name="by_pair")
+                by_pair[g] = done.tile([P, PAIR_SLOTS], F32, name="by_pair")
+                by_square[g] = done.tile([P, DIM], F32, name="by_square")
                 first = psum_work.tile([P, 2 * P], F32, name="first", tag="work")
                 for b in range(BLOCKS):
                     nc.tensor.matmul_mx(
@@ -327,13 +341,13 @@ def tile_taylorsoftmaxattention_pa_kernel(tc, x, Wk, bk, Wv, bv, out_0, out_1, o
                 for h in range(GROUP_HEADS):
                     rows = slice(h * DIM, (h + 1) * DIM)
                     nc.scalar.copy(out=small[rows, g, 0, :], in_=sums[rows, 0, h, :])
-                    nc.scalar.mul(out=by_pair[g][rows, 0, :], in_=sums[rows, 1, h, :], mul=0.5)
+                    nc.scalar.copy(out=by_square[g][rows, :], in_=sums[rows, 1, h, :])
                 total = done.tile([P, BLOCKS], F32)
                 nc.scalar.activation(out=total[:], in_=v_sums[g][:], func=ACT.Copy, accum_out=small[:, g, 1, 0:1])
             for chunk in range(CHUNKS):
-                columns = slice(chunk * CHUNK * P, (chunk + 1) * CHUNK * P)
+                columns = slice(chunk * CHUNK * GROUP_HEADS, (chunk + 1) * CHUNK * GROUP_HEADS)
                 if c == 0:
-                    acc[chunk] = psum_acc.tile([P, CHUNK * P], F32, name="acc", tag="acc%d" % chunk)
+                    acc[chunk] = psum_acc.tile([P, CHUNK * GROUP_HEADS], F32, name="acc", tag="acc%d" % chunk)
                 nc.tensor.matmul_mx(
                     out=acc[chunk][:],
                     lhsT=v_codes[g][:, c, :].bitcast(FP8X4),
@@ -344,58 +358,80 @@ def tile_taylorsoftmaxattention_pa_kernel(tc, x, Wk, bk, Wv, bv, out_0, out_1, o
                     stop=last,
                 )
                 if last:
-                    sums = acc[chunk][:].rearrange("p (s m i) -> p s m i", s=CHUNK, m=GROUP_HEADS)
+                    sums = acc[chunk][:].rearrange("p (q m) -> p m q", m=GROUP_HEADS)
                     for h in range(GROUP_HEADS):
                         rows = slice(h * DIM, (h + 1) * DIM)
-                        nc.scalar.copy(out=by_pair[g][rows, chunk * CHUNK + 1 : (chunk + 1) * CHUNK + 1, :], in_=sums[rows, :, h, :])
-            if last:
-                spread(g)
+                        nc.scalar.copy(out=by_pair[g][rows, chunk * CHUNK : (chunk + 1) * CHUNK], in_=sums[rows, h, :])
 
-        def spread(g):
-            nc.scalar.copy(out=by_shift[:, :, 0 : SHIFTS + 1], in_=by_pair[g][:].rearrange("p s a -> p a s"))
-            nc.scalar.copy(
-                out=by_shift[:, SHIFTS - 1 : DIM - 1, DIM + 2 : DIM + 1 + SHIFTS],
-                in_=by_pair[g][:, 1:SHIFTS, SHIFTS:DIM].rearrange("p s a -> p a s"),
+        def lay_square(g, copies):
+            square[g] = done.tile([P, DIM * DIAG], F32, name="square", align_bytes=64)
+            for span, copy in zip(SPANS, copies):
+                spans = DIM // (2 * span)
+                order = "p (b i j) -> p b i j" if span >= 8 else "p (i b j) -> p b i j"
+                sums = by_pair[g][:, FIRST_PAIR[span] : FIRST_PAIR[span] + DIM // 2 * span].rearrange(order, b=spans, i=span)
+                cells = square[g][:].rearrange("p (b w) -> p b w", b=spans)
+                upper = cells[:, :, span : span + span * DIM].rearrange("p b (i r) -> p b i r", r=DIM)[:, :, :, 0:span]
+                lower = cells[:, :, span * DIM : 2 * span * DIM].rearrange("p b (j r) -> p b j r", r=DIM)[:, :, :, 0:span]
+                copy(out=upper, in_=sums)
+                copy(out=lower, in_=sums.rearrange("p b i j -> p b j i"))
+            nc.scalar.copy(out=square[g][:].rearrange("p (i w) -> p i w", w=DIAG)[:, :, 0], in_=by_square[g][:])
+
+        def turn_square(g, part, parts):
+            rows = slice(part * DIM // parts, (part + 1) * DIM // parts)
+            if part == 0:
+                turned_square[g] = done.tile([P, DIM, DIM], F32, name="turned_square", align_bytes=64)
+            nc.vector.transpose(
+                out=turned_square[g][:, rows, :].rearrange("p w e -> p (w e)"), in_=square[g][:, rows.start * DIM : rows.stop * DIM]
             )
 
-        def finish(g):
-            full = done.tile([P, DIM, DIM], F32, align_bytes=64)
-            nc.vector.tensor_tensor(
-                out=full[:], in0=square[:, :, 0:DIM], in1=square[:, :, 0:DIM].rearrange("p a b -> p b a"), op=ALU.add
+        def store(g, part, parts):
+            rows = slice(part * DIM // parts, (part + 1) * DIM // parts)
+            nc.scalar.copy(out=stage[g][:, rows, 1:OUT_DIM], in_=turned_square[g][:, rows, :])
+            nc.sync.dma_start(
+                out=kv_mod_rows[g][:, rows.start * OUT_DIM : rows.stop * OUT_DIM], in_=stage[g][:, rows, :].rearrange("p w e -> p (w e)")
             )
-            turned = done.tile([P, DIM, DIM], F32, align_bytes=64)
-            nc.vector.transpose(out=turned[:].rearrange("p b e -> p (b e)"), in_=full[:].rearrange("p b a -> p (b a)"))
-            nc.scalar.copy(out=stage[g][:, :, 1:OUT_DIM], in_=turned[:])
-            nc.sync.dma_start(out=kv_mod_rows[g], in_=stage[g][:].rearrange("p w e -> p (w e)"))
 
         turn_weights(0)
+        turn_biases()
         quantise_weights(0)
         prepare_tokens(0)
-        project(0)
-        for c in range(1, BLOCKS):
-            prepare_tokens(c)
-        normalise(0)
-        project(1)
+        prepare_tokens(1)
+        start_k(0)
+        prepare_tokens(2)
+        finish_k(0)
+        make_w(0)
+        prepare_tokens(3)
+        make_kn_and_v(0)
+        start_k(1)
+        finish_k(1)
 
         for step in range(STEPS):
             g, c = divmod(step, BLOCKS)
             multiply(step)
             if step + 1 < STEPS:
-                normalise(step + 1)
-            if c == 1 and g + 1 < GROUPS:
+                make_w(step + 1)
+                make_kn_and_v(step + 1)
+            if c == 0 and g + 1 < GROUPS:
                 turn_weights(g + 1)
             quantise(step)
             if c == 1 and g + 1 < GROUPS:
                 quantise_weights(g + 1)
             if step + 2 < STEPS:
-                project(step + 2)
+                start_k(step + 2)
+                finish_k(step + 2)
             if c == 0 and g > 0:
-                finish(g - 1)
+                lay_square(g - 1, [nc.scalar.copy] * len(SPANS))
+            if c == 1 and g > 0:
+                turn_square(g - 1, 0, 1)
+                store(g - 1, 0, 1)
             contract(step)
 
+        lay_square(GROUPS - 1, [nc.vector.tensor_copy] * 2 + [nc.scalar.copy] * 3)
+        for part in range(2):
+            turn_square(GROUPS - 1, part, 2)
+            store(GROUPS - 1, part, 2)
         nc.vector.transpose(out=small_turned[:].rearrange("p g s e -> p (g s e)"), in_=small[:].rearrange("p g s d -> p (g s d)"))
         nc.scalar.copy(out=kv_stage[:, :, 1:OUT_DIM], in_=small_turned[:, :, 0, :])
         nc.scalar.copy(out=vsum_stage[:, :, 1:OUT_DIM], in_=small_turned[:, :, 1, :])
         nc.sync.dma_start(out=kv_rows, in_=kv_stage[:])
         nc.sync.dma_start(out=vsum_rows, in_=vsum_stage[0:P:DIM, :, :])
-        finish(GROUPS - 1)

@@ -10,7 +10,6 @@ U8 = mybir.dt.uint8
 FP8X4 = mybir.dt.float8_e4m3fn_x4
 ACT = mybir.ActivationFunctionType
 ALU = mybir.AluOpType
-AXIS = mybir.AxisListType
 
 P = 128
 PACK = 4
@@ -95,10 +94,6 @@ def tile_taylorsoftmaxattention_pa_kernel(tc, x, Wk, bk, Wv, bv, out_0, out_1, o
         nc.vector.tensor_copy(
             out=ident_by_feature[:].rearrange("p (d h) -> p d h", h=GROUP_HEADS), in_=ident[:].rearrange("p (h d) -> p d h", h=GROUP_HEADS)
         )
-        head_ones = keep.tile([P, GROUP_HEADS], F32)
-        nc.vector.tensor_reduce(
-            out=head_ones[:], in_=ident[:].rearrange("p (h d) -> p h d", h=GROUP_HEADS), op=ALU.add, axis=AXIS.X
-        )
 
         x_codes = keep.tile([P, TOKENS], U32, align_bytes=64)
         x_scales = keep.tile([P, TOKENS], U8, align_bytes=64)
@@ -118,7 +113,7 @@ def tile_taylorsoftmaxattention_pa_kernel(tc, x, Wk, bk, Wv, bv, out_0, out_1, o
         bias_cols = keep.tile([P, 2 * GROUPS], F32)
 
         w_grouped = {}
-        k_feat, squares, k_tok, factor, factor_squared = {}, {}, {}, {}, {}
+        k_feat, k_tok, factor, factor_squared = {}, {}, {}, {}
         k_packed, w_packed, first_bf, v_bf = {}, {}, {}, {}
         v_codes, v_scales, first_codes, first_scales, kk_codes, kk_scales = {}, {}, {}, {}, {}, {}
         acc, gram, v_sums, stage, by_pair, by_square, square, turned_square = {}, {}, {}, {}, {}, {}, {}, {}
@@ -185,27 +180,31 @@ def tile_taylorsoftmaxattention_pa_kernel(tc, x, Wk, bk, Wv, bv, out_0, out_1, o
             project(k_sums[:], 0, step)
             bias = bias_cols[:, g : g + 1]
             k_feat[step] = prep.tile([P, K_PASS], F32, name="k_feat")
-            nc.scalar.activation(out=k_feat[step][:], in_=k_sums[:], func=ACT.Identity, bias=bias, scale=1.0)
-            squares[step] = prep.tile([P, K_PASS], F32, name="squares")
-            nc.scalar.activation(out=squares[step][:], in_=k_sums[:], func=ACT.Square, bias=bias, scale=1.0)
+            nc.scalar.activation(
+                out=k_feat[step][:].rearrange("p (u e n) -> p u e n", u=2, e=2),
+                in_=k_sums[:].rearrange("p (u n e) -> p u e n", u=2, e=2),
+                func=ACT.Identity,
+                bias=bias,
+                scale=1.0,
+            )
 
         def finish_k(step):
             k_tok[step] = psum_k.tile([P, P, PACK], F32, name="k_tok", tag="k")
             for t in range(PACK):
                 nc.tensor.transpose(out=k_tok[step][:, :, t], in_=k_feat[step][:, t * P : (t + 1) * P], identity=ident_by_feature[:])
-            norms = psum_work.tile([P, PACK, GROUP_HEADS], F32, tag="work")
-            for t in range(PACK):
-                nc.tensor.matmul(out=norms[:, t, :], lhsT=squares[step][:, t * P : (t + 1) * P], rhs=head_ones[:], start=True, stop=True)
+            squares = prep.tile([P, CELL, DIM], F32)
+            norms = prep.tile([P, CELL], F32)
+            k_cells = by_cell(k_tok[step])
+            for x in range(CELL):
+                nc.scalar.activation(out=squares[:, x, :], in_=k_cells[:, :, x], func=ACT.Square, accum_out=norms[:, x : x + 1])
             k_packed[step] = prep.tile([P, DIM, CELL], F32, name="k_packed")
-            nc.scalar.copy(out=k_packed[step][:], in_=by_cell(k_tok[step]))
-            above_floor = prep.tile([P, GROUP_HEADS, PACK], F32)
-            nc.scalar.activation(
-                out=above_floor[:], in_=norms[:].rearrange("p t h -> p h t"), func=ACT.Relu, bias=minus_floor[:], scale=1.0
-            )
+            nc.scalar.copy(out=k_packed[step][:], in_=k_cells)
+            above_floor = prep.tile([P, CELL], F32)
+            nc.scalar.activation(out=above_floor[:], in_=norms[:], func=ACT.Relu, bias=minus_floor[:], scale=1.0)
             factor[step] = prep.tile([P, CELL], F32, name="factor")
             nc.scalar.activation(
                 out=factor[step][:],
-                in_=above_floor[:].rearrange("p h t -> p (h t)"),
+                in_=above_floor[:],
                 func=ACT.Abs_reciprocal_sqrt,
                 bias=scaled_floor[:],
                 scale=1.0 / (SCALE * SCALE),
@@ -249,7 +248,7 @@ def tile_taylorsoftmaxattention_pa_kernel(tc, x, Wk, bk, Wv, bv, out_0, out_1, o
                     start=(c == 0 and t == 0),
                     stop=(c == BLOCKS - 1 and t == PACK - 1),
                 )
-            v_feat = prep.tile([P, K_PASS], F32)
+            v_feat = prep.tile([P, K_PASS], BF16)
             nc.scalar.activation(
                 out=v_feat[:],
                 in_=v_sum_bank[:],
@@ -258,15 +257,16 @@ def tile_taylorsoftmaxattention_pa_kernel(tc, x, Wk, bk, Wv, bv, out_0, out_1, o
                 scale=1.0 / TOKENS,
                 accum_out=v_sums[g][:, c : c + 1],
             )
-            v_tok = psum_work.tile([P, PACK, P], F32, name="v_tok", tag="work")
-            for t in range(PACK):
-                nc.tensor.transpose(out=v_tok[:, t, :], in_=v_feat[:, t * P : (t + 1) * P], identity=ident[:])
+            v_tok = psum_work.tile([P, 2, P], F32, name="v_tok", tag="work")
+            v_words = v_feat[:].bitcast(F32)
+            for u in range(2):
+                nc.tensor.transpose(out=v_tok[:, u, :], in_=v_words[:, u * P : (u + 1) * P], identity=ident[:])
             first_bf[step] = prep.tile([P, 2, P, PACK], BF16, name="first_bf", align_bytes=64)
             kn_words = kn_rows[:, :, 0:P].rearrange("p t f -> p f t")
             nc.scalar.copy(out=first_bf[step][:, 0, :, :], in_=kn_words)
             nc.scalar.activation(out=first_bf[step][:, 1, :, :], in_=kn_words, func=ACT.Square)
             v_bf[step] = prep.tile([P, P, PACK], BF16, name="v_bf", align_bytes=64)
-            nc.scalar.copy(out=v_bf[step][:], in_=v_tok[:].rearrange("p t f -> p f t"))
+            nc.scalar.copy(out=v_bf[step][:].bitcast(F32), in_=v_tok[:].rearrange("p u f -> p f u"))
             if c == BLOCKS - 1:
                 stage[g] = done.tile([P, DIM, OUT_DIM], F32, name="stage")
                 for h in range(GROUP_HEADS):

@@ -34,8 +34,8 @@ PAIR_SLOTS = 512
 CHUNK = 128
 CHUNKS = PAIR_SLOTS // CHUNK
 HALF = PAIR_SLOTS // 2
-VECTOR_PARTS = [(16, 0), (4, 1), (4, 2), (4, 3), (2, 0), (2, 1), (1, 0)]
-GPSIMD_PARTS = [(8, 0), (8, 1), (4, 0)]
+VECTOR_PARTS = [(16, 0), (4, 0), (4, 1), (4, 2), (4, 3), (2, 0), (2, 1), (1, 0)]
+GPSIMD_PARTS = [(8, 0), (8, 1)]
 GRAM_COLS = P + 2
 DIAG = DIM + 1
 
@@ -100,8 +100,10 @@ def tile_taylorsoftmaxattention_pa_kernel(tc, x, Wk, bk, Wv, bv, out_0, out_1, o
         w_codes = keep.tile([P, GROUPS, 2 * P], U32, align_bytes=64)
         w_scales = keep.tile([P, GROUPS, 2 * P], U8, align_bytes=64)
 
-        kn_rows = keep.tile([P, PACK, GRAM_COLS], F32)
-        nc.gpsimd.memset(kn_rows[:], 1.0)
+        kn_rows = []
+        for parity in range(2):
+            kn_rows.append(keep.tile([P, PACK, GRAM_COLS], F32, name="kn_rows%d" % parity))
+            nc.gpsimd.memset(kn_rows[parity][:], 1.0)
         kk_bf = keep.tile([P, PAIR_SLOTS, CELL], BF16, align_bytes=64)
         nc.gpsimd.memset(kk_bf[:, PAIRS:PAIR_SLOTS, :], 0.0)
         small = keep.tile([P, GROUPS, 2, DIM], F32, align_bytes=64)
@@ -113,10 +115,10 @@ def tile_taylorsoftmaxattention_pa_kernel(tc, x, Wk, bk, Wv, bv, out_0, out_1, o
         bias_cols = keep.tile([P, 2 * GROUPS], F32)
 
         w_grouped = {}
-        k_feat, k_tok, factor, factor_squared = {}, {}, {}, {}
+        k_feat, v_feat, k_tok, factor, factor_squared = {}, {}, {}, {}, {}
         k_packed, w_packed, first_bf, v_bf = {}, {}, {}, {}
         v_codes, v_scales, first_codes, first_scales, kk_codes, kk_scales = {}, {}, {}, {}, {}, {}
-        acc, gram, v_sums, stage, by_pair, by_square, square, turned_square = {}, {}, {}, {}, {}, {}, {}, {}
+        acc, first, gram, v_sums, stage, by_pair, by_square, square, turned_square = {}, {}, {}, {}, {}, {}, {}, {}, {}
 
         def turn_weights(g):
             turned = psum_work.tile([P, 2, 2, P], F32, tag="work")
@@ -174,24 +176,40 @@ def tile_taylorsoftmaxattention_pa_kernel(tc, x, Wk, bk, Wv, bv, out_0, out_1, o
                 stop=True,
             )
 
-        def start_k(step):
-            g = step // BLOCKS
+        def start(step):
+            g, c = divmod(step, BLOCKS)
             k_sums = psum_k.tile([P, K_PASS], F32, name="k_sums", tag="k")
             project(k_sums[:], 0, step)
-            bias = bias_cols[:, g : g + 1]
+            v_sum_bank = psum_work.tile([P, K_PASS], F32, name="v_sum_bank", tag="work")
+            project(v_sum_bank[:], 1, step)
             k_feat[step] = prep.tile([P, K_PASS], F32, name="k_feat")
             nc.scalar.activation(
                 out=k_feat[step][:].rearrange("p (u e n) -> p u e n", u=2, e=2),
                 in_=k_sums[:].rearrange("p (u n e) -> p u e n", u=2, e=2),
                 func=ACT.Identity,
-                bias=bias,
+                bias=bias_cols[:, g : g + 1],
                 scale=1.0,
             )
+            if c == 0:
+                v_sums[g] = prep.tile([P, BLOCKS], F32, name="v_sums")
+            v_feat[step] = prep.tile([P, K_PASS], BF16, name="v_feat")
+            nc.scalar.activation(
+                out=v_feat[step][:],
+                in_=v_sum_bank[:],
+                func=ACT.Identity,
+                bias=bias_cols[:, GROUPS + g : GROUPS + g + 1],
+                scale=1.0 / TOKENS,
+                accum_out=v_sums[g][:, c : c + 1],
+            )
 
-        def finish_k(step):
+        def turn(step):
             k_tok[step] = psum_k.tile([P, P, PACK], F32, name="k_tok", tag="k")
             for t in range(PACK):
                 nc.tensor.transpose(out=k_tok[step][:, :, t], in_=k_feat[step][:, t * P : (t + 1) * P], identity=ident_by_feature[:])
+            v_tok = psum_work.tile([P, 2, P], F32, name="v_tok", tag="work")
+            v_words = v_feat[step][:].bitcast(F32)
+            for u in range(2):
+                nc.tensor.transpose(out=v_tok[:, u, :], in_=v_words[:, u * P : (u + 1) * P], identity=ident[:])
             squares = prep.tile([P, CELL, DIM], F32)
             norms = prep.tile([P, CELL], F32)
             k_cells = by_cell(k_tok[step])
@@ -201,6 +219,8 @@ def tile_taylorsoftmaxattention_pa_kernel(tc, x, Wk, bk, Wv, bv, out_0, out_1, o
             nc.scalar.copy(out=k_packed[step][:], in_=k_cells)
             above_floor = prep.tile([P, CELL], F32)
             nc.scalar.activation(out=above_floor[:], in_=norms[:], func=ACT.Relu, bias=minus_floor[:], scale=1.0)
+            v_bf[step] = prep.tile([P, P, PACK], BF16, name="v_bf", align_bytes=64)
+            nc.scalar.copy(out=v_bf[step][:].bitcast(F32), in_=v_tok[:].rearrange("p u f -> p f u"))
             factor[step] = prep.tile([P, CELL], F32, name="factor")
             nc.scalar.activation(
                 out=factor[step][:],
@@ -224,49 +244,32 @@ def tile_taylorsoftmaxattention_pa_kernel(tc, x, Wk, bk, Wv, bv, out_0, out_1, o
                 op=ALU.mult,
             )
 
-        def make_kn_and_v(step):
+        def normalise(step):
             g, c = divmod(step, BLOCKS)
+            rows = kn_rows[step % 2]
             k_cells = k_tok[step][:].rearrange("p (d h) t -> p h d t", h=GROUP_HEADS)
             for t in range(PACK):
                 for h in range(GROUP_HEADS):
                     nc.scalar.activation(
-                        out=kn_rows[:, t, h * DIM : (h + 1) * DIM],
+                        out=rows[:, t, h * DIM : (h + 1) * DIM],
                         in_=k_cells[:, h, :, t],
                         func=ACT.Copy,
                         scale=factor[step][:, h * PACK + t : h * PACK + t + 1],
                     )
             if c == 0:
                 gram[g] = psum_gram.tile([P, GRAM_COLS], F32, name="gram")
-                v_sums[g] = prep.tile([P, BLOCKS], F32, name="v_sums")
-            v_sum_bank = psum_work.tile([P, K_PASS], F32, name="v_sum_bank", tag="work")
-            project(v_sum_bank[:], 1, step)
             for t in range(PACK):
                 nc.tensor.matmul(
                     out=gram[g][:],
-                    lhsT=kn_rows[:, t, 0:P],
-                    rhs=kn_rows[:, t, :],
+                    lhsT=rows[:, t, 0:P],
+                    rhs=rows[:, t, :],
                     start=(c == 0 and t == 0),
                     stop=(c == BLOCKS - 1 and t == PACK - 1),
                 )
-            v_feat = prep.tile([P, K_PASS], BF16)
-            nc.scalar.activation(
-                out=v_feat[:],
-                in_=v_sum_bank[:],
-                func=ACT.Identity,
-                bias=bias_cols[:, GROUPS + g : GROUPS + g + 1],
-                scale=1.0 / TOKENS,
-                accum_out=v_sums[g][:, c : c + 1],
-            )
-            v_tok = psum_work.tile([P, 2, P], F32, name="v_tok", tag="work")
-            v_words = v_feat[:].bitcast(F32)
-            for u in range(2):
-                nc.tensor.transpose(out=v_tok[:, u, :], in_=v_words[:, u * P : (u + 1) * P], identity=ident[:])
             first_bf[step] = prep.tile([P, 2, P, PACK], BF16, name="first_bf", align_bytes=64)
-            kn_words = kn_rows[:, :, 0:P].rearrange("p t f -> p f t")
+            kn_words = rows[:, :, 0:P].rearrange("p t f -> p f t")
             nc.scalar.copy(out=first_bf[step][:, 0, :, :], in_=kn_words)
             nc.scalar.activation(out=first_bf[step][:, 1, :, :], in_=kn_words, func=ACT.Square)
-            v_bf[step] = prep.tile([P, P, PACK], BF16, name="v_bf", align_bytes=64)
-            nc.scalar.copy(out=v_bf[step][:].bitcast(F32), in_=v_tok[:].rearrange("p u f -> p f u"))
             if c == BLOCKS - 1:
                 stage[g] = done.tile([P, DIM, OUT_DIM], F32, name="stage")
                 for h in range(GROUP_HEADS):
@@ -283,16 +286,16 @@ def tile_taylorsoftmaxattention_pa_kernel(tc, x, Wk, bk, Wv, bv, out_0, out_1, o
                 for span, part in parts:
                     if span >= 8:
                         shape = [P, span, span, CELL]
-                        start = FIRST_PAIR[span] + part * span * span
+                        slot = FIRST_PAIR[span] + part * span * span
                         low = part * 2 * span
                         left = k[:, low : low + span, :].unsqueeze(2)
                         right = w[:, low + span : low + 2 * span, :].unsqueeze(1)
                     else:
                         shape = [P, DIM // (2 * span), span, CELL]
-                        start = FIRST_PAIR[span] + part * (DIM // 2)
+                        slot = FIRST_PAIR[span] + part * (DIM // 2)
                         left = k.rearrange("p (b r) x -> p b r x", r=2 * span)[:, :, part, :].unsqueeze(2)
                         right = w.rearrange("p (b r) x -> p b r x", r=2 * span)[:, :, span : 2 * span, :]
-                    out = kk_bf[:, start : start + shape[1] * span, :].rearrange("p (a j) x -> p a j x", j=span)
+                    out = kk_bf[:, slot : slot + shape[1] * span, :].rearrange("p (a j) x -> p a j x", j=span)
                     engine.tensor_tensor(out=out, in0=left.to_broadcast(shape), in1=right.to_broadcast(shape), op=ALU.mult)
 
         def quantise(step):
@@ -322,28 +325,6 @@ def tile_taylorsoftmaxattention_pa_kernel(tc, x, Wk, bk, Wv, bv, out_0, out_1, o
 
         def contract(step):
             g, c = divmod(step, BLOCKS)
-            last = c == BLOCKS - 1
-            if last:
-                by_pair[g] = done.tile([P, PAIR_SLOTS], F32, name="by_pair")
-                by_square[g] = done.tile([P, DIM], F32, name="by_square")
-                first = psum_work.tile([P, 2 * P], F32, name="first", tag="work")
-                for b in range(BLOCKS):
-                    nc.tensor.matmul_mx(
-                        out=first[:],
-                        lhsT=v_codes[g][:, b, :].bitcast(FP8X4),
-                        lhsT_scale=v_scales[g][:, b, :],
-                        rhs=first_codes[g][:, b, :].bitcast(FP8X4),
-                        rhs_scale=first_scales[g][:, b, :],
-                        start=(b == 0),
-                        stop=(b == BLOCKS - 1),
-                    )
-                sums = first[:].rearrange("p (s m i) -> p s m i", s=2, m=GROUP_HEADS)
-                for h in range(GROUP_HEADS):
-                    rows = slice(h * DIM, (h + 1) * DIM)
-                    nc.scalar.copy(out=small[rows, g, 0, :], in_=sums[rows, 0, h, :])
-                    nc.scalar.copy(out=by_square[g][rows, :], in_=sums[rows, 1, h, :])
-                total = done.tile([P, BLOCKS], F32)
-                nc.scalar.activation(out=total[:], in_=v_sums[g][:], func=ACT.Copy, accum_out=small[:, g, 1, 0:1])
             for chunk in range(CHUNKS):
                 columns = slice(chunk * CHUNK * GROUP_HEADS, (chunk + 1) * CHUNK * GROUP_HEADS)
                 if c == 0:
@@ -355,13 +336,36 @@ def tile_taylorsoftmaxattention_pa_kernel(tc, x, Wk, bk, Wv, bv, out_0, out_1, o
                     rhs=kk_codes[step][:, columns].bitcast(FP8X4),
                     rhs_scale=kk_scales[step][:, columns],
                     start=(c == 0),
-                    stop=last,
+                    stop=(c == BLOCKS - 1),
                 )
-                if last:
-                    sums = acc[chunk][:].rearrange("p (q m) -> p m q", m=GROUP_HEADS)
-                    for h in range(GROUP_HEADS):
-                        rows = slice(h * DIM, (h + 1) * DIM)
-                        nc.scalar.copy(out=by_pair[g][rows, chunk * CHUNK : (chunk + 1) * CHUNK], in_=sums[rows, h, :])
+            if c == BLOCKS - 1:
+                first[g] = psum_work.tile([P, 2 * P], F32, name="first", tag="work")
+                for b in range(BLOCKS):
+                    nc.tensor.matmul_mx(
+                        out=first[g][:],
+                        lhsT=v_codes[g][:, b, :].bitcast(FP8X4),
+                        lhsT_scale=v_scales[g][:, b, :],
+                        rhs=first_codes[g][:, b, :].bitcast(FP8X4),
+                        rhs_scale=first_scales[g][:, b, :],
+                        start=(b == 0),
+                        stop=(b == BLOCKS - 1),
+                    )
+
+        def collect(g):
+            by_pair[g] = done.tile([P, PAIR_SLOTS], F32, name="by_pair")
+            by_square[g] = done.tile([P, DIM], F32, name="by_square")
+            for chunk in range(CHUNKS):
+                sums = acc[chunk][:].rearrange("p (q m) -> p m q", m=GROUP_HEADS)
+                for h in range(GROUP_HEADS):
+                    rows = slice(h * DIM, (h + 1) * DIM)
+                    nc.scalar.copy(out=by_pair[g][rows, chunk * CHUNK : (chunk + 1) * CHUNK], in_=sums[rows, h, :])
+            sums = first[g][:].rearrange("p (s m i) -> p s m i", s=2, m=GROUP_HEADS)
+            for h in range(GROUP_HEADS):
+                rows = slice(h * DIM, (h + 1) * DIM)
+                nc.scalar.copy(out=small[rows, g, 0, :], in_=sums[rows, 0, h, :])
+                nc.scalar.copy(out=by_square[g][rows, :], in_=sums[rows, 1, h, :])
+            total = done.tile([P, BLOCKS], F32)
+            nc.scalar.activation(out=total[:], in_=v_sums[g][:], func=ACT.Copy, accum_out=small[:, g, 1, 0:1])
 
         def lay_square(g, copies):
             square[g] = done.tile([P, DIM * DIAG], F32, name="square", align_bytes=64)
@@ -396,35 +400,39 @@ def tile_taylorsoftmaxattention_pa_kernel(tc, x, Wk, bk, Wv, bv, out_0, out_1, o
         quantise_weights(0)
         prepare_tokens(0)
         prepare_tokens(1)
-        start_k(0)
+        start(0)
         prepare_tokens(2)
-        finish_k(0)
+        turn(0)
         make_w(0)
         prepare_tokens(3)
-        make_kn_and_v(0)
-        start_k(1)
-        finish_k(1)
+        normalise(0)
+        start(1)
+        turn(1)
+        normalise(1)
 
         for step in range(STEPS):
             g, c = divmod(step, BLOCKS)
             multiply(step)
             if step + 1 < STEPS:
                 make_w(step + 1)
-                make_kn_and_v(step + 1)
             if c == 0 and g + 1 < GROUPS:
                 turn_weights(g + 1)
             quantise(step)
             if c == 1 and g + 1 < GROUPS:
                 quantise_weights(g + 1)
             if step + 2 < STEPS:
-                start_k(step + 2)
-                finish_k(step + 2)
+                start(step + 2)
+                turn(step + 2)
+            contract(step)
+            if step + 2 < STEPS:
+                normalise(step + 2)
+            if c == BLOCKS - 1:
+                collect(g)
             if c == 0 and g > 0:
                 lay_square(g - 1, [nc.scalar.copy] * len(SPANS))
             if c == 1 and g > 0:
                 turn_square(g - 1, 0, 1)
                 store(g - 1, 0, 1)
-            contract(step)
 
         lay_square(GROUPS - 1, [nc.vector.tensor_copy] * 2 + [nc.scalar.copy] * 3)
         for part in range(2):

@@ -68,9 +68,11 @@ def tile_taylorsoftmaxattention_pa_kernel(tc, x, Wk, bk, Wv, bv, out_0, out_1, o
         bias_rows = keep.tile([2 * GROUPS, P], BF16)
         nc.scalar.dma_start(out=bias_rows[0:GROUPS, :], in_=bk.rearrange("(g f) -> g f", g=GROUPS))
         nc.scalar.dma_start(out=bias_rows[GROUPS : 2 * GROUPS, :], in_=bv.rearrange("(g f) -> g f", g=GROUPS))
+        for half in range(2):
+            rows = slice(2 * half, 2 * half + 2)
+            nc.sync.dma_start(out=x_raw[:, rows, :], in_=x_rows[:, rows, :])
         nc.sync.dma_start(out=w_raw[:, 0, 0, :], in_=wk_rows[:, 0, :])
         nc.sync.dma_start(out=w_raw[:, 0, 1, :], in_=wv_rows[:, 0, :])
-        nc.sync.dma_start(out=x_raw[:, 0:PACK, :], in_=x_rows[:, 0:PACK, :])
         for c in range(1, BLOCKS):
             nc.sync.dma_start(out=x_raw[:, PACK * c : PACK * (c + 1), :], in_=x_rows[:, PACK * c : PACK * (c + 1), :])
         nc.sync.dma_start(out=w_raw[:, 1:GROUPS, 0, :], in_=wk_rows[:, 1:GROUPS, :])
@@ -114,7 +116,7 @@ def tile_taylorsoftmaxattention_pa_kernel(tc, x, Wk, bk, Wv, bv, out_0, out_1, o
         nc.gpsimd.memset(vsum_stage[:], 1.0)
         bias_cols = keep.tile([P, 2 * GROUPS], F32)
 
-        w_grouped = {}
+        w_grouped, x_grouped = {}, {}
         k_feat, v_feat, k_tok, factor, factor_squared = {}, {}, {}, {}, {}
         k_packed, w_packed, first_bf, v_bf = {}, {}, {}, {}
         v_codes, v_scales, first_codes, first_scales, kk_codes, kk_scales = {}, {}, {}, {}, {}, {}
@@ -126,14 +128,16 @@ def tile_taylorsoftmaxattention_pa_kernel(tc, x, Wk, bk, Wv, bv, out_0, out_1, o
                 for u in range(2):
                     nc.tensor.transpose(out=turned[:, m, u, :], in_=w_words[:, g, m, u * P : (u + 1) * P], identity=ident[:])
             w_grouped[g] = prep.tile([P, 2, P, PACK], BF16, name="w_grouped", align_bytes=64)
-            nc.scalar.copy(out=w_grouped[g][:].bitcast(F32), in_=turned[:].rearrange("p m u o -> p m o u"))
+            for m in range(2):
+                nc.scalar.copy(out=w_grouped[g][:, m, :, :].bitcast(F32), in_=turned[:, m, :, :].rearrange("p u o -> p o u"))
 
         def quantise_weights(g):
-            nc.vector.quantize_mx(
-                out=w_codes[:, g, :].bitcast(FP8X4),
-                scales=w_scales[:, g, :],
-                in_=w_grouped[g][:].rearrange("p m o k -> p (m o k)"),
-            )
+            for m in range(2):
+                nc.vector.quantize_mx(
+                    out=w_codes[:, g, m * P : (m + 1) * P].bitcast(FP8X4),
+                    scales=w_scales[:, g, m * P : (m + 1) * P],
+                    in_=w_grouped[g][:, m, :, :].rearrange("p o k -> p (o k)"),
+                )
 
         def turn_biases():
             nc.vector.tensor_copy(out=bias_square[0 : 2 * GROUPS, :], in_=bias_rows[:])
@@ -142,9 +146,9 @@ def tile_taylorsoftmaxattention_pa_kernel(tc, x, Wk, bk, Wv, bv, out_0, out_1, o
             nc.scalar.copy(out=bias_cols[:, 0:GROUPS], in_=bias_turned[:, 0:GROUPS])
             nc.scalar.mul(out=bias_cols[:, GROUPS : 2 * GROUPS], in_=bias_turned[:, GROUPS : 2 * GROUPS], mul=1.0 / TOKENS)
 
-        def prepare_tokens(c):
-            x_grouped = prep.tile([P, K_PASS, PACK], BF16, align_bytes=64)
-            pairs = x_grouped[:].bitcast(F32).rearrange("p (j n) u -> p j n u", j=PACK)
+        def turn_tokens(c):
+            x_grouped[c] = prep.tile([P, K_PASS, PACK], BF16, name="x_grouped", align_bytes=64)
+            pairs = x_grouped[c][:].bitcast(F32).rearrange("p (j n) u -> p j n u", j=PACK)
             for half in range(2):
                 turned = psum_acc.tile([P, 2, 2, P], F32, name="x_turned", tag="acc%d" % ((2 * c + half) % CHUNKS))
                 for j in range(2):
@@ -154,13 +158,15 @@ def tile_taylorsoftmaxattention_pa_kernel(tc, x, Wk, bk, Wv, bv, out_0, out_1, o
                             in_=x_words[:, PACK * c + 2 * half + j, u * P : (u + 1) * P],
                             identity=ident[:],
                         )
-                copy = nc.scalar.copy if c == 0 and half == 0 else nc.vector.tensor_copy
+                copy = nc.scalar.copy if c == 0 and half == 1 else nc.vector.tensor_copy
                 copy(out=pairs[:, 2 * half : 2 * half + 2, :, :], in_=turned[:].rearrange("p j u n -> p j n u"))
+
+        def quantise_tokens(c):
             block = slice(c * K_PASS, (c + 1) * K_PASS)
             nc.vector.quantize_mx(
                 out=x_codes[:, block].bitcast(FP8X4),
                 scales=x_scales[:, block],
-                in_=x_grouped[:].rearrange("p n k -> p (n k)"),
+                in_=x_grouped[c][:].rearrange("p n k -> p (n k)"),
             )
 
         def project(sums, m, step):
@@ -235,9 +241,9 @@ def tile_taylorsoftmaxattention_pa_kernel(tc, x, Wk, bk, Wv, bv, out_0, out_1, o
         def by_cell(tile):
             return tile[:].rearrange("p (d h) t -> p d (h t)", h=GROUP_HEADS)
 
-        def make_w(step):
+        def make_w(step, engine):
             w_packed[step] = prep.tile([P, DIM, CELL], F32, name="w_packed")
-            nc.gpsimd.tensor_tensor(
+            engine.tensor_tensor(
                 out=w_packed[step][:],
                 in0=k_packed[step][:],
                 in1=factor_squared[step][:].unsqueeze(1).to_broadcast([P, DIM, CELL]),
@@ -245,7 +251,6 @@ def tile_taylorsoftmaxattention_pa_kernel(tc, x, Wk, bk, Wv, bv, out_0, out_1, o
             )
 
         def normalise(step):
-            g, c = divmod(step, BLOCKS)
             rows = kn_rows[step % 2]
             k_cells = k_tok[step][:].rearrange("p (d h) t -> p h d t", h=GROUP_HEADS)
             for t in range(PACK):
@@ -256,6 +261,17 @@ def tile_taylorsoftmaxattention_pa_kernel(tc, x, Wk, bk, Wv, bv, out_0, out_1, o
                         func=ACT.Copy,
                         scale=factor[step][:, h * PACK + t : h * PACK + t + 1],
                     )
+
+        def make_first(step):
+            first_bf[step] = prep.tile([P, 2, P, PACK], BF16, name="first_bf", align_bytes=64)
+            kn_words = kn_rows[step % 2][:, :, 0:P].rearrange("p t (f r) -> p f t r", r=4)
+            first_words = first_bf[step][:].rearrange("p s (f r) t -> p s f t r", r=4)
+            nc.scalar.copy(out=first_words[:, 0], in_=kn_words)
+            nc.scalar.activation(out=first_words[:, 1], in_=kn_words, func=ACT.Square)
+
+        def add_gram(step):
+            g, c = divmod(step, BLOCKS)
+            rows = kn_rows[step % 2]
             if c == 0:
                 gram[g] = psum_gram.tile([P, GRAM_COLS], F32, name="gram")
             for t in range(PACK):
@@ -266,16 +282,13 @@ def tile_taylorsoftmaxattention_pa_kernel(tc, x, Wk, bk, Wv, bv, out_0, out_1, o
                     start=(c == 0 and t == 0),
                     stop=(c == BLOCKS - 1 and t == PACK - 1),
                 )
-            first_bf[step] = prep.tile([P, 2, P, PACK], BF16, name="first_bf", align_bytes=64)
-            kn_words = rows[:, :, 0:P].rearrange("p t f -> p f t")
-            nc.scalar.copy(out=first_bf[step][:, 0, :, :], in_=kn_words)
-            nc.scalar.activation(out=first_bf[step][:, 1, :, :], in_=kn_words, func=ACT.Square)
-            if c == BLOCKS - 1:
-                stage[g] = done.tile([P, DIM, OUT_DIM], F32, name="stage")
-                for h in range(GROUP_HEADS):
-                    rows = slice(h * DIM, (h + 1) * DIM)
-                    nc.scalar.mul(out=stage[g][rows, :, 0], in_=gram[g][rows, h * DIM : (h + 1) * DIM], mul=1.0 / TOKENS)
-                nc.scalar.mul(out=kv_stage[:, g, 0:1], in_=gram[g][:, P : P + 1], mul=1.0 / TOKENS)
+
+        def collect_gram(g):
+            stage[g] = done.tile([P, DIM, OUT_DIM], F32, name="stage")
+            for h in range(GROUP_HEADS):
+                rows = slice(h * DIM, (h + 1) * DIM)
+                nc.scalar.mul(out=stage[g][rows, :, 0], in_=gram[g][rows, h * DIM : (h + 1) * DIM], mul=1.0 / TOKENS)
+            nc.scalar.mul(out=kv_stage[:, g, 0:1], in_=gram[g][:, P : P + 1], mul=1.0 / TOKENS)
 
         def multiply(step):
             w = w_packed[step][:]
@@ -315,16 +328,29 @@ def tile_taylorsoftmaxattention_pa_kernel(tc, x, Wk, bk, Wv, bv, out_0, out_1, o
             )
             kk_codes[step] = prod.tile([P, PAIR_SLOTS * GROUP_HEADS], U32, name="kk_codes", align_bytes=64)
             kk_scales[step] = prod.tile([P, PAIR_SLOTS * GROUP_HEADS], U8, name="kk_scales", align_bytes=64)
-            for half in range(PAIR_SLOTS // HALF):
-                columns = slice(half * HALF * GROUP_HEADS, (half + 1) * HALF * GROUP_HEADS)
+            width = CHUNK if step == STEPS - 1 else HALF
+            for pairs in [slice(p, p + width) for p in range(0, PAIR_SLOTS, width)]:
+                columns = slice(pairs.start * GROUP_HEADS, pairs.stop * GROUP_HEADS)
                 nc.vector.quantize_mx(
                     out=kk_codes[step][:, columns].bitcast(FP8X4),
                     scales=kk_scales[step][:, columns],
-                    in_=kk_bf[:, half * HALF : (half + 1) * HALF, :].rearrange("p q x -> p (q x)"),
+                    in_=kk_bf[:, pairs, :].rearrange("p q x -> p (q x)"),
                 )
 
         def contract(step):
             g, c = divmod(step, BLOCKS)
+            if c == BLOCKS - 1:
+                first[g] = psum_work.tile([P, 2 * P], F32, name="first", tag="work")
+                for b in range(BLOCKS):
+                    nc.tensor.matmul_mx(
+                        out=first[g][:],
+                        lhsT=v_codes[g][:, b, :].bitcast(FP8X4),
+                        lhsT_scale=v_scales[g][:, b, :],
+                        rhs=first_codes[g][:, b, :].bitcast(FP8X4),
+                        rhs_scale=first_scales[g][:, b, :],
+                        start=(b == 0),
+                        stop=(b == BLOCKS - 1),
+                    )
             for chunk in range(CHUNKS):
                 columns = slice(chunk * CHUNK * GROUP_HEADS, (chunk + 1) * CHUNK * GROUP_HEADS)
                 if c == 0:
@@ -338,27 +364,9 @@ def tile_taylorsoftmaxattention_pa_kernel(tc, x, Wk, bk, Wv, bv, out_0, out_1, o
                     start=(c == 0),
                     stop=(c == BLOCKS - 1),
                 )
-            if c == BLOCKS - 1:
-                first[g] = psum_work.tile([P, 2 * P], F32, name="first", tag="work")
-                for b in range(BLOCKS):
-                    nc.tensor.matmul_mx(
-                        out=first[g][:],
-                        lhsT=v_codes[g][:, b, :].bitcast(FP8X4),
-                        lhsT_scale=v_scales[g][:, b, :],
-                        rhs=first_codes[g][:, b, :].bitcast(FP8X4),
-                        rhs_scale=first_scales[g][:, b, :],
-                        start=(b == 0),
-                        stop=(b == BLOCKS - 1),
-                    )
 
-        def collect(g):
-            by_pair[g] = done.tile([P, PAIR_SLOTS], F32, name="by_pair")
+        def collect_first(g):
             by_square[g] = done.tile([P, DIM], F32, name="by_square")
-            for chunk in range(CHUNKS):
-                sums = acc[chunk][:].rearrange("p (q m) -> p m q", m=GROUP_HEADS)
-                for h in range(GROUP_HEADS):
-                    rows = slice(h * DIM, (h + 1) * DIM)
-                    nc.scalar.copy(out=by_pair[g][rows, chunk * CHUNK : (chunk + 1) * CHUNK], in_=sums[rows, h, :])
             sums = first[g][:].rearrange("p (s m i) -> p s m i", s=2, m=GROUP_HEADS)
             for h in range(GROUP_HEADS):
                 rows = slice(h * DIM, (h + 1) * DIM)
@@ -367,17 +375,27 @@ def tile_taylorsoftmaxattention_pa_kernel(tc, x, Wk, bk, Wv, bv, out_0, out_1, o
             total = done.tile([P, BLOCKS], F32)
             nc.scalar.activation(out=total[:], in_=v_sums[g][:], func=ACT.Copy, accum_out=small[:, g, 1, 0:1])
 
-        def lay_square(g, copies):
-            square[g] = done.tile([P, DIM * DIAG], F32, name="square", align_bytes=64)
-            for span, copy in zip(SPANS, copies):
-                spans = DIM // (2 * span)
-                order = "p (b i j) -> p b i j" if span >= 8 else "p (i b j) -> p b i j"
-                sums = by_pair[g][:, FIRST_PAIR[span] : FIRST_PAIR[span] + DIM // 2 * span].rearrange(order, b=spans, i=span)
-                cells = square[g][:].rearrange("p (b w) -> p b w", b=spans)
-                upper = cells[:, :, span : span + span * DIM].rearrange("p b (i r) -> p b i r", r=DIM)[:, :, :, 0:span]
-                lower = cells[:, :, span * DIM : 2 * span * DIM].rearrange("p b (j r) -> p b j r", r=DIM)[:, :, :, 0:span]
-                copy(out=upper, in_=sums)
-                copy(out=lower, in_=sums.rearrange("p b i j -> p b j i"))
+        def collect(g, chunk, copy):
+            if chunk == 0:
+                by_pair[g] = done.tile([P, PAIR_SLOTS], F32, name="by_pair")
+            sums = acc[chunk][:].rearrange("p (q m) -> p m q", m=GROUP_HEADS)
+            for h in range(GROUP_HEADS):
+                rows = slice(h * DIM, (h + 1) * DIM)
+                copy(out=by_pair[g][rows, chunk * CHUNK : (chunk + 1) * CHUNK], in_=sums[rows, h, :])
+
+        def lay(g, span, copy):
+            if span == SPANS[0]:
+                square[g] = done.tile([P, DIM * DIAG], F32, name="square", align_bytes=64)
+            spans = DIM // (2 * span)
+            order = "p (b i j) -> p b i j" if span >= 8 else "p (i b j) -> p b i j"
+            sums = by_pair[g][:, FIRST_PAIR[span] : FIRST_PAIR[span] + DIM // 2 * span].rearrange(order, b=spans, i=span)
+            cells = square[g][:].rearrange("p (b w) -> p b w", b=spans)
+            upper = cells[:, :, span : span + span * DIM].rearrange("p b (i r) -> p b i r", r=DIM)[:, :, :, 0:span]
+            lower = cells[:, :, span * DIM : 2 * span * DIM].rearrange("p b (j r) -> p b j r", r=DIM)[:, :, :, 0:span]
+            copy(out=upper, in_=sums)
+            copy(out=lower, in_=sums.rearrange("p b i j -> p b j i"))
+
+        def lay_diagonal(g):
             nc.scalar.copy(out=square[g][:].rearrange("p (i w) -> p i w", w=DIAG)[:, :, 0], in_=by_square[g][:])
 
         def turn_square(g, part, parts):
@@ -395,30 +413,39 @@ def tile_taylorsoftmaxattention_pa_kernel(tc, x, Wk, bk, Wv, bv, out_0, out_1, o
                 out=kv_mod_rows[g][:, rows.start * OUT_DIM : rows.stop * OUT_DIM], in_=stage[g][:, rows, :].rearrange("p w e -> p (w e)")
             )
 
+        turn_tokens(0)
         turn_weights(0)
         turn_biases()
+        quantise_tokens(0)
         quantise_weights(0)
-        prepare_tokens(0)
-        prepare_tokens(1)
+        turn_tokens(1)
         start(0)
-        prepare_tokens(2)
+        quantise_tokens(1)
+        turn_tokens(2)
         turn(0)
-        make_w(0)
-        prepare_tokens(3)
+        quantise_tokens(2)
         normalise(0)
+        turn_tokens(3)
+        quantise_tokens(3)
+        make_w(0, nc.vector)
         start(1)
         turn(1)
+        make_first(0)
+        add_gram(0)
         normalise(1)
+        make_first(1)
+        add_gram(1)
 
         for step in range(STEPS):
             g, c = divmod(step, BLOCKS)
+            last_group = g == GROUPS - 1
             multiply(step)
             if step + 1 < STEPS:
-                make_w(step + 1)
-            if c == 0 and g + 1 < GROUPS:
+                make_w(step + 1, nc.gpsimd)
+            if c == 0 and not last_group:
                 turn_weights(g + 1)
             quantise(step)
-            if c == 1 and g + 1 < GROUPS:
+            if c == 1 and not last_group:
                 quantise_weights(g + 1)
             if step + 2 < STEPS:
                 start(step + 2)
@@ -426,20 +453,37 @@ def tile_taylorsoftmaxattention_pa_kernel(tc, x, Wk, bk, Wv, bv, out_0, out_1, o
             contract(step)
             if step + 2 < STEPS:
                 normalise(step + 2)
-            if c == BLOCKS - 1:
-                collect(g)
+                make_first(step + 2)
+                add_gram(step + 2)
+            if c == 1:
+                collect_gram(g)
+            if c == BLOCKS - 1 and not last_group:
+                collect_first(g)
+                for chunk in range(CHUNKS):
+                    collect(g, chunk, nc.scalar.copy)
             if c == 0 and g > 0:
-                lay_square(g - 1, [nc.scalar.copy] * len(SPANS))
+                for span in SPANS:
+                    lay(g - 1, span, nc.scalar.copy)
+                lay_diagonal(g - 1)
             if c == 1 and g > 0:
                 turn_square(g - 1, 0, 1)
                 store(g - 1, 0, 1)
 
-        lay_square(GROUPS - 1, [nc.vector.tensor_copy] * 2 + [nc.scalar.copy] * 3)
-        for part in range(2):
-            turn_square(GROUPS - 1, part, 2)
-            store(GROUPS - 1, part, 2)
+        g = GROUPS - 1
+        collect_first(g)
         nc.vector.transpose(out=small_turned[:].rearrange("p g s e -> p (g s e)"), in_=small[:].rearrange("p g s d -> p (g s d)"))
+        collect(g, 0, nc.scalar.copy)
+        collect(g, 1, nc.scalar.copy)
+        lay(g, 16, nc.scalar.copy)
+        collect(g, 2, nc.vector.tensor_copy)
+        collect(g, 3, nc.vector.tensor_copy)
+        for span in [8, 4, 2, 1]:
+            lay(g, span, nc.vector.tensor_copy)
+        lay_diagonal(g)
         nc.scalar.copy(out=kv_stage[:, :, 1:OUT_DIM], in_=small_turned[:, :, 0, :])
-        nc.scalar.copy(out=vsum_stage[:, :, 1:OUT_DIM], in_=small_turned[:, :, 1, :])
         nc.sync.dma_start(out=kv_rows, in_=kv_stage[:])
+        nc.scalar.copy(out=vsum_stage[:, :, 1:OUT_DIM], in_=small_turned[:, :, 1, :])
         nc.sync.dma_start(out=vsum_rows, in_=vsum_stage[0:P:DIM, :, :])
+        for part in range(4):
+            turn_square(g, part, 4)
+            store(g, part, 4)

@@ -221,8 +221,6 @@ def tile_taylorsoftmaxattention_pa_kernel(tc, x, Wk, bk, Wv, bv, out_0, out_1, o
             k_cells = by_cell(k_tok[step])
             for x in range(CELL):
                 nc.scalar.activation(out=squares[:, x, :], in_=k_cells[:, :, x], func=ACT.Square, accum_out=norms[:, x : x + 1])
-            k_packed[step] = prep.tile([P, DIM, CELL], F32, name="k_packed")
-            nc.scalar.copy(out=k_packed[step][:], in_=k_cells)
             above_floor = prep.tile([P, CELL], F32)
             nc.scalar.activation(out=above_floor[:], in_=norms[:], func=ACT.Relu, bias=minus_floor[:], scale=1.0)
             v_bf[step] = prep.tile([P, P, PACK], BF16, name="v_bf", align_bytes=64)
@@ -235,6 +233,8 @@ def tile_taylorsoftmaxattention_pa_kernel(tc, x, Wk, bk, Wv, bv, out_0, out_1, o
                 bias=scaled_floor[:],
                 scale=1.0 / (SCALE * SCALE),
             )
+            k_packed[step] = prep.tile([P, DIM, CELL], F32, name="k_packed")
+            nc.scalar.copy(out=k_packed[step][:], in_=k_cells)
             factor_squared[step] = prep.tile([P, CELL], F32, name="factor_squared")
             nc.scalar.activation(out=factor_squared[step][:], in_=factor[step][:], func=ACT.Square)
 
@@ -465,7 +465,7 @@ def tile_taylorsoftmaxattention_pa_kernel(tc, x, Wk, bk, Wv, bv, out_0, out_1, o
                 for span in SPANS:
                     lay(g - 1, span, nc.scalar.copy)
                 lay_diagonal(g - 1)
-            if c == 1 and g > 0:
+            if c == 2 and g > 0:
                 turn_square(g - 1, 0, 1)
                 store(g - 1, 0, 1)
 

@@ -27,15 +27,15 @@ GROUPS = HEADS // GROUP_HEADS
 BLOCKS = TOKENS // K_PASS
 STEPS = GROUPS * BLOCKS
 CELL = GROUP_HEADS * PACK
-SPANS = [16, 8, 4, 2, 1]
-FIRST_PAIR = {16: 0, 8: 256, 4: 384, 2: 448, 1: 480}
+SPANS = [(16, 0), (16, 1), (8, 0), (4, 0), (2, 0), (1, 0)]
+FIRST_PAIR = {(16, 0): 0, (8, 0): 128, (16, 1): 256, (4, 0): 384, (2, 0): 448, (1, 0): 480}
 PAIRS = DIM * (DIM - 1) // 2
 PAIR_SLOTS = 512
 CHUNK = 128
 CHUNKS = PAIR_SLOTS // CHUNK
 HALF = PAIR_SLOTS // 2
-VECTOR_PARTS = [(16, 0), (4, 0), (4, 1), (4, 2), (4, 3), (2, 0), (2, 1), (1, 0)]
-GPSIMD_PARTS = [(8, 0), (8, 1)]
+VECTOR_PARTS = [(16, 0), (8, 0), (8, 1), (4, 0), (4, 1), (4, 2), (4, 3), (2, 0), (2, 1), (1, 0)]
+GPSIMD_PARTS = [(16, 1)]
 GRAM_COLS = P + 2
 DIAG = DIM + 1
 
@@ -55,12 +55,13 @@ def tile_taylorsoftmaxattention_pa_kernel(tc, x, Wk, bk, Wv, bv, out_0, out_1, o
     with ExitStack() as ctx:
         keep = ctx.enter_context(tc.tile_pool(name="keep", bufs=1))
         prep = ctx.enter_context(tc.tile_pool(name="prep", bufs=2))
+        ahead = ctx.enter_context(tc.tile_pool(name="ahead", bufs=3))
         prod = ctx.enter_context(tc.tile_pool(name="prod", bufs=2))
         done = ctx.enter_context(tc.tile_pool(name="done", bufs=2))
-        psum_acc = ctx.enter_context(tc.psum_pool(name="psum_acc", bufs=1))
+        psum_acc = ctx.enter_context(tc.psum_pool(name="psum_acc", bufs=2))
         psum_gram = ctx.enter_context(tc.psum_pool(name="psum_gram", bufs=1))
-        psum_k = ctx.enter_context(tc.psum_pool(name="psum_k", bufs=2))
-        psum_work = ctx.enter_context(tc.psum_pool(name="psum_work", bufs=1))
+        psum_k = ctx.enter_context(tc.psum_pool(name="psum_k", bufs=3))
+        psum_work = ctx.enter_context(tc.psum_pool(name="psum_work", bufs=2))
         ctx.enter_context(tc.manual_schedule())
 
         w_raw = keep.tile([P, GROUPS, 2, CHANNELS], BF16)
@@ -117,7 +118,7 @@ def tile_taylorsoftmaxattention_pa_kernel(tc, x, Wk, bk, Wv, bv, out_0, out_1, o
         bias_cols = keep.tile([P, 2 * GROUPS], F32)
 
         w_grouped, x_grouped = {}, {}
-        k_feat, v_feat, k_tok, factor, factor_squared = {}, {}, {}, {}, {}
+        k_sums, v_sum_bank, k_feat, v_feat, k_tok, v_tok, norms, factor, factor_squared = {}, {}, {}, {}, {}, {}, {}, {}, {}
         k_packed, w_packed, first_bf, v_bf = {}, {}, {}, {}
         v_codes, v_scales, first_codes, first_scales, kk_codes, kk_scales = {}, {}, {}, {}, {}, {}
         acc, first, gram, v_sums, stage, by_pair, by_square, square, turned_square = {}, {}, {}, {}, {}, {}, {}, {}, {}
@@ -150,7 +151,7 @@ def tile_taylorsoftmaxattention_pa_kernel(tc, x, Wk, bk, Wv, bv, out_0, out_1, o
             x_grouped[c] = prep.tile([P, K_PASS, PACK], BF16, name="x_grouped", align_bytes=64)
             pairs = x_grouped[c][:].bitcast(F32).rearrange("p (j n) u -> p j n u", j=PACK)
             for half in range(2):
-                turned = psum_acc.tile([P, 2, 2, P], F32, name="x_turned", tag="acc%d" % ((2 * c + half) % CHUNKS))
+                turned = psum_acc.tile([P, 2, 2, P], F32, name="x_turned", tag="acc")
                 for j in range(2):
                     for u in range(2):
                         nc.tensor.transpose(
@@ -182,50 +183,63 @@ def tile_taylorsoftmaxattention_pa_kernel(tc, x, Wk, bk, Wv, bv, out_0, out_1, o
                 stop=True,
             )
 
-        def start(step):
-            g, c = divmod(step, BLOCKS)
-            k_sums = psum_k.tile([P, K_PASS], F32, name="k_sums", tag="k")
-            project(k_sums[:], 0, step)
-            v_sum_bank = psum_work.tile([P, K_PASS], F32, name="v_sum_bank", tag="work")
-            project(v_sum_bank[:], 1, step)
+        def project_k(step):
+            k_sums[step] = psum_work.tile([P, K_PASS], F32, name="k_sums", tag="work")
+            project(k_sums[step][:], 0, step)
+
+        def project_v(step):
+            v_sum_bank[step] = psum_work.tile([P, K_PASS], F32, name="v_sum_bank", tag="work")
+            project(v_sum_bank[step][:], 1, step)
+
+        def empty_k(step):
+            g = step // BLOCKS
             k_feat[step] = prep.tile([P, K_PASS], F32, name="k_feat")
             nc.scalar.activation(
                 out=k_feat[step][:].rearrange("p (u e n) -> p u e n", u=2, e=2),
-                in_=k_sums[:].rearrange("p (u n e) -> p u e n", u=2, e=2),
+                in_=k_sums[step][:].rearrange("p (u n e) -> p u e n", u=2, e=2),
                 func=ACT.Identity,
                 bias=bias_cols[:, g : g + 1],
                 scale=1.0,
             )
+
+        def empty_v(step):
+            g, c = divmod(step, BLOCKS)
             if c == 0:
-                v_sums[g] = prep.tile([P, BLOCKS], F32, name="v_sums")
+                v_sums[g] = ahead.tile([P, BLOCKS], F32, name="v_sums")
             v_feat[step] = prep.tile([P, K_PASS], BF16, name="v_feat")
             nc.scalar.activation(
                 out=v_feat[step][:],
-                in_=v_sum_bank[:],
+                in_=v_sum_bank[step][:],
                 func=ACT.Identity,
                 bias=bias_cols[:, GROUPS + g : GROUPS + g + 1],
                 scale=1.0 / TOKENS,
                 accum_out=v_sums[g][:, c : c + 1],
             )
 
-        def turn(step):
+        def turn_k(step):
             k_tok[step] = psum_k.tile([P, P, PACK], F32, name="k_tok", tag="k")
             for t in range(PACK):
                 nc.tensor.transpose(out=k_tok[step][:, :, t], in_=k_feat[step][:, t * P : (t + 1) * P], identity=ident_by_feature[:])
-            v_tok = psum_work.tile([P, 2, P], F32, name="v_tok", tag="work")
+
+        def turn_v(step):
+            v_tok[step] = psum_work.tile([P, 2, P], F32, name="v_tok", tag="work")
             v_words = v_feat[step][:].bitcast(F32)
             for u in range(2):
-                nc.tensor.transpose(out=v_tok[:, u, :], in_=v_words[:, u * P : (u + 1) * P], identity=ident[:])
+                nc.tensor.transpose(out=v_tok[step][:, u, :], in_=v_words[:, u * P : (u + 1) * P], identity=ident[:])
+
+        def add_squares(step):
             squares = prep.tile([P, CELL, DIM], F32)
-            norms = prep.tile([P, CELL], F32)
+            norms[step] = prep.tile([P, CELL], F32, name="norms")
             k_cells = by_cell(k_tok[step])
             for x in range(CELL):
-                nc.scalar.activation(out=squares[:, x, :], in_=k_cells[:, :, x], func=ACT.Square, accum_out=norms[:, x : x + 1])
+                nc.scalar.activation(out=squares[:, x, :], in_=k_cells[:, :, x], func=ACT.Square, accum_out=norms[step][:, x : x + 1])
+
+        def make_factor(step):
             above_floor = prep.tile([P, CELL], F32)
-            nc.scalar.activation(out=above_floor[:], in_=norms[:], func=ACT.Relu, bias=minus_floor[:], scale=1.0)
-            v_bf[step] = prep.tile([P, P, PACK], BF16, name="v_bf", align_bytes=64)
-            nc.scalar.copy(out=v_bf[step][:].bitcast(F32), in_=v_tok[:].rearrange("p u f -> p f u"))
-            factor[step] = prep.tile([P, CELL], F32, name="factor")
+            nc.scalar.activation(out=above_floor[:], in_=norms[step][:], func=ACT.Relu, bias=minus_floor[:], scale=1.0)
+            v_bf[step] = ahead.tile([P, P, PACK], BF16, name="v_bf", align_bytes=64)
+            nc.scalar.copy(out=v_bf[step][:].bitcast(F32), in_=v_tok[step][:].rearrange("p u f -> p f u"))
+            factor[step] = ahead.tile([P, CELL], F32, name="factor")
             nc.scalar.activation(
                 out=factor[step][:],
                 in_=above_floor[:],
@@ -233,9 +247,9 @@ def tile_taylorsoftmaxattention_pa_kernel(tc, x, Wk, bk, Wv, bv, out_0, out_1, o
                 bias=scaled_floor[:],
                 scale=1.0 / (SCALE * SCALE),
             )
-            k_packed[step] = prep.tile([P, DIM, CELL], F32, name="k_packed")
-            nc.scalar.copy(out=k_packed[step][:], in_=k_cells)
-            factor_squared[step] = prep.tile([P, CELL], F32, name="factor_squared")
+            k_packed[step] = ahead.tile([P, DIM, CELL], F32, name="k_packed")
+            nc.scalar.copy(out=k_packed[step][:], in_=by_cell(k_tok[step]))
+            factor_squared[step] = ahead.tile([P, CELL], F32, name="factor_squared")
             nc.scalar.activation(out=factor_squared[step][:], in_=factor[step][:], func=ACT.Square)
 
         def by_cell(tile):
@@ -263,7 +277,7 @@ def tile_taylorsoftmaxattention_pa_kernel(tc, x, Wk, bk, Wv, bv, out_0, out_1, o
                     )
 
         def make_first(step):
-            first_bf[step] = prep.tile([P, 2, P, PACK], BF16, name="first_bf", align_bytes=64)
+            first_bf[step] = ahead.tile([P, 2, P, PACK], BF16, name="first_bf", align_bytes=64)
             kn_words = kn_rows[step % 2][:, :, 0:P].rearrange("p t (f r) -> p f t r", r=4)
             first_words = first_bf[step][:].rearrange("p s (f r) t -> p s f t r", r=4)
             nc.scalar.copy(out=first_words[:, 0], in_=kn_words)
@@ -297,15 +311,20 @@ def tile_taylorsoftmaxattention_pa_kernel(tc, x, Wk, bk, Wv, bv, out_0, out_1, o
                 (nc.gpsimd, k_packed[step][:], GPSIMD_PARTS),
             ]:
                 for span, part in parts:
-                    if span >= 8:
+                    if span == 16:
+                        shape = [P, 8, 16, CELL]
+                        slot = FIRST_PAIR[16, part]
+                        left = k[:, 8 * part : 8 * part + 8, :].unsqueeze(2)
+                        right = w[:, 16:32, :].unsqueeze(1)
+                    elif span == 8:
                         shape = [P, span, span, CELL]
-                        slot = FIRST_PAIR[span] + part * span * span
+                        slot = FIRST_PAIR[span, 0] + part * span * span
                         low = part * 2 * span
                         left = k[:, low : low + span, :].unsqueeze(2)
                         right = w[:, low + span : low + 2 * span, :].unsqueeze(1)
                     else:
                         shape = [P, DIM // (2 * span), span, CELL]
-                        slot = FIRST_PAIR[span] + part * (DIM // 2)
+                        slot = FIRST_PAIR[span, 0] + part * (DIM // 2)
                         left = k.rearrange("p (b r) x -> p b r x", r=2 * span)[:, :, part, :].unsqueeze(2)
                         right = w.rearrange("p (b r) x -> p b r x", r=2 * span)[:, :, span : 2 * span, :]
                     out = kk_bf[:, slot : slot + shape[1] * span, :].rearrange("p (a j) x -> p a j x", j=span)
@@ -318,6 +337,8 @@ def tile_taylorsoftmaxattention_pa_kernel(tc, x, Wk, bk, Wv, bv, out_0, out_1, o
                 v_scales[g] = prod.tile([P, BLOCKS, P], U8, name="v_scales", align_bytes=64)
                 first_codes[g] = prod.tile([P, BLOCKS, 2 * P], U32, name="first_codes", align_bytes=64)
                 first_scales[g] = prod.tile([P, BLOCKS, 2 * P], U8, name="first_scales", align_bytes=64)
+                kk_codes[g] = prod.tile([P, BLOCKS, PAIR_SLOTS * GROUP_HEADS], U32, name="kk_codes", align_bytes=64)
+                kk_scales[g] = prod.tile([P, BLOCKS, PAIR_SLOTS * GROUP_HEADS], U8, name="kk_scales", align_bytes=64)
             nc.vector.quantize_mx(
                 out=v_codes[g][:, c, :].bitcast(FP8X4), scales=v_scales[g][:, c, :], in_=v_bf[step][:].rearrange("p f t -> p (f t)")
             )
@@ -326,43 +347,43 @@ def tile_taylorsoftmaxattention_pa_kernel(tc, x, Wk, bk, Wv, bv, out_0, out_1, o
                 scales=first_scales[g][:, c, :],
                 in_=first_bf[step][:].rearrange("p s f t -> p (s f t)"),
             )
-            kk_codes[step] = prod.tile([P, PAIR_SLOTS * GROUP_HEADS], U32, name="kk_codes", align_bytes=64)
-            kk_scales[step] = prod.tile([P, PAIR_SLOTS * GROUP_HEADS], U8, name="kk_scales", align_bytes=64)
             width = CHUNK if step == STEPS - 1 else HALF
             for pairs in [slice(p, p + width) for p in range(0, PAIR_SLOTS, width)]:
+                if c == 0 and g + 1 < GROUPS and pairs.stop == PAIR_SLOTS:
+                    quantise_weights(g + 1)
                 columns = slice(pairs.start * GROUP_HEADS, pairs.stop * GROUP_HEADS)
                 nc.vector.quantize_mx(
-                    out=kk_codes[step][:, columns].bitcast(FP8X4),
-                    scales=kk_scales[step][:, columns],
+                    out=kk_codes[g][:, c, columns].bitcast(FP8X4),
+                    scales=kk_scales[g][:, c, columns],
                     in_=kk_bf[:, pairs, :].rearrange("p q x -> p (q x)"),
                 )
 
-        def contract(step):
-            g, c = divmod(step, BLOCKS)
-            if c == BLOCKS - 1:
-                first[g] = psum_work.tile([P, 2 * P], F32, name="first", tag="work")
-                for b in range(BLOCKS):
-                    nc.tensor.matmul_mx(
-                        out=first[g][:],
-                        lhsT=v_codes[g][:, b, :].bitcast(FP8X4),
-                        lhsT_scale=v_scales[g][:, b, :],
-                        rhs=first_codes[g][:, b, :].bitcast(FP8X4),
-                        rhs_scale=first_scales[g][:, b, :],
-                        start=(b == 0),
-                        stop=(b == BLOCKS - 1),
-                    )
-            for chunk in range(CHUNKS):
-                columns = slice(chunk * CHUNK * GROUP_HEADS, (chunk + 1) * CHUNK * GROUP_HEADS)
-                if c == 0:
-                    acc[chunk] = psum_acc.tile([P, CHUNK * GROUP_HEADS], F32, name="acc", tag="acc%d" % chunk)
+        def contract_first(g, blocks):
+            if blocks.start == 0:
+                pool, tag = (psum_acc, "acc") if g < GROUPS - 1 else (psum_work, "work")
+                first[g] = pool.tile([P, 2 * P], F32, name="first", tag=tag)
+            for b in blocks:
+                nc.tensor.matmul_mx(
+                    out=first[g][:],
+                    lhsT=v_codes[g][:, b, :].bitcast(FP8X4),
+                    lhsT_scale=v_scales[g][:, b, :],
+                    rhs=first_codes[g][:, b, :].bitcast(FP8X4),
+                    rhs_scale=first_scales[g][:, b, :],
+                    start=(b == 0),
+                    stop=(b == BLOCKS - 1),
+                )
+
+        def contract(g, chunk, blocks):
+            columns = slice(chunk * CHUNK * GROUP_HEADS, (chunk + 1) * CHUNK * GROUP_HEADS)
+            for b in blocks:
                 nc.tensor.matmul_mx(
                     out=acc[chunk][:],
-                    lhsT=v_codes[g][:, c, :].bitcast(FP8X4),
-                    lhsT_scale=v_scales[g][:, c, :],
-                    rhs=kk_codes[step][:, columns].bitcast(FP8X4),
-                    rhs_scale=kk_scales[step][:, columns],
-                    start=(c == 0),
-                    stop=(c == BLOCKS - 1),
+                    lhsT=v_codes[g][:, b, :].bitcast(FP8X4),
+                    lhsT_scale=v_scales[g][:, b, :],
+                    rhs=kk_codes[g][:, b, columns].bitcast(FP8X4),
+                    rhs_scale=kk_scales[g][:, b, columns],
+                    start=(b == 0),
+                    stop=(b == BLOCKS - 1),
                 )
 
         def collect_first(g):
@@ -383,12 +404,18 @@ def tile_taylorsoftmaxattention_pa_kernel(tc, x, Wk, bk, Wv, bv, out_0, out_1, o
                 rows = slice(h * DIM, (h + 1) * DIM)
                 copy(out=by_pair[g][rows, chunk * CHUNK : (chunk + 1) * CHUNK], in_=sums[rows, h, :])
 
-        def lay(g, span, copy):
-            if span == SPANS[0]:
+        def lay(g, span, half, copy):
+            if (span, half) == (16, 0):
                 square[g] = done.tile([P, DIM * DIAG], F32, name="square", align_bytes=64)
+            if span == 16:
+                sums = by_pair[g][:, FIRST_PAIR[16, half] : FIRST_PAIR[16, half] + 128].rearrange("p (i j) -> p i j", i=8)
+                rows = square[g][:].rearrange("p (i r) -> p i r", r=DIM)
+                copy(out=rows[:, 8 * half : 8 * half + 8, 16:32], in_=sums)
+                copy(out=rows[:, 16:32, 8 * half : 8 * half + 8], in_=sums.rearrange("p i j -> p j i"))
+                return
             spans = DIM // (2 * span)
             order = "p (b i j) -> p b i j" if span >= 8 else "p (i b j) -> p b i j"
-            sums = by_pair[g][:, FIRST_PAIR[span] : FIRST_PAIR[span] + DIM // 2 * span].rearrange(order, b=spans, i=span)
+            sums = by_pair[g][:, FIRST_PAIR[span, 0] : FIRST_PAIR[span, 0] + DIM // 2 * span].rearrange(order, b=spans, i=span)
             cells = square[g][:].rearrange("p (b w) -> p b w", b=spans)
             upper = cells[:, :, span : span + span * DIM].rearrange("p b (i r) -> p b i r", r=DIM)[:, :, :, 0:span]
             lower = cells[:, :, span * DIM : 2 * span * DIM].rearrange("p b (j r) -> p b j r", r=DIM)[:, :, :, 0:span]
@@ -413,72 +440,121 @@ def tile_taylorsoftmaxattention_pa_kernel(tc, x, Wk, bk, Wv, bv, out_0, out_1, o
                 out=kv_mod_rows[g][:, rows.start * OUT_DIM : rows.stop * OUT_DIM], in_=stage[g][:, rows, :].rearrange("p w e -> p (w e)")
             )
 
+        all_blocks = range(BLOCKS)
         turn_tokens(0)
         turn_weights(0)
         turn_biases()
         quantise_tokens(0)
         quantise_weights(0)
         turn_tokens(1)
-        start(0)
+        project_k(0)
+        project_v(0)
+        empty_k(0)
+        empty_v(0)
+        turn_k(0)
+        turn_v(0)
         quantise_tokens(1)
         turn_tokens(2)
-        turn(0)
+        add_squares(0)
+        make_factor(0)
         quantise_tokens(2)
-        normalise(0)
         turn_tokens(3)
         quantise_tokens(3)
         make_w(0, nc.vector)
-        start(1)
-        turn(1)
+        project_k(1)
+        project_v(1)
+        empty_k(1)
+        empty_v(1)
+        turn_k(1)
+        turn_v(1)
+        normalise(0)
+        add_squares(1)
+        make_factor(1)
+        turn_weights(1)
         make_first(0)
         add_gram(0)
+        project_k(2)
+        empty_k(2)
+        turn_k(2)
+        project_v(2)
         normalise(1)
-        make_first(1)
+        empty_v(2)
         add_gram(1)
+        turn_v(2)
+        make_first(1)
 
         for step in range(STEPS):
             g, c = divmod(step, BLOCKS)
             last_group = g == GROUPS - 1
             multiply(step)
-            if step + 1 < STEPS:
-                make_w(step + 1, nc.gpsimd)
-            if c == 0 and not last_group:
-                turn_weights(g + 1)
-            quantise(step)
-            if c == 1 and not last_group:
-                quantise_weights(g + 1)
-            if step + 2 < STEPS:
-                start(step + 2)
-                turn(step + 2)
-            contract(step)
-            if step + 2 < STEPS:
-                normalise(step + 2)
-                make_first(step + 2)
-                add_gram(step + 2)
-            if c == 1:
-                collect_gram(g)
-            if c == BLOCKS - 1 and not last_group:
-                collect_first(g)
-                for chunk in range(CHUNKS):
-                    collect(g, chunk, nc.scalar.copy)
-            if c == 0 and g > 0:
-                for span in SPANS:
-                    lay(g - 1, span, nc.scalar.copy)
-                lay_diagonal(g - 1)
-            if c == 2 and g > 0:
+            if step == STEPS - 1:
                 turn_square(g - 1, 0, 1)
                 store(g - 1, 0, 1)
+            if step + 1 < STEPS:
+                make_w(step + 1, nc.gpsimd)
+            quantise(step)
+            if step + 3 < STEPS:
+                project_k(step + 3)
+            if g > 0 and c < 2:
+                for chunk in (2 * c, 2 * c + 1):
+                    acc[chunk] = psum_acc.tile([P, CHUNK * GROUP_HEADS], F32, name="acc", tag="acc")
+                    contract(g - 1, chunk, all_blocks)
+            if g > 0 and c == 2:
+                contract_first(g - 1, all_blocks)
+            if step + 2 < STEPS:
+                add_squares(step + 2)
+            if step + 3 < STEPS:
+                empty_k(step + 3)
+                turn_k(step + 3)
+            if step + 2 < STEPS:
+                make_factor(step + 2)
+            if step + 3 < STEPS:
+                project_v(step + 3)
+            if step + 2 < STEPS:
+                normalise(step + 2)
+                add_gram(step + 2)
+            if step + 3 < STEPS:
+                empty_v(step + 3)
+                turn_v(step + 3)
+            if step + 2 < STEPS:
+                make_first(step + 2)
+            if c == 1:
+                collect_gram(g)
+            if g > 0 and c < 2:
+                for chunk in (2 * c, 2 * c + 1):
+                    collect(g - 1, chunk, nc.scalar.copy)
+            if g > 0 and c == 2:
+                collect_first(g - 1)
+                for span, half in SPANS:
+                    lay(g - 1, span, half, nc.scalar.copy)
+                lay_diagonal(g - 1)
+            if c == 3 and g < GROUPS - 2:
+                turn_weights(g + 2)
+            if step == STEPS - 2:
+                for chunk in range(CHUNKS):
+                    pool, tag = (psum_acc, "acc") if chunk < 2 else (psum_k, "k")
+                    acc[chunk] = pool.tile([P, CHUNK * GROUP_HEADS], F32, name="acc", tag=tag)
+                    contract(g, chunk, range(0, BLOCKS - 1))
+            if c == 0 and g > 1:
+                turn_square(g - 2, 0, 1)
+                store(g - 2, 0, 1)
+        g = GROUPS - 1
+        contract_first(g, all_blocks)
+        for chunk in range(CHUNKS):
+            contract(g, chunk, range(BLOCKS - 1, BLOCKS))
 
         g = GROUPS - 1
         collect_first(g)
         nc.vector.transpose(out=small_turned[:].rearrange("p g s e -> p (g s e)"), in_=small[:].rearrange("p g s d -> p (g s d)"))
         collect(g, 0, nc.scalar.copy)
-        collect(g, 1, nc.scalar.copy)
-        lay(g, 16, nc.scalar.copy)
-        collect(g, 2, nc.vector.tensor_copy)
+        lay(g, 16, 0, nc.scalar.copy)
+        collect(g, 1, nc.vector.tensor_copy)
+        collect(g, 2, nc.scalar.copy)
+        lay(g, 16, 1, nc.scalar.copy)
+        lay(g, 8, 0, nc.vector.tensor_copy)
         collect(g, 3, nc.vector.tensor_copy)
-        for span in [8, 4, 2, 1]:
-            lay(g, span, nc.vector.tensor_copy)
+        for span in [4, 2, 1]:
+            lay(g, span, 0, nc.vector.tensor_copy)
         lay_diagonal(g)
         nc.scalar.copy(out=kv_stage[:, :, 1:OUT_DIM], in_=small_turned[:, :, 0, :])
         nc.sync.dma_start(out=kv_rows, in_=kv_stage[:])

@@ -69,9 +69,8 @@ def tile_taylorsoftmaxattention_pa_kernel(tc, x, Wk, bk, Wv, bv, out_0, out_1, o
         bias_rows = keep.tile([2 * GROUPS, P], BF16)
         nc.scalar.dma_start(out=bias_rows[0:GROUPS, :], in_=bk.rearrange("(g f) -> g f", g=GROUPS))
         nc.scalar.dma_start(out=bias_rows[GROUPS : 2 * GROUPS, :], in_=bv.rearrange("(g f) -> g f", g=GROUPS))
-        for half in range(2):
-            rows = slice(2 * half, 2 * half + 2)
-            nc.sync.dma_start(out=x_raw[:, rows, :], in_=x_rows[:, rows, :])
+        for j in range(PACK):
+            nc.sync.dma_start(out=x_raw[:, j : j + 1, :], in_=x_rows[:, j : j + 1, :])
         nc.sync.dma_start(out=w_raw[:, 0, 0, :], in_=wk_rows[:, 0, :])
         nc.sync.dma_start(out=w_raw[:, 0, 1, :], in_=wv_rows[:, 0, :])
         for c in range(1, BLOCKS):
@@ -124,7 +123,8 @@ def tile_taylorsoftmaxattention_pa_kernel(tc, x, Wk, bk, Wv, bv, out_0, out_1, o
         acc, first, gram, v_sums, stage, by_pair, by_square, square, turned_square = {}, {}, {}, {}, {}, {}, {}, {}, {}
 
         def turn_weights(g):
-            turned = psum_work.tile([P, 2, 2, P], F32, tag="work")
+            pool, tag = (psum_k, "k") if g == 0 else (psum_work, "work")
+            turned = pool.tile([P, 2, 2, P], F32, name="w_turned", tag=tag)
             for m in range(2):
                 for u in range(2):
                     nc.tensor.transpose(out=turned[:, m, u, :], in_=w_words[:, g, m, u * P : (u + 1) * P], identity=ident[:])
@@ -147,7 +147,26 @@ def tile_taylorsoftmaxattention_pa_kernel(tc, x, Wk, bk, Wv, bv, out_0, out_1, o
             nc.scalar.copy(out=bias_cols[:, 0:GROUPS], in_=bias_turned[:, 0:GROUPS])
             nc.scalar.mul(out=bias_cols[:, GROUPS : 2 * GROUPS], in_=bias_turned[:, GROUPS : 2 * GROUPS], mul=1.0 / TOKENS)
 
-        def turn_tokens(c):
+        def turn_first_tokens():
+            x_grouped[0] = prep.tile([P, K_PASS, PACK], BF16, name="x_grouped", align_bytes=64)
+            pairs = x_grouped[0][:].bitcast(F32).rearrange("p (j n) u -> p j n u", j=PACK)
+            for j in range(PACK):
+                pool, tag = (psum_acc, "acc") if j < 2 else (psum_work, "work")
+                turned = pool.tile([P, 2, P], F32, name="x_first_turned", tag=tag)
+                for u in range(2):
+                    nc.tensor.transpose(out=turned[:, u, :], in_=x_words[:, j, u * P : (u + 1) * P], identity=ident[:])
+                copy = nc.vector.tensor_copy if j % 2 == 0 else nc.scalar.copy
+                copy(out=pairs[:, j, :, :], in_=turned[:].rearrange("p u n -> p n u"))
+
+        def quantise_first_tokens(half):
+            tokens = slice(half * K_PASS // 2, (half + 1) * K_PASS // 2)
+            nc.vector.quantize_mx(
+                out=x_codes[:, tokens].bitcast(FP8X4),
+                scales=x_scales[:, tokens],
+                in_=x_grouped[0][:, tokens, :].rearrange("p n k -> p (n k)"),
+            )
+
+        def turn_tokens(c, copy):
             x_grouped[c] = prep.tile([P, K_PASS, PACK], BF16, name="x_grouped", align_bytes=64)
             pairs = x_grouped[c][:].bitcast(F32).rearrange("p (j n) u -> p j n u", j=PACK)
             for half in range(2):
@@ -159,7 +178,6 @@ def tile_taylorsoftmaxattention_pa_kernel(tc, x, Wk, bk, Wv, bv, out_0, out_1, o
                             in_=x_words[:, PACK * c + 2 * half + j, u * P : (u + 1) * P],
                             identity=ident[:],
                         )
-                copy = nc.scalar.copy if c == 0 and half == 1 else nc.vector.tensor_copy
                 copy(out=pairs[:, 2 * half : 2 * half + 2, :, :], in_=turned[:].rearrange("p j u n -> p j n u"))
 
         def quantise_tokens(c):
@@ -248,18 +266,21 @@ def tile_taylorsoftmaxattention_pa_kernel(tc, x, Wk, bk, Wv, bv, out_0, out_1, o
                 scale=1.0 / (SCALE * SCALE),
             )
             k_packed[step] = ahead.tile([P, DIM, CELL], F32, name="k_packed")
-            nc.scalar.copy(out=k_packed[step][:], in_=by_cell(k_tok[step]))
             factor_squared[step] = ahead.tile([P, CELL], F32, name="factor_squared")
+            if step > 0:
+                nc.scalar.copy(out=k_packed[step][:], in_=by_cell(k_tok[step]))
             nc.scalar.activation(out=factor_squared[step][:], in_=factor[step][:], func=ACT.Square)
+            if step == 0:
+                nc.scalar.copy(out=k_packed[step][:], in_=by_cell(k_tok[step]))
 
         def by_cell(tile):
             return tile[:].rearrange("p (d h) t -> p d (h t)", h=GROUP_HEADS)
 
-        def make_w(step, engine):
+        def make_w(step, engine, k_cells):
             w_packed[step] = prep.tile([P, DIM, CELL], F32, name="w_packed")
             engine.tensor_tensor(
                 out=w_packed[step][:],
-                in0=k_packed[step][:],
+                in0=k_cells,
                 in1=factor_squared[step][:].unsqueeze(1).to_broadcast([P, DIM, CELL]),
                 op=ALU.mult,
             )
@@ -304,65 +325,61 @@ def tile_taylorsoftmaxattention_pa_kernel(tc, x, Wk, bk, Wv, bv, out_0, out_1, o
                 nc.scalar.mul(out=stage[g][rows, :, 0], in_=gram[g][rows, h * DIM : (h + 1) * DIM], mul=1.0 / TOKENS)
             nc.scalar.mul(out=kv_stage[:, g, 0:1], in_=gram[g][:, P : P + 1], mul=1.0 / TOKENS)
 
-        def multiply(step):
+        def multiply(step, engine, k, parts):
             w = w_packed[step][:]
-            for engine, k, parts in [
-                (nc.vector, by_cell(k_tok[step]), VECTOR_PARTS),
-                (nc.gpsimd, k_packed[step][:], GPSIMD_PARTS),
-            ]:
-                for span, part in parts:
-                    if span == 16:
-                        shape = [P, 8, 16, CELL]
-                        slot = FIRST_PAIR[16, part]
-                        left = k[:, 8 * part : 8 * part + 8, :].unsqueeze(2)
-                        right = w[:, 16:32, :].unsqueeze(1)
-                    elif span == 8:
-                        shape = [P, span, span, CELL]
-                        slot = FIRST_PAIR[span, 0] + part * span * span
-                        low = part * 2 * span
-                        left = k[:, low : low + span, :].unsqueeze(2)
-                        right = w[:, low + span : low + 2 * span, :].unsqueeze(1)
-                    else:
-                        shape = [P, DIM // (2 * span), span, CELL]
-                        slot = FIRST_PAIR[span, 0] + part * (DIM // 2)
-                        left = k.rearrange("p (b r) x -> p b r x", r=2 * span)[:, :, part, :].unsqueeze(2)
-                        right = w.rearrange("p (b r) x -> p b r x", r=2 * span)[:, :, span : 2 * span, :]
-                    out = kk_bf[:, slot : slot + shape[1] * span, :].rearrange("p (a j) x -> p a j x", j=span)
-                    engine.tensor_tensor(out=out, in0=left.to_broadcast(shape), in1=right.to_broadcast(shape), op=ALU.mult)
+            for span, part in parts:
+                if span == 16:
+                    shape = [P, 8, 16, CELL]
+                    slot = FIRST_PAIR[16, part]
+                    left = k[:, 8 * part : 8 * part + 8, :].unsqueeze(2)
+                    right = w[:, 16:32, :].unsqueeze(1)
+                elif span == 8:
+                    shape = [P, span, span, CELL]
+                    slot = FIRST_PAIR[span, 0] + part * span * span
+                    low = part * 2 * span
+                    left = k[:, low : low + span, :].unsqueeze(2)
+                    right = w[:, low + span : low + 2 * span, :].unsqueeze(1)
+                else:
+                    shape = [P, DIM // (2 * span), span, CELL]
+                    slot = FIRST_PAIR[span, 0] + part * (DIM // 2)
+                    left = k.rearrange("p (b r) x -> p b r x", r=2 * span)[:, :, part, :].unsqueeze(2)
+                    right = w.rearrange("p (b r) x -> p b r x", r=2 * span)[:, :, span : 2 * span, :]
+                out = kk_bf[:, slot : slot + shape[1] * span, :].rearrange("p (a j) x -> p a j x", j=span)
+                engine.tensor_tensor(out=out, in0=left.to_broadcast(shape), in1=right.to_broadcast(shape), op=ALU.mult)
 
-        def quantise(step):
+        def open_codes(g):
+            v_codes[g] = prod.tile([P, BLOCKS, P], U32, name="v_codes", align_bytes=64)
+            v_scales[g] = prod.tile([P, BLOCKS, P], U8, name="v_scales", align_bytes=64)
+            first_codes[g] = prod.tile([P, BLOCKS, 2 * P], U32, name="first_codes", align_bytes=64)
+            first_scales[g] = prod.tile([P, BLOCKS, 2 * P], U8, name="first_scales", align_bytes=64)
+            kk_codes[g] = prod.tile([P, BLOCKS, PAIR_SLOTS * GROUP_HEADS], U32, name="kk_codes", align_bytes=64)
+            kk_scales[g] = prod.tile([P, BLOCKS, PAIR_SLOTS * GROUP_HEADS], U8, name="kk_scales", align_bytes=64)
+
+        def quantise_v(step):
             g, c = divmod(step, BLOCKS)
-            if c == 0:
-                v_codes[g] = prod.tile([P, BLOCKS, P], U32, name="v_codes", align_bytes=64)
-                v_scales[g] = prod.tile([P, BLOCKS, P], U8, name="v_scales", align_bytes=64)
-                first_codes[g] = prod.tile([P, BLOCKS, 2 * P], U32, name="first_codes", align_bytes=64)
-                first_scales[g] = prod.tile([P, BLOCKS, 2 * P], U8, name="first_scales", align_bytes=64)
-                kk_codes[g] = prod.tile([P, BLOCKS, PAIR_SLOTS * GROUP_HEADS], U32, name="kk_codes", align_bytes=64)
-                kk_scales[g] = prod.tile([P, BLOCKS, PAIR_SLOTS * GROUP_HEADS], U8, name="kk_scales", align_bytes=64)
             nc.vector.quantize_mx(
                 out=v_codes[g][:, c, :].bitcast(FP8X4), scales=v_scales[g][:, c, :], in_=v_bf[step][:].rearrange("p f t -> p (f t)")
             )
+
+        def quantise_first(step):
+            g, c = divmod(step, BLOCKS)
             nc.vector.quantize_mx(
                 out=first_codes[g][:, c, :].bitcast(FP8X4),
                 scales=first_scales[g][:, c, :],
                 in_=first_bf[step][:].rearrange("p s f t -> p (s f t)"),
             )
-            width = CHUNK if step == STEPS - 1 else HALF
-            for pairs in [slice(p, p + width) for p in range(0, PAIR_SLOTS, width)]:
-                if c == 0 and g + 1 < GROUPS and pairs.stop == PAIR_SLOTS:
-                    quantise_weights(g + 1)
-                columns = slice(pairs.start * GROUP_HEADS, pairs.stop * GROUP_HEADS)
-                nc.vector.quantize_mx(
-                    out=kk_codes[g][:, c, columns].bitcast(FP8X4),
-                    scales=kk_scales[g][:, c, columns],
-                    in_=kk_bf[:, pairs, :].rearrange("p q x -> p (q x)"),
-                )
 
-        def contract_first(g, blocks):
-            if blocks.start == 0:
-                pool, tag = (psum_acc, "acc") if g < GROUPS - 1 else (psum_work, "work")
-                first[g] = pool.tile([P, 2 * P], F32, name="first", tag=tag)
-            for b in blocks:
+        def quantise_pairs(step, pairs):
+            g, c = divmod(step, BLOCKS)
+            columns = slice(pairs.start * GROUP_HEADS, pairs.stop * GROUP_HEADS)
+            nc.vector.quantize_mx(
+                out=kk_codes[g][:, c, columns].bitcast(FP8X4),
+                scales=kk_scales[g][:, c, columns],
+                in_=kk_bf[:, pairs, :].rearrange("p q x -> p (q x)"),
+            )
+
+        def contract_first(g):
+            for b in range(BLOCKS):
                 nc.tensor.matmul_mx(
                     out=first[g][:],
                     lhsT=v_codes[g][:, b, :].bitcast(FP8X4),
@@ -433,20 +450,21 @@ def tile_taylorsoftmaxattention_pa_kernel(tc, x, Wk, bk, Wv, bv, out_0, out_1, o
                 out=turned_square[g][:, rows, :].rearrange("p w e -> p (w e)"), in_=square[g][:, rows.start * DIM : rows.stop * DIM]
             )
 
-        def store(g, part, parts):
+        def store(g, part, parts, copy):
             rows = slice(part * DIM // parts, (part + 1) * DIM // parts)
-            nc.scalar.copy(out=stage[g][:, rows, 1:OUT_DIM], in_=turned_square[g][:, rows, :])
+            copy(out=stage[g][:, rows, 1:OUT_DIM], in_=turned_square[g][:, rows, :])
             nc.sync.dma_start(
                 out=kv_mod_rows[g][:, rows.start * OUT_DIM : rows.stop * OUT_DIM], in_=stage[g][:, rows, :].rearrange("p w e -> p (w e)")
             )
 
         all_blocks = range(BLOCKS)
-        turn_tokens(0)
+        turn_first_tokens()
         turn_weights(0)
         turn_biases()
-        quantise_tokens(0)
+        quantise_first_tokens(0)
+        quantise_first_tokens(1)
         quantise_weights(0)
-        turn_tokens(1)
+        turn_tokens(1, nc.vector.tensor_copy)
         project_k(0)
         project_v(0)
         empty_k(0)
@@ -454,13 +472,11 @@ def tile_taylorsoftmaxattention_pa_kernel(tc, x, Wk, bk, Wv, bv, out_0, out_1, o
         turn_k(0)
         turn_v(0)
         quantise_tokens(1)
-        turn_tokens(2)
+        turn_tokens(2, nc.vector.tensor_copy)
         add_squares(0)
         make_factor(0)
         quantise_tokens(2)
-        turn_tokens(3)
-        quantise_tokens(3)
-        make_w(0, nc.vector)
+        make_w(0, nc.vector, by_cell(k_tok[0]))
         project_k(1)
         project_v(1)
         empty_k(1)
@@ -470,6 +486,7 @@ def tile_taylorsoftmaxattention_pa_kernel(tc, x, Wk, bk, Wv, bv, out_0, out_1, o
         normalise(0)
         add_squares(1)
         make_factor(1)
+        turn_tokens(3, nc.scalar.copy)
         turn_weights(1)
         make_first(0)
         add_gram(0)
@@ -483,16 +500,21 @@ def tile_taylorsoftmaxattention_pa_kernel(tc, x, Wk, bk, Wv, bv, out_0, out_1, o
         turn_v(2)
         make_first(1)
 
-        for step in range(STEPS):
+        for step in range(STEPS - 1):
             g, c = divmod(step, BLOCKS)
-            last_group = g == GROUPS - 1
-            multiply(step)
-            if step == STEPS - 1:
-                turn_square(g - 1, 0, 1)
-                store(g - 1, 0, 1)
-            if step + 1 < STEPS:
-                make_w(step + 1, nc.gpsimd)
-            quantise(step)
+            if c == 0:
+                open_codes(g)
+            multiply(step, nc.vector, by_cell(k_tok[step]), VECTOR_PARTS)
+            multiply(step, nc.gpsimd, k_packed[step][:], GPSIMD_PARTS)
+            make_w(step + 1, nc.gpsimd, k_packed[step + 1][:])
+            if step == 0:
+                quantise_tokens(3)
+            quantise_v(step)
+            quantise_pairs(step, slice(0, HALF))
+            quantise_first(step)
+            if c == 0 and g + 1 < GROUPS:
+                quantise_weights(g + 1)
+            quantise_pairs(step, slice(HALF, PAIR_SLOTS))
             if step + 3 < STEPS:
                 project_k(step + 3)
             if g > 0 and c < 2:
@@ -500,7 +522,8 @@ def tile_taylorsoftmaxattention_pa_kernel(tc, x, Wk, bk, Wv, bv, out_0, out_1, o
                     acc[chunk] = psum_acc.tile([P, CHUNK * GROUP_HEADS], F32, name="acc", tag="acc")
                     contract(g - 1, chunk, all_blocks)
             if g > 0 and c == 2:
-                contract_first(g - 1, all_blocks)
+                first[g - 1] = psum_acc.tile([P, 2 * P], F32, name="first", tag="acc")
+                contract_first(g - 1)
             if step + 2 < STEPS:
                 add_squares(step + 2)
             if step + 3 < STEPS:
@@ -530,36 +553,48 @@ def tile_taylorsoftmaxattention_pa_kernel(tc, x, Wk, bk, Wv, bv, out_0, out_1, o
                 lay_diagonal(g - 1)
             if c == 3 and g < GROUPS - 2:
                 turn_weights(g + 2)
-            if step == STEPS - 2:
-                for chunk in range(CHUNKS):
-                    pool, tag = (psum_acc, "acc") if chunk < 2 else (psum_k, "k")
-                    acc[chunk] = pool.tile([P, CHUNK * GROUP_HEADS], F32, name="acc", tag=tag)
-                    contract(g, chunk, range(0, BLOCKS - 1))
             if c == 0 and g > 1:
                 turn_square(g - 2, 0, 1)
-                store(g - 2, 0, 1)
-        g = GROUPS - 1
-        contract_first(g, all_blocks)
-        for chunk in range(CHUNKS):
-            contract(g, chunk, range(BLOCKS - 1, BLOCKS))
+                store(g - 2, 0, 1, nc.scalar.copy)
 
-        g = GROUPS - 1
-        collect_first(g)
-        nc.vector.transpose(out=small_turned[:].rearrange("p g s e -> p (g s e)"), in_=small[:].rearrange("p g s d -> p (g s d)"))
+        step, g = STEPS - 1, GROUPS - 1
+        first[g] = psum_work.tile([P, 2 * P], F32, name="first", tag="work")
+        for chunk in range(CHUNKS):
+            pool, tag = (psum_acc, "acc") if chunk < 2 else (psum_k, "k")
+            acc[chunk] = pool.tile([P, CHUNK * GROUP_HEADS], F32, name="acc", tag=tag)
+            contract(g, chunk, range(BLOCKS - 1))
+        multiply(step, nc.gpsimd, k_packed[step][:], GPSIMD_PARTS)
+        multiply(step, nc.vector, by_cell(k_tok[step]), VECTOR_PARTS[:5])
+        quantise_v(step)
+        for chunk in range(2):
+            quantise_pairs(step, slice(chunk * CHUNK, (chunk + 1) * CHUNK))
+            contract(g, chunk, range(BLOCKS - 1, BLOCKS))
+        multiply(step, nc.vector, by_cell(k_tok[step]), VECTOR_PARTS[5:])
+        turn_square(g - 1, 0, 1)
         collect(g, 0, nc.scalar.copy)
+        collect(g, 1, nc.scalar.copy)
         lay(g, 16, 0, nc.scalar.copy)
-        collect(g, 1, nc.vector.tensor_copy)
+        lay(g, 8, 0, nc.scalar.copy)
+        quantise_first(step)
+        contract_first(g)
+        for chunk in range(2, CHUNKS):
+            quantise_pairs(step, slice(chunk * CHUNK, (chunk + 1) * CHUNK))
+            contract(g, chunk, range(BLOCKS - 1, BLOCKS))
+        store(g - 1, 0, 1, nc.scalar.copy)
+        collect_first(g)
+        lay_diagonal(g)
+
         collect(g, 2, nc.scalar.copy)
         lay(g, 16, 1, nc.scalar.copy)
-        lay(g, 8, 0, nc.vector.tensor_copy)
         collect(g, 3, nc.vector.tensor_copy)
         for span in [4, 2, 1]:
             lay(g, span, 0, nc.vector.tensor_copy)
-        lay_diagonal(g)
+        nc.vector.transpose(out=small_turned[:].rearrange("p g s e -> p (g s e)"), in_=small[:].rearrange("p g s d -> p (g s d)"))
+        for part in range(4):
+            turn_square(g, part, 4)
         nc.scalar.copy(out=kv_stage[:, :, 1:OUT_DIM], in_=small_turned[:, :, 0, :])
         nc.sync.dma_start(out=kv_rows, in_=kv_stage[:])
         nc.scalar.copy(out=vsum_stage[:, :, 1:OUT_DIM], in_=small_turned[:, :, 1, :])
         nc.sync.dma_start(out=vsum_rows, in_=vsum_stage[0:P:DIM, :, :])
         for part in range(4):
-            turn_square(g, part, 4)
-            store(g, part, 4)
+            store(g, part, 4, nc.scalar.copy if part < 2 else nc.vector.tensor_copy)

@@ -27,14 +27,17 @@ GROUPS = HEADS // GROUP_HEADS
 BLOCKS = TOKENS // K_PASS
 STEPS = GROUPS * BLOCKS
 CELL = GROUP_HEADS * PACK
-SPANS = [(16, 0), (16, 1), (8, 0), (4, 0), (2, 0), (1, 0)]
-FIRST_PAIR = {(16, 0): 0, (8, 0): 128, (16, 1): 256, (4, 0): 384, (2, 0): 448, (1, 0): 480}
+SPANS = [(16, 0), (16, 1), (16, 2), (8, 0), (4, 0), (2, 0), (1, 0)]
+LAY_16 = [slice(0, 6), slice(6, 8), slice(8, 16)]
+FIRST_PAIR = {(16, 0): 0, (8, 0): 96, (2, 0): 224, (4, 0): 256, (1, 0): 320, (16, 1): 352}
+PAD = slice(336, 352)
+ROWS_16 = [slice(0, 6), slice(6, 16)]
 PAIRS = DIM * (DIM - 1) // 2
 PAIR_SLOTS = 512
 CHUNK = 128
 CHUNKS = PAIR_SLOTS // CHUNK
 HALF = PAIR_SLOTS // 2
-VECTOR_PARTS = [(16, 0), (8, 0), (8, 1), (4, 0), (4, 1), (4, 2), (4, 3), (2, 0), (2, 1), (1, 0)]
+VECTOR_PARTS = [(16, 0), (8, 0), (8, 1), (2, 0), (2, 1), (4, 0), (4, 1), (4, 2), (4, 3), (1, 0)]
 GPSIMD_PARTS = [(16, 1)]
 GRAM_COLS = P + 2
 DIAG = DIM + 1
@@ -57,15 +60,17 @@ def tile_taylorsoftmaxattention_pa_kernel(tc, x, Wk, bk, Wv, bv, out_0, out_1, o
         prep = ctx.enter_context(tc.tile_pool(name="prep", bufs=2))
         ahead = ctx.enter_context(tc.tile_pool(name="ahead", bufs=3))
         prod = ctx.enter_context(tc.tile_pool(name="prod", bufs=2))
+        codes = ctx.enter_context(tc.tile_pool(name="codes", bufs=3))
         done = ctx.enter_context(tc.tile_pool(name="done", bufs=2))
-        psum_acc = ctx.enter_context(tc.psum_pool(name="psum_acc", bufs=2))
+        once = ctx.enter_context(tc.tile_pool(name="once", bufs=1))
+        psum_acc = ctx.enter_context(tc.psum_pool(name="psum_acc", bufs=1))
         psum_gram = ctx.enter_context(tc.psum_pool(name="psum_gram", bufs=1))
-        psum_k = ctx.enter_context(tc.psum_pool(name="psum_k", bufs=3))
-        psum_work = ctx.enter_context(tc.psum_pool(name="psum_work", bufs=2))
+        psum_k = ctx.enter_context(tc.psum_pool(name="psum_k", bufs=2))
+        psum_work = ctx.enter_context(tc.psum_pool(name="psum_work", bufs=4))
         ctx.enter_context(tc.manual_schedule())
 
         w_raw = keep.tile([P, GROUPS, 2, CHANNELS], BF16)
-        x_raw = keep.tile([P, TOKENS // P, CHANNELS], BF16)
+        x_raw = prod.tile([P, TOKENS // P, CHANNELS], BF16, name="kk_codes", align_bytes=64)
         bias_rows = keep.tile([2 * GROUPS, P], BF16)
         nc.scalar.dma_start(out=bias_rows[0:GROUPS, :], in_=bk.rearrange("(g f) -> g f", g=GROUPS))
         nc.scalar.dma_start(out=bias_rows[GROUPS : 2 * GROUPS, :], in_=bv.rearrange("(g f) -> g f", g=GROUPS))
@@ -92,6 +97,10 @@ def tile_taylorsoftmaxattention_pa_kernel(tc, x, Wk, bk, Wv, bv, out_0, out_1, o
         nc.vector.memset(scaled_floor[:], EPS * EPS / (SCALE * SCALE))
         bias_square = keep.tile([P, P], F32)
         nc.vector.memset(bias_square[:], 0.0)
+        head_marks = keep.tile([P, GROUP_HEADS], F32)
+        nc.vector.tensor_reduce(
+            out=head_marks[:], in_=ident[:].rearrange("p (h d) -> p h d", h=GROUP_HEADS), op=ALU.add, axis=mybir.AxisListType.X
+        )
         ident_by_feature = keep.tile([P, P], F32)
         nc.vector.tensor_copy(
             out=ident_by_feature[:].rearrange("p (d h) -> p d h", h=GROUP_HEADS), in_=ident[:].rearrange("p (h d) -> p d h", h=GROUP_HEADS)
@@ -103,11 +112,11 @@ def tile_taylorsoftmaxattention_pa_kernel(tc, x, Wk, bk, Wv, bv, out_0, out_1, o
         w_scales = keep.tile([P, GROUPS, 2 * P], U8, align_bytes=64)
 
         kn_rows = []
-        for parity in range(2):
+        for parity in range(5):
             kn_rows.append(keep.tile([P, PACK, GRAM_COLS], F32, name="kn_rows%d" % parity))
-            nc.gpsimd.memset(kn_rows[parity][:], 1.0)
+            nc.gpsimd.memset(kn_rows[parity][:, :, P:GRAM_COLS], 1.0)
         kk_bf = keep.tile([P, PAIR_SLOTS, CELL], BF16, align_bytes=64)
-        nc.gpsimd.memset(kk_bf[:, PAIRS:PAIR_SLOTS, :], 0.0)
+        nc.gpsimd.memset(kk_bf[:, PAD, :], 0.0)
         small = keep.tile([P, GROUPS, 2, DIM], F32, align_bytes=64)
         nc.gpsimd.memset(small[:], 0.0)
         small_turned = keep.tile([P, GROUPS, 2, DIM], F32, align_bytes=64)
@@ -117,13 +126,14 @@ def tile_taylorsoftmaxattention_pa_kernel(tc, x, Wk, bk, Wv, bv, out_0, out_1, o
         bias_cols = keep.tile([P, 2 * GROUPS], F32)
 
         w_grouped, x_grouped = {}, {}
-        k_sums, v_sum_bank, k_feat, v_feat, k_tok, v_tok, norms, factor, factor_squared = {}, {}, {}, {}, {}, {}, {}, {}, {}
-        k_packed, w_packed, first_bf, v_bf = {}, {}, {}, {}
+        k_squares, k_sums, v_sum_bank, k_feat, v_feat, k_tok, k_rows, v_tok, norms, factor = {}, {}, {}, {}, {}, {}, {}, {}, {}, {}
+        kn_turned, kn_feat, kn_tok, packed, first_bf, v_bf = {}, {}, {}, {}, {}, {}
         v_codes, v_scales, first_codes, first_scales, kk_codes, kk_scales = {}, {}, {}, {}, {}, {}
+        operands = {}
         acc, first, gram, v_sums, stage, by_pair, by_square, square, turned_square = {}, {}, {}, {}, {}, {}, {}, {}, {}
 
         def turn_weights(g):
-            pool, tag = (psum_k, "k") if g == 0 else (psum_work, "work")
+            pool, tag = [(psum_k, "k"), (psum_acc, "acc"), (psum_work, "work"), (psum_work, "work")][g]
             turned = pool.tile([P, 2, 2, P], F32, name="w_turned", tag=tag)
             for m in range(2):
                 for u in range(2):
@@ -148,10 +158,10 @@ def tile_taylorsoftmaxattention_pa_kernel(tc, x, Wk, bk, Wv, bv, out_0, out_1, o
             nc.scalar.mul(out=bias_cols[:, GROUPS : 2 * GROUPS], in_=bias_turned[:, GROUPS : 2 * GROUPS], mul=1.0 / TOKENS)
 
         def turn_first_tokens():
-            x_grouped[0] = prep.tile([P, K_PASS, PACK], BF16, name="x_grouped", align_bytes=64)
+            x_grouped[0] = ahead.tile([P, K_PASS, PACK], BF16, name="x_grouped", align_bytes=64)
             pairs = x_grouped[0][:].bitcast(F32).rearrange("p (j n) u -> p j n u", j=PACK)
             for j in range(PACK):
-                pool, tag = (psum_acc, "acc") if j < 2 else (psum_work, "work")
+                pool, tag = (psum_acc, "acc") if j == 0 else (psum_work, "work")
                 turned = pool.tile([P, 2, P], F32, name="x_first_turned", tag=tag)
                 for u in range(2):
                     nc.tensor.transpose(out=turned[:, u, :], in_=x_words[:, j, u * P : (u + 1) * P], identity=ident[:])
@@ -166,11 +176,12 @@ def tile_taylorsoftmaxattention_pa_kernel(tc, x, Wk, bk, Wv, bv, out_0, out_1, o
                 in_=x_grouped[0][:, tokens, :].rearrange("p n k -> p (n k)"),
             )
 
-        def turn_tokens(c, copy):
-            x_grouped[c] = prep.tile([P, K_PASS, PACK], BF16, name="x_grouped", align_bytes=64)
+        def turn_tokens(c):
+            x_grouped[c] = ahead.tile([P, K_PASS, PACK], BF16, name="x_grouped", align_bytes=64)
             pairs = x_grouped[c][:].bitcast(F32).rearrange("p (j n) u -> p j n u", j=PACK)
             for half in range(2):
-                turned = psum_acc.tile([P, 2, 2, P], F32, name="x_turned", tag="acc")
+                pool, tag = (psum_acc, "acc") if half == 0 else (psum_k, "k")
+                turned = pool.tile([P, 2, 2, P], F32, name="x_turned", tag=tag)
                 for j in range(2):
                     for u in range(2):
                         nc.tensor.transpose(
@@ -178,7 +189,7 @@ def tile_taylorsoftmaxattention_pa_kernel(tc, x, Wk, bk, Wv, bv, out_0, out_1, o
                             in_=x_words[:, PACK * c + 2 * half + j, u * P : (u + 1) * P],
                             identity=ident[:],
                         )
-                copy(out=pairs[:, 2 * half : 2 * half + 2, :, :], in_=turned[:].rearrange("p j u n -> p j n u"))
+                nc.vector.tensor_copy(out=pairs[:, 2 * half : 2 * half + 2, :, :], in_=turned[:].rearrange("p j u n -> p j n u"))
 
         def quantise_tokens(c):
             block = slice(c * K_PASS, (c + 1) * K_PASS)
@@ -220,6 +231,29 @@ def tile_taylorsoftmaxattention_pa_kernel(tc, x, Wk, bk, Wv, bv, out_0, out_1, o
                 scale=1.0,
             )
 
+        def square_k(step):
+            g = step // BLOCKS
+            k_squares[step] = prep.tile([P, K_PASS], F32, name="k_squares")
+            nc.scalar.activation(
+                out=k_squares[step][:].rearrange("p (u e n) -> p u e n", u=2, e=2),
+                in_=k_sums[step][:].rearrange("p (u n e) -> p u e n", u=2, e=2),
+                func=ACT.Square,
+                bias=bias_cols[:, g : g + 1],
+                scale=1.0,
+            )
+
+        def add_squares(step):
+            bank = psum_work.tile([P, PACK, P], F32, name="bank", tag="work")
+            v_tok[step], norms[step] = bank[:, 0:2, :], bank[:, 2, 0:CELL]
+            for t in range(PACK):
+                nc.tensor.matmul(
+                    out=norms[step][:, t * GROUP_HEADS : (t + 1) * GROUP_HEADS],
+                    lhsT=k_squares[step][:, t * P : (t + 1) * P],
+                    rhs=head_marks[:],
+                    start=True,
+                    stop=True,
+                )
+
         def empty_v(step):
             g, c = divmod(step, BLOCKS)
             if c == 0:
@@ -235,28 +269,33 @@ def tile_taylorsoftmaxattention_pa_kernel(tc, x, Wk, bk, Wv, bv, out_0, out_1, o
             )
 
         def turn_k(step):
-            k_tok[step] = psum_k.tile([P, P, PACK], F32, name="k_tok", tag="k")
+            if step == 0:
+                k_tok[step] = psum_k.tile([P, P, PACK], F32, name="k_tok", tag="k")
+                for t in range(PACK):
+                    nc.tensor.transpose(out=k_tok[step][:, :, t], in_=k_feat[step][:, t * P : (t + 1) * P], identity=ident_by_feature[:])
+                k_rows[step] = k_tok[step][:].rearrange("p (d h) t -> p t h d", h=GROUP_HEADS)
+                return
+            k_tok[step] = psum_work.tile([P, PACK, P], F32, name="k_tok", tag="work")
             for t in range(PACK):
-                nc.tensor.transpose(out=k_tok[step][:, :, t], in_=k_feat[step][:, t * P : (t + 1) * P], identity=ident_by_feature[:])
+                nc.tensor.transpose(out=k_tok[step][:, t, :], in_=k_feat[step][:, t * P : (t + 1) * P], identity=ident[:])
+            k_rows[step] = k_tok[step][:].rearrange("p t (h d) -> p t h d", h=GROUP_HEADS)
 
         def turn_v(step):
-            v_tok[step] = psum_work.tile([P, 2, P], F32, name="v_tok", tag="work")
             v_words = v_feat[step][:].bitcast(F32)
             for u in range(2):
                 nc.tensor.transpose(out=v_tok[step][:, u, :], in_=v_words[:, u * P : (u + 1) * P], identity=ident[:])
 
-        def add_squares(step):
-            squares = prep.tile([P, CELL, DIM], F32)
-            norms[step] = prep.tile([P, CELL], F32, name="norms")
-            k_cells = by_cell(k_tok[step])
-            for x in range(CELL):
-                nc.scalar.activation(out=squares[:, x, :], in_=k_cells[:, :, x], func=ACT.Square, accum_out=norms[step][:, x : x + 1])
-
         def make_factor(step):
             above_floor = prep.tile([P, CELL], F32)
-            nc.scalar.activation(out=above_floor[:], in_=norms[step][:], func=ACT.Relu, bias=minus_floor[:], scale=1.0)
+            nc.scalar.activation(
+                out=above_floor[:].rearrange("p (h t) -> p t h", h=GROUP_HEADS),
+                in_=norms[step].rearrange("p (t h) -> p t h", h=GROUP_HEADS),
+                func=ACT.Relu,
+                bias=minus_floor[:],
+                scale=1.0,
+            )
             v_bf[step] = ahead.tile([P, P, PACK], BF16, name="v_bf", align_bytes=64)
-            nc.scalar.copy(out=v_bf[step][:].bitcast(F32), in_=v_tok[step][:].rearrange("p u f -> p f u"))
+            nc.scalar.copy(out=v_bf[step][:].bitcast(F32), in_=v_tok[step].rearrange("p u f -> p f u"))
             factor[step] = ahead.tile([P, CELL], F32, name="factor")
             nc.scalar.activation(
                 out=factor[step][:],
@@ -265,48 +304,72 @@ def tile_taylorsoftmaxattention_pa_kernel(tc, x, Wk, bk, Wv, bv, out_0, out_1, o
                 bias=scaled_floor[:],
                 scale=1.0 / (SCALE * SCALE),
             )
-            k_packed[step] = ahead.tile([P, DIM, CELL], F32, name="k_packed")
-            factor_squared[step] = ahead.tile([P, CELL], F32, name="factor_squared")
-            if step > 0:
-                nc.scalar.copy(out=k_packed[step][:], in_=by_cell(k_tok[step]))
-            nc.scalar.activation(out=factor_squared[step][:], in_=factor[step][:], func=ACT.Square)
-            if step == 0:
-                nc.scalar.copy(out=k_packed[step][:], in_=by_cell(k_tok[step]))
 
         def by_cell(tile):
             return tile[:].rearrange("p (d h) t -> p d (h t)", h=GROUP_HEADS)
 
-        def make_w(step, engine, k_cells):
-            w_packed[step] = prep.tile([P, DIM, CELL], F32, name="w_packed")
-            engine.tensor_tensor(
-                out=w_packed[step][:],
-                in0=k_cells,
-                in1=factor_squared[step][:].unsqueeze(1).to_broadcast([P, DIM, CELL]),
+        def start_first_step():
+            factor_squared = keep.tile([P, CELL], F32)
+            nc.scalar.activation(out=factor_squared[:], in_=factor[0][:], func=ACT.Square)
+            w_packed = keep.tile([P, DIM, CELL], F32)
+            nc.vector.tensor_tensor(
+                out=w_packed[:],
+                in0=by_cell(k_tok[0]),
+                in1=factor_squared[:].unsqueeze(1).to_broadcast([P, DIM, CELL]),
                 op=ALU.mult,
             )
+            k_packed = keep.tile([P, DIM, CELL], F32)
+            nc.scalar.copy(out=k_packed[:], in_=by_cell(k_tok[0]))
+            operands[0] = by_cell(k_tok[0]), k_packed[:], w_packed[:]
+
+        def turn_back(step):
+            kn_turned[step] = psum_work.tile([P, PACK, P], F32, name="kn_turned", tag="work")
+            for t in range(PACK):
+                nc.tensor.transpose(out=kn_turned[step][:, t, :], in_=kn_rows[step % 5][:, t, 0:P], identity=ident[:])
+
+        def copy_back(step):
+            kn_feat[step] = prep.tile([P, PACK, P], F32, name="kn_feat")
+            nc.scalar.copy(out=kn_feat[step][:], in_=kn_turned[step][:])
+
+        def turn_kn(step):
+            kn_tok[step] = psum_k.tile([P, P, PACK], F32, name="kn_tok", tag="k")
+            for t in range(PACK):
+                nc.tensor.transpose(out=kn_tok[step][:, :, t], in_=kn_feat[step][:, t, :], identity=ident_by_feature[:])
+
+        def pack(step):
+            packed[step] = ahead.tile([P, DIM, CELL], F32, name="packed")
+            nc.scalar.copy(out=packed[step][:], in_=by_cell(kn_tok[step]))
+            operands[step] = by_cell(kn_tok[step]), packed[step][:], packed[step][:]
 
         def normalise(step):
-            rows = kn_rows[step % 2]
-            k_cells = k_tok[step][:].rearrange("p (d h) t -> p h d t", h=GROUP_HEADS)
+            rows = kn_rows[step % 5]
             for t in range(PACK):
                 for h in range(GROUP_HEADS):
                     nc.scalar.activation(
                         out=rows[:, t, h * DIM : (h + 1) * DIM],
-                        in_=k_cells[:, h, :, t],
+                        in_=k_rows[step][:, t, h, :],
                         func=ACT.Copy,
                         scale=factor[step][:, h * PACK + t : h * PACK + t + 1],
                     )
 
-        def make_first(step):
-            first_bf[step] = ahead.tile([P, 2, P, PACK], BF16, name="first_bf", align_bytes=64)
-            kn_words = kn_rows[step % 2][:, :, 0:P].rearrange("p t (f r) -> p f t r", r=4)
-            first_words = first_bf[step][:].rearrange("p s (f r) t -> p s f t r", r=4)
-            nc.scalar.copy(out=first_words[:, 0], in_=kn_words)
-            nc.scalar.activation(out=first_words[:, 1], in_=kn_words, func=ACT.Square)
+        def first_operands(step):
+            if step == 0:
+                kn = kn_rows[0][:, :, 0:P].rearrange("p t (h d) -> p d h t", h=GROUP_HEADS)
+                return kn, first_bf[step][:].rearrange("p s d (h t) -> p s d h t", h=GROUP_HEADS)
+            return by_cell(kn_tok[step]), first_bf[step][:]
+
+        def first_kn(step):
+            first_bf[step] = ahead.tile([P, 2, DIM, CELL], BF16, name="first_bf", align_bytes=64)
+            kn, cells = first_operands(step)
+            nc.scalar.copy(out=cells[:, 0], in_=kn)
+
+        def first_squares(step):
+            kn, cells = first_operands(step)
+            nc.scalar.activation(out=cells[:, 1], in_=kn, func=ACT.Square)
 
         def add_gram(step):
             g, c = divmod(step, BLOCKS)
-            rows = kn_rows[step % 2]
+            rows = kn_rows[step % 5]
             if c == 0:
                 gram[g] = psum_gram.tile([P, GRAM_COLS], F32, name="gram")
             for t in range(PACK):
@@ -319,19 +382,21 @@ def tile_taylorsoftmaxattention_pa_kernel(tc, x, Wk, bk, Wv, bv, out_0, out_1, o
                 )
 
         def collect_gram(g):
-            stage[g] = done.tile([P, DIM, OUT_DIM], F32, name="stage")
+            stage[g] = ahead.tile([P, DIM, OUT_DIM], F32, name="stage")
             for h in range(GROUP_HEADS):
                 rows = slice(h * DIM, (h + 1) * DIM)
                 nc.scalar.mul(out=stage[g][rows, :, 0], in_=gram[g][rows, h * DIM : (h + 1) * DIM], mul=1.0 / TOKENS)
             nc.scalar.mul(out=kv_stage[:, g, 0:1], in_=gram[g][:, P : P + 1], mul=1.0 / TOKENS)
 
-        def multiply(step, engine, k, parts):
-            w = w_packed[step][:]
+        def multiply(step, engine, engine_reads_psum, parts):
+            w = operands[step][2]
+            k = operands[step][0 if engine_reads_psum else 1]
             for span, part in parts:
                 if span == 16:
-                    shape = [P, 8, 16, CELL]
+                    rows = ROWS_16[part]
+                    shape = [P, rows.stop - rows.start, 16, CELL]
                     slot = FIRST_PAIR[16, part]
-                    left = k[:, 8 * part : 8 * part + 8, :].unsqueeze(2)
+                    left = k[:, rows, :].unsqueeze(2)
                     right = w[:, 16:32, :].unsqueeze(1)
                 elif span == 8:
                     shape = [P, span, span, CELL]
@@ -348,10 +413,10 @@ def tile_taylorsoftmaxattention_pa_kernel(tc, x, Wk, bk, Wv, bv, out_0, out_1, o
                 engine.tensor_tensor(out=out, in0=left.to_broadcast(shape), in1=right.to_broadcast(shape), op=ALU.mult)
 
         def open_codes(g):
-            v_codes[g] = prod.tile([P, BLOCKS, P], U32, name="v_codes", align_bytes=64)
-            v_scales[g] = prod.tile([P, BLOCKS, P], U8, name="v_scales", align_bytes=64)
-            first_codes[g] = prod.tile([P, BLOCKS, 2 * P], U32, name="first_codes", align_bytes=64)
-            first_scales[g] = prod.tile([P, BLOCKS, 2 * P], U8, name="first_scales", align_bytes=64)
+            v_codes[g] = codes.tile([P, BLOCKS, P], U32, name="v_codes", align_bytes=64)
+            v_scales[g] = codes.tile([P, BLOCKS, P], U8, name="v_scales", align_bytes=64)
+            first_codes[g] = codes.tile([P, BLOCKS, 2 * P], U32, name="first_codes", align_bytes=64)
+            first_scales[g] = codes.tile([P, BLOCKS, 2 * P], U8, name="first_scales", align_bytes=64)
             kk_codes[g] = prod.tile([P, BLOCKS, PAIR_SLOTS * GROUP_HEADS], U32, name="kk_codes", align_bytes=64)
             kk_scales[g] = prod.tile([P, BLOCKS, PAIR_SLOTS * GROUP_HEADS], U8, name="kk_scales", align_bytes=64)
 
@@ -366,7 +431,7 @@ def tile_taylorsoftmaxattention_pa_kernel(tc, x, Wk, bk, Wv, bv, out_0, out_1, o
             nc.vector.quantize_mx(
                 out=first_codes[g][:, c, :].bitcast(FP8X4),
                 scales=first_scales[g][:, c, :],
-                in_=first_bf[step][:].rearrange("p s f t -> p (s f t)"),
+                in_=first_bf[step][:].rearrange("p s d x -> p (s d x)"),
             )
 
         def quantise_pairs(step, pairs):
@@ -405,7 +470,7 @@ def tile_taylorsoftmaxattention_pa_kernel(tc, x, Wk, bk, Wv, bv, out_0, out_1, o
 
         def collect_first(g):
             by_square[g] = done.tile([P, DIM], F32, name="by_square")
-            sums = first[g][:].rearrange("p (s m i) -> p s m i", s=2, m=GROUP_HEADS)
+            sums = first[g][:].rearrange("p (s i m) -> p s m i", s=2, m=GROUP_HEADS)
             for h in range(GROUP_HEADS):
                 rows = slice(h * DIM, (h + 1) * DIM)
                 nc.scalar.copy(out=small[rows, g, 0, :], in_=sums[rows, 0, h, :])
@@ -423,12 +488,16 @@ def tile_taylorsoftmaxattention_pa_kernel(tc, x, Wk, bk, Wv, bv, out_0, out_1, o
 
         def lay(g, span, half, copy):
             if (span, half) == (16, 0):
-                square[g] = done.tile([P, DIM * DIAG], F32, name="square", align_bytes=64)
+                square[g] = once.tile([P, DIM * DIAG], F32, name="square", align_bytes=64)
             if span == 16:
-                sums = by_pair[g][:, FIRST_PAIR[16, half] : FIRST_PAIR[16, half] + 128].rearrange("p (i j) -> p i j", i=8)
-                rows = square[g][:].rearrange("p (i r) -> p i r", r=DIM)
-                copy(out=rows[:, 8 * half : 8 * half + 8, 16:32], in_=sums)
-                copy(out=rows[:, 16:32, 8 * half : 8 * half + 8], in_=sums.rearrange("p i j -> p j i"))
+                rows = LAY_16[half]
+                part = 0 if rows.start < ROWS_16[1].start else 1
+                pair = FIRST_PAIR[16, part] + 16 * (rows.start - ROWS_16[part].start)
+                count = rows.stop - rows.start
+                sums = by_pair[g][:, pair : pair + 16 * count].rearrange("p (i j) -> p i j", i=count)
+                cells = square[g][:].rearrange("p (i r) -> p i r", r=DIM)
+                copy(out=cells[:, rows, 16:32], in_=sums)
+                copy(out=cells[:, 16:32, rows], in_=sums.rearrange("p i j -> p j i"))
                 return
             spans = DIM // (2 * span)
             order = "p (b i j) -> p b i j" if span >= 8 else "p (i b j) -> p b i j"
@@ -445,7 +514,7 @@ def tile_taylorsoftmaxattention_pa_kernel(tc, x, Wk, bk, Wv, bv, out_0, out_1, o
         def turn_square(g, part, parts):
             rows = slice(part * DIM // parts, (part + 1) * DIM // parts)
             if part == 0:
-                turned_square[g] = done.tile([P, DIM, DIM], F32, name="turned_square", align_bytes=64)
+                turned_square[g] = once.tile([P, DIM, DIM], F32, name="turned_square", align_bytes=64)
             nc.vector.transpose(
                 out=turned_square[g][:, rows, :].rearrange("p w e -> p (w e)"), in_=square[g][:, rows.start * DIM : rows.stop * DIM]
             )
@@ -458,123 +527,178 @@ def tile_taylorsoftmaxattention_pa_kernel(tc, x, Wk, bk, Wv, bv, out_0, out_1, o
             )
 
         all_blocks = range(BLOCKS)
+
+        def open_chunk(chunk, pool, tag):
+            acc[chunk] = pool.tile([P, CHUNK * GROUP_HEADS], F32, name="acc", tag=tag)
+
+        def prepare(step):
+            a, b, e = step + 3, step + 2, step + 1
+            g, c = divmod(step, BLOCKS)
+            if a == 3 or a == BLOCKS:
+                project_k(a)
+            if a < STEPS:
+                project_v(a)
+            if e > 1:
+                add_gram(e)
+            else:
+                turn_weights(1)
+                add_gram(0)
+                add_gram(1)
+            if b < STEPS:
+                make_factor(b)
+            if a < STEPS:
+                empty_k(a)
+                turn_k(a)
+            if g > 1 and c == 0:
+                collect_first(g - 2)
+            if e > 1:
+                pack(e)
+            if b < STEPS:
+                normalise(b)
+                turn_back(b)
+            if a < STEPS:
+                square_k(a)
+                add_squares(a)
+                empty_v(a)
+                turn_v(a)
+            if 0 < g < GROUPS - 1:
+                open_chunk(c, psum_acc, "acc")
+                contract(g - 1, c, all_blocks)
+            first_kn(e)
+            first_squares(e)
+            if c == 2 and g < GROUPS - 2:
+                turn_weights(g + 2)
+            if a + 1 < STEPS and a + 1 != BLOCKS:
+                project_k(a + 1)
+            if b < STEPS:
+                copy_back(b)
+                turn_kn(b)
+            if c == 2:
+                collect_gram(g)
+            if 0 < g < GROUPS - 1:
+                collect(g - 1, c, nc.scalar.copy)
+            if step == 2:
+                first_kn(0)
+                first_squares(0)
+
         turn_first_tokens()
         turn_weights(0)
         turn_biases()
         quantise_first_tokens(0)
         quantise_first_tokens(1)
         quantise_weights(0)
-        turn_tokens(1, nc.vector.tensor_copy)
+        turn_tokens(1)
         project_k(0)
         project_v(0)
+        square_k(0)
         empty_k(0)
         empty_v(0)
+        turn_tokens(2)
+        quantise_tokens(1)
+        add_squares(0)
         turn_k(0)
         turn_v(0)
-        quantise_tokens(1)
-        turn_tokens(2, nc.vector.tensor_copy)
-        add_squares(0)
-        make_factor(0)
-        quantise_tokens(2)
-        make_w(0, nc.vector, by_cell(k_tok[0]))
+        turn_tokens(3)
         project_k(1)
+        make_factor(0)
+        start_first_step()
+        quantise_tokens(2)
         project_v(1)
         empty_k(1)
+        square_k(1)
         empty_v(1)
         turn_k(1)
-        turn_v(1)
-        normalise(0)
         add_squares(1)
-        make_factor(1)
-        turn_tokens(3, nc.scalar.copy)
-        turn_weights(1)
-        make_first(0)
-        add_gram(0)
+        turn_v(1)
         project_k(2)
+        make_factor(1)
         empty_k(2)
         turn_k(2)
-        project_v(2)
         normalise(1)
+        turn_back(1)
+        project_v(2)
+        square_k(2)
+        add_squares(2)
+        normalise(0)
+        copy_back(1)
+        turn_kn(1)
         empty_v(2)
-        add_gram(1)
         turn_v(2)
-        make_first(1)
+        pack(1)
 
         for step in range(STEPS - 1):
             g, c = divmod(step, BLOCKS)
             if c == 0:
                 open_codes(g)
-            multiply(step, nc.vector, by_cell(k_tok[step]), VECTOR_PARTS)
-            multiply(step, nc.gpsimd, k_packed[step][:], GPSIMD_PARTS)
-            make_w(step + 1, nc.gpsimd, k_packed[step + 1][:])
+            multiply(step, nc.vector, True, VECTOR_PARTS)
+            multiply(step, nc.gpsimd, False, GPSIMD_PARTS)
+            if g > 1 and c == 2:
+                turn_square(g - 2, 0, 1)
             if step == 0:
                 quantise_tokens(3)
             quantise_v(step)
             quantise_pairs(step, slice(0, HALF))
-            quantise_first(step)
-            if c == 0 and g + 1 < GROUPS:
-                quantise_weights(g + 1)
+            if step > 1:
+                quantise_first(step - 1)
+            if step == 3:
+                quantise_first(0)
+            if step == 1:
+                quantise_weights(1)
+            if c == 3 and g < GROUPS - 2:
+                quantise_weights(g + 2)
             quantise_pairs(step, slice(HALF, PAIR_SLOTS))
-            if step + 3 < STEPS:
-                project_k(step + 3)
-            if g > 0 and c < 2:
-                for chunk in (2 * c, 2 * c + 1):
-                    acc[chunk] = psum_acc.tile([P, CHUNK * GROUP_HEADS], F32, name="acc", tag="acc")
-                    contract(g - 1, chunk, all_blocks)
-            if g > 0 and c == 2:
+            prepare(step)
+            if 0 < g < GROUPS - 1 and c == 3:
                 first[g - 1] = psum_acc.tile([P, 2 * P], F32, name="first", tag="acc")
                 contract_first(g - 1)
-            if step + 2 < STEPS:
-                add_squares(step + 2)
-            if step + 3 < STEPS:
-                empty_k(step + 3)
-                turn_k(step + 3)
-            if step + 2 < STEPS:
-                make_factor(step + 2)
-            if step + 3 < STEPS:
-                project_v(step + 3)
-            if step + 2 < STEPS:
-                normalise(step + 2)
-                add_gram(step + 2)
-            if step + 3 < STEPS:
-                empty_v(step + 3)
-                turn_v(step + 3)
-            if step + 2 < STEPS:
-                make_first(step + 2)
-            if c == 1:
-                collect_gram(g)
-            if g > 0 and c < 2:
-                for chunk in (2 * c, 2 * c + 1):
+            if g > 1 and c < 2:
+                for span, half in SPANS[3 * c : 3 * c + 3 + c]:
+                    lay(g - 2, span, half, nc.scalar.copy)
+            if g > 1 and c == 1:
+                lay_diagonal(g - 2)
+            if g > 1 and c == 2:
+                store(g - 2, 0, 1, nc.scalar.copy)
+            if step == STEPS - 4:
+                open_chunk(0, psum_acc, "acc")
+                contract(g - 1, 0, all_blocks)
+                collect(g - 1, 0, nc.scalar.copy)
+            if step == STEPS - 3:
+                for chunk in (1, 2):
+                    open_chunk(chunk, psum_work, "work")
+                    contract(g - 1, chunk, all_blocks)
                     collect(g - 1, chunk, nc.scalar.copy)
-            if g > 0 and c == 2:
+            if step == STEPS - 2:
+                first[g - 1] = psum_acc.tile([P, 2 * P], F32, name="first", tag="acc")
+                contract_first(g - 1)
+                open_chunk(3, psum_work, "work")
+                contract(g - 1, 3, all_blocks)
                 collect_first(g - 1)
+                collect(g - 1, 3, nc.scalar.copy)
                 for span, half in SPANS:
                     lay(g - 1, span, half, nc.scalar.copy)
                 lay_diagonal(g - 1)
-            if c == 3 and g < GROUPS - 2:
-                turn_weights(g + 2)
-            if c == 0 and g > 1:
-                turn_square(g - 2, 0, 1)
-                store(g - 2, 0, 1, nc.scalar.copy)
 
         step, g = STEPS - 1, GROUPS - 1
-        first[g] = psum_work.tile([P, 2 * P], F32, name="first", tag="work")
+        first[g] = psum_k.tile([P, 2 * P], F32, name="first", tag="k")
         for chunk in range(CHUNKS):
-            pool, tag = (psum_acc, "acc") if chunk < 2 else (psum_k, "k")
-            acc[chunk] = pool.tile([P, CHUNK * GROUP_HEADS], F32, name="acc", tag=tag)
+            if chunk == 0:
+                open_chunk(chunk, psum_acc, "acc")
+            else:
+                open_chunk(chunk, psum_work, "work")
             contract(g, chunk, range(BLOCKS - 1))
-        multiply(step, nc.gpsimd, k_packed[step][:], GPSIMD_PARTS)
-        multiply(step, nc.vector, by_cell(k_tok[step]), VECTOR_PARTS[:5])
+        multiply(step, nc.gpsimd, False, GPSIMD_PARTS)
+        multiply(step, nc.vector, True, VECTOR_PARTS)
         quantise_v(step)
         for chunk in range(2):
             quantise_pairs(step, slice(chunk * CHUNK, (chunk + 1) * CHUNK))
             contract(g, chunk, range(BLOCKS - 1, BLOCKS))
-        multiply(step, nc.vector, by_cell(k_tok[step]), VECTOR_PARTS[5:])
         turn_square(g - 1, 0, 1)
         collect(g, 0, nc.scalar.copy)
         collect(g, 1, nc.scalar.copy)
         lay(g, 16, 0, nc.scalar.copy)
         lay(g, 8, 0, nc.scalar.copy)
+        lay(g, 2, 0, nc.scalar.copy)
+        quantise_first(step - 1)
         quantise_first(step)
         contract_first(g)
         for chunk in range(2, CHUNKS):
@@ -585,10 +709,11 @@ def tile_taylorsoftmaxattention_pa_kernel(tc, x, Wk, bk, Wv, bv, out_0, out_1, o
         lay_diagonal(g)
 
         collect(g, 2, nc.scalar.copy)
-        lay(g, 16, 1, nc.scalar.copy)
+        lay(g, 4, 0, nc.scalar.copy)
+        lay(g, 1, 0, nc.scalar.copy)
         collect(g, 3, nc.vector.tensor_copy)
-        for span in [4, 2, 1]:
-            lay(g, span, 0, nc.vector.tensor_copy)
+        lay(g, 16, 1, nc.vector.tensor_copy)
+        lay(g, 16, 2, nc.vector.tensor_copy)
         nc.vector.transpose(out=small_turned[:].rearrange("p g s e -> p (g s e)"), in_=small[:].rearrange("p g s d -> p (g s d)"))
         for part in range(4):
             turn_square(g, part, 4)

@@ -61,8 +61,8 @@ def tile_taylorsoftmaxattention_pa_kernel(tc, x, Wk, bk, Wv, bv, out_0, out_1, o
         ahead = ctx.enter_context(tc.tile_pool(name="ahead", bufs=3))
         prod = ctx.enter_context(tc.tile_pool(name="prod", bufs=2))
         codes = ctx.enter_context(tc.tile_pool(name="codes", bufs=3))
+        firsts = ctx.enter_context(tc.tile_pool(name="firsts", bufs=4))
         done = ctx.enter_context(tc.tile_pool(name="done", bufs=2))
-        once = ctx.enter_context(tc.tile_pool(name="once", bufs=1))
         psum_acc = ctx.enter_context(tc.psum_pool(name="psum_acc", bufs=1))
         psum_gram = ctx.enter_context(tc.psum_pool(name="psum_gram", bufs=1))
         psum_k = ctx.enter_context(tc.psum_pool(name="psum_k", bufs=2))
@@ -133,7 +133,7 @@ def tile_taylorsoftmaxattention_pa_kernel(tc, x, Wk, bk, Wv, bv, out_0, out_1, o
         acc, first, gram, v_sums, stage, by_pair, by_square, square, turned_square = {}, {}, {}, {}, {}, {}, {}, {}, {}
 
         def turn_weights(g):
-            pool, tag = [(psum_k, "k"), (psum_acc, "acc"), (psum_work, "work"), (psum_work, "work")][g]
+            pool, tag = (psum_k, "k") if g == 0 else (psum_acc, "acc")
             turned = pool.tile([P, 2, 2, P], F32, name="w_turned", tag=tag)
             for m in range(2):
                 for u in range(2):
@@ -180,7 +180,7 @@ def tile_taylorsoftmaxattention_pa_kernel(tc, x, Wk, bk, Wv, bv, out_0, out_1, o
             x_grouped[c] = ahead.tile([P, K_PASS, PACK], BF16, name="x_grouped", align_bytes=64)
             pairs = x_grouped[c][:].bitcast(F32).rearrange("p (j n) u -> p j n u", j=PACK)
             for half in range(2):
-                pool, tag = (psum_acc, "acc") if half == 0 else (psum_k, "k")
+                pool, tag = [(psum_acc, "acc"), (psum_k, "k"), (psum_gram, "gram"), (psum_work, "work"), (psum_acc, "acc"), (psum_k, "k")][2 * c - 2 + half]
                 turned = pool.tile([P, 2, 2, P], F32, name="x_turned", tag=tag)
                 for j in range(2):
                     for u in range(2):
@@ -244,10 +244,11 @@ def tile_taylorsoftmaxattention_pa_kernel(tc, x, Wk, bk, Wv, bv, out_0, out_1, o
 
         def add_squares(step):
             bank = psum_work.tile([P, PACK, P], F32, name="bank", tag="work")
-            v_tok[step], norms[step] = bank[:, 0:2, :], bank[:, 2, 0:CELL]
+            v_tok[step] = bank[:, 0:2, :]
+            norms[step] = bank[:, 2, 0:CELL].rearrange("p (t h) -> p t h", h=GROUP_HEADS)
             for t in range(PACK):
                 nc.tensor.matmul(
-                    out=norms[step][:, t * GROUP_HEADS : (t + 1) * GROUP_HEADS],
+                    out=norms[step][:, t, :],
                     lhsT=k_squares[step][:, t * P : (t + 1) * P],
                     rhs=head_marks[:],
                     start=True,
@@ -281,15 +282,26 @@ def tile_taylorsoftmaxattention_pa_kernel(tc, x, Wk, bk, Wv, bv, out_0, out_1, o
             k_rows[step] = k_tok[step][:].rearrange("p t (h d) -> p t h d", h=GROUP_HEADS)
 
         def turn_v(step):
+            if step == 0:
+                first_bank = psum_work.tile([P, 2, P], F32, name="first_bank", tag="work")
+                v_tok[0] = first_bank[:]
             v_words = v_feat[step][:].bitcast(F32)
             for u in range(2):
                 nc.tensor.transpose(out=v_tok[step][:, u, :], in_=v_words[:, u * P : (u + 1) * P], identity=ident[:])
+
+        def add_first_squares():
+            squares = ahead.tile([P, CELL, DIM], F32, name="packed")
+            norms_by_cell = keep.tile([P, CELL], F32)
+            k_cells = by_cell(k_tok[0])
+            for x in range(CELL):
+                nc.scalar.activation(out=squares[:, x, :], in_=k_cells[:, :, x], func=ACT.Square, accum_out=norms_by_cell[:, x : x + 1])
+            norms[0] = norms_by_cell[:].rearrange("p (h t) -> p t h", h=GROUP_HEADS)
 
         def make_factor(step):
             above_floor = prep.tile([P, CELL], F32)
             nc.scalar.activation(
                 out=above_floor[:].rearrange("p (h t) -> p t h", h=GROUP_HEADS),
-                in_=norms[step].rearrange("p (t h) -> p t h", h=GROUP_HEADS),
+                in_=norms[step],
                 func=ACT.Relu,
                 bias=minus_floor[:],
                 scale=1.0,
@@ -309,18 +321,19 @@ def tile_taylorsoftmaxattention_pa_kernel(tc, x, Wk, bk, Wv, bv, out_0, out_1, o
             return tile[:].rearrange("p (d h) t -> p d (h t)", h=GROUP_HEADS)
 
         def start_first_step():
+            packed[0] = ahead.tile([P, DIM, CELL], F32, name="packed")
+            nc.vector.tensor_copy(out=packed[0][:], in_=by_cell(k_tok[0]))
+            k_rows[0] = packed[0][:].rearrange("p d (h t) -> p t h d", h=GROUP_HEADS)
             factor_squared = keep.tile([P, CELL], F32)
             nc.scalar.activation(out=factor_squared[:], in_=factor[0][:], func=ACT.Square)
-            w_packed = keep.tile([P, DIM, CELL], F32)
+            w_packed = ahead.tile([P, DIM, CELL], F32, name="packed")
             nc.vector.tensor_tensor(
                 out=w_packed[:],
                 in0=by_cell(k_tok[0]),
                 in1=factor_squared[:].unsqueeze(1).to_broadcast([P, DIM, CELL]),
                 op=ALU.mult,
             )
-            k_packed = keep.tile([P, DIM, CELL], F32)
-            nc.scalar.copy(out=k_packed[:], in_=by_cell(k_tok[0]))
-            operands[0] = by_cell(k_tok[0]), k_packed[:], w_packed[:]
+            operands[0] = by_cell(k_tok[0]), packed[0][:], w_packed[:]
 
         def turn_back(step):
             kn_turned[step] = psum_work.tile([P, PACK, P], F32, name="kn_turned", tag="work")
@@ -356,10 +369,10 @@ def tile_taylorsoftmaxattention_pa_kernel(tc, x, Wk, bk, Wv, bv, out_0, out_1, o
             if step == 0:
                 kn = kn_rows[0][:, :, 0:P].rearrange("p t (h d) -> p d h t", h=GROUP_HEADS)
                 return kn, first_bf[step][:].rearrange("p s d (h t) -> p s d h t", h=GROUP_HEADS)
-            return by_cell(kn_tok[step]), first_bf[step][:]
+            return packed[step][:], first_bf[step][:]
 
         def first_kn(step):
-            first_bf[step] = ahead.tile([P, 2, DIM, CELL], BF16, name="first_bf", align_bytes=64)
+            first_bf[step] = firsts.tile([P, 2, DIM, CELL], BF16, name="first_bf", align_bytes=64)
             kn, cells = first_operands(step)
             nc.scalar.copy(out=cells[:, 0], in_=kn)
 
@@ -371,7 +384,7 @@ def tile_taylorsoftmaxattention_pa_kernel(tc, x, Wk, bk, Wv, bv, out_0, out_1, o
             g, c = divmod(step, BLOCKS)
             rows = kn_rows[step % 5]
             if c == 0:
-                gram[g] = psum_gram.tile([P, GRAM_COLS], F32, name="gram")
+                gram[g] = psum_gram.tile([P, GRAM_COLS], F32, name="gram", tag="gram")
             for t in range(PACK):
                 nc.tensor.matmul(
                     out=gram[g][:],
@@ -488,7 +501,7 @@ def tile_taylorsoftmaxattention_pa_kernel(tc, x, Wk, bk, Wv, bv, out_0, out_1, o
 
         def lay(g, span, half, copy):
             if (span, half) == (16, 0):
-                square[g] = once.tile([P, DIM * DIAG], F32, name="square", align_bytes=64)
+                square[g] = done.tile([P, DIM * DIAG], F32, name="square", align_bytes=64)
             if span == 16:
                 rows = LAY_16[half]
                 part = 0 if rows.start < ROWS_16[1].start else 1
@@ -514,7 +527,7 @@ def tile_taylorsoftmaxattention_pa_kernel(tc, x, Wk, bk, Wv, bv, out_0, out_1, o
         def turn_square(g, part, parts):
             rows = slice(part * DIM // parts, (part + 1) * DIM // parts)
             if part == 0:
-                turned_square[g] = once.tile([P, DIM, DIM], F32, name="turned_square", align_bytes=64)
+                turned_square[g] = done.tile([P, DIM, DIM], F32, name="turned_square", align_bytes=64)
             nc.vector.transpose(
                 out=turned_square[g][:, rows, :].rearrange("p w e -> p (w e)"), in_=square[g][:, rows.start * DIM : rows.stop * DIM]
             )
@@ -534,49 +547,51 @@ def tile_taylorsoftmaxattention_pa_kernel(tc, x, Wk, bk, Wv, bv, out_0, out_1, o
         def prepare(step):
             a, b, e = step + 3, step + 2, step + 1
             g, c = divmod(step, BLOCKS)
-            if a == 3 or a == BLOCKS:
-                project_k(a)
             if a < STEPS:
-                project_v(a)
-            if e > 1:
-                add_gram(e)
-            else:
-                turn_weights(1)
-                add_gram(0)
-                add_gram(1)
+                project_k(a)
             if b < STEPS:
                 make_factor(b)
-            if a < STEPS:
-                empty_k(a)
-                turn_k(a)
             if g > 1 and c == 0:
                 collect_first(g - 2)
+            if g > 0 and c == 0:
+                collect_gram(g - 1)
+            if a < STEPS:
+                project_v(a)
+            if 0 < g < GROUPS - 1:
+                open_chunk(c, psum_acc, "acc")
+                contract(g - 1, c, all_blocks)
+            if step == 2:
+                add_gram(0)
+                add_gram(1)
+            if step > 1:
+                add_gram(step)
+            if step == STEPS - 2:
+                add_gram(STEPS - 1)
             if e > 1:
                 pack(e)
             if b < STEPS:
                 normalise(b)
                 turn_back(b)
             if a < STEPS:
+                empty_k(a)
+                turn_k(a)
                 square_k(a)
                 add_squares(a)
                 empty_v(a)
                 turn_v(a)
-            if 0 < g < GROUPS - 1:
-                open_chunk(c, psum_acc, "acc")
-                contract(g - 1, c, all_blocks)
             first_kn(e)
             first_squares(e)
-            if c == 2 and g < GROUPS - 2:
-                turn_weights(g + 2)
-            if a + 1 < STEPS and a + 1 != BLOCKS:
-                project_k(a + 1)
             if b < STEPS:
                 copy_back(b)
                 turn_kn(b)
-            if c == 2:
+            if step == STEPS - 2:
                 collect_gram(g)
             if 0 < g < GROUPS - 1:
                 collect(g - 1, c, nc.scalar.copy)
+            if c == 1 and g < GROUPS - 2:
+                turn_weights(g + 2)
+            if step == 1:
+                normalise(0)
             if step == 2:
                 first_kn(0)
                 first_squares(0)
@@ -590,38 +605,37 @@ def tile_taylorsoftmaxattention_pa_kernel(tc, x, Wk, bk, Wv, bv, out_0, out_1, o
         turn_tokens(1)
         project_k(0)
         project_v(0)
-        square_k(0)
         empty_k(0)
         empty_v(0)
         turn_tokens(2)
         quantise_tokens(1)
-        add_squares(0)
         turn_k(0)
-        turn_v(0)
         turn_tokens(3)
+        turn_v(0)
+        quantise_tokens(2)
         project_k(1)
+        project_v(1)
+        add_first_squares()
         make_factor(0)
         start_first_step()
-        quantise_tokens(2)
-        project_v(1)
         empty_k(1)
+        turn_k(1)
         square_k(1)
         empty_v(1)
-        turn_k(1)
+        turn_weights(1)
         add_squares(1)
         turn_v(1)
         project_k(2)
-        make_factor(1)
         empty_k(2)
+        make_factor(1)
+        project_v(2)
         turn_k(2)
         normalise(1)
         turn_back(1)
-        project_v(2)
         square_k(2)
-        add_squares(2)
-        normalise(0)
         copy_back(1)
         turn_kn(1)
+        add_squares(2)
         empty_v(2)
         turn_v(2)
         pack(1)
@@ -632,32 +646,32 @@ def tile_taylorsoftmaxattention_pa_kernel(tc, x, Wk, bk, Wv, bv, out_0, out_1, o
                 open_codes(g)
             multiply(step, nc.vector, True, VECTOR_PARTS)
             multiply(step, nc.gpsimd, False, GPSIMD_PARTS)
-            if g > 1 and c == 2:
+            if g > 1 and c == 3:
                 turn_square(g - 2, 0, 1)
             if step == 0:
                 quantise_tokens(3)
             quantise_v(step)
             quantise_pairs(step, slice(0, HALF))
-            if step > 1:
-                quantise_first(step - 1)
             if step == 3:
                 quantise_first(0)
-            if step == 1:
+            if step > 2:
+                quantise_first(step - 2)
+            if step == 0:
                 quantise_weights(1)
-            if c == 3 and g < GROUPS - 2:
+            if c == 2 and g < GROUPS - 2:
                 quantise_weights(g + 2)
             quantise_pairs(step, slice(HALF, PAIR_SLOTS))
             prepare(step)
             if 0 < g < GROUPS - 1 and c == 3:
-                first[g - 1] = psum_acc.tile([P, 2 * P], F32, name="first", tag="acc")
+                first[g - 1] = psum_work.tile([P, 2 * P], F32, name="first", tag="work")
                 contract_first(g - 1)
+            if g > 1 and c == 3:
+                store(g - 2, 0, 1, nc.scalar.copy)
             if g > 1 and c < 2:
                 for span, half in SPANS[3 * c : 3 * c + 3 + c]:
                     lay(g - 2, span, half, nc.scalar.copy)
             if g > 1 and c == 1:
                 lay_diagonal(g - 2)
-            if g > 1 and c == 2:
-                store(g - 2, 0, 1, nc.scalar.copy)
             if step == STEPS - 4:
                 open_chunk(0, psum_acc, "acc")
                 contract(g - 1, 0, all_blocks)
@@ -688,32 +702,35 @@ def tile_taylorsoftmaxattention_pa_kernel(tc, x, Wk, bk, Wv, bv, out_0, out_1, o
             contract(g, chunk, range(BLOCKS - 1))
         multiply(step, nc.gpsimd, False, GPSIMD_PARTS)
         multiply(step, nc.vector, True, VECTOR_PARTS)
+        turn_square(g - 2, 0, 1)
+        store(g - 2, 0, 1, nc.scalar.copy)
         quantise_v(step)
         for chunk in range(2):
             quantise_pairs(step, slice(chunk * CHUNK, (chunk + 1) * CHUNK))
             contract(g, chunk, range(BLOCKS - 1, BLOCKS))
-        turn_square(g - 1, 0, 1)
         collect(g, 0, nc.scalar.copy)
         collect(g, 1, nc.scalar.copy)
         lay(g, 16, 0, nc.scalar.copy)
         lay(g, 8, 0, nc.scalar.copy)
         lay(g, 2, 0, nc.scalar.copy)
+        quantise_first(step - 2)
         quantise_first(step - 1)
         quantise_first(step)
         contract_first(g)
         for chunk in range(2, CHUNKS):
             quantise_pairs(step, slice(chunk * CHUNK, (chunk + 1) * CHUNK))
             contract(g, chunk, range(BLOCKS - 1, BLOCKS))
-        store(g - 1, 0, 1, nc.scalar.copy)
+        turn_square(g - 1, 0, 1)
+
         collect_first(g)
         lay_diagonal(g)
-
-        collect(g, 2, nc.scalar.copy)
+        collect(g, 2, nc.vector.tensor_copy)
+        collect(g, 3, nc.vector.tensor_copy)
         lay(g, 4, 0, nc.scalar.copy)
         lay(g, 1, 0, nc.scalar.copy)
-        collect(g, 3, nc.vector.tensor_copy)
         lay(g, 16, 1, nc.vector.tensor_copy)
         lay(g, 16, 2, nc.vector.tensor_copy)
+        store(g - 1, 0, 1, nc.scalar.copy)
         nc.vector.transpose(out=small_turned[:].rearrange("p g s e -> p (g s e)"), in_=small[:].rearrange("p g s d -> p (g s d)"))
         for part in range(4):
             turn_square(g, part, 4)

@@ -125,7 +125,7 @@ def tile_taylorsoftmaxattention_pa_kernel(tc, x, Wk, bk, Wv, bv, out_0, out_1, o
         nc.gpsimd.memset(vsum_stage[:], 1.0)
         bias_cols = keep.tile([P, 2 * GROUPS], F32)
 
-        w_grouped, x_grouped = {}, {}
+        w_turned, w_grouped, x_grouped = {}, {}, {}
         k_squares, k_sums, v_sum_bank, k_feat, v_feat, k_tok, k_rows, v_tok, norms, factor = {}, {}, {}, {}, {}, {}, {}, {}, {}, {}
         kn_turned, kn_feat, kn_tok, packed, first_bf, v_bf = {}, {}, {}, {}, {}, {}
         v_codes, v_scales, first_codes, first_scales, kk_codes, kk_scales = {}, {}, {}, {}, {}, {}
@@ -133,14 +133,16 @@ def tile_taylorsoftmaxattention_pa_kernel(tc, x, Wk, bk, Wv, bv, out_0, out_1, o
         acc, first, gram, v_sums, stage, by_pair, by_square, square, turned_square = {}, {}, {}, {}, {}, {}, {}, {}, {}
 
         def turn_weights(g):
-            pool, tag = (psum_k, "k") if g == 0 else (psum_acc, "acc")
-            turned = pool.tile([P, 2, 2, P], F32, name="w_turned", tag=tag)
+            pool, tag = (psum_k, "k") if g == 0 else (psum_work, "work")
+            w_turned[g] = pool.tile([P, 2, 2, P], F32, name="w_turned", tag=tag)
             for m in range(2):
                 for u in range(2):
-                    nc.tensor.transpose(out=turned[:, m, u, :], in_=w_words[:, g, m, u * P : (u + 1) * P], identity=ident[:])
+                    nc.tensor.transpose(out=w_turned[g][:, m, u, :], in_=w_words[:, g, m, u * P : (u + 1) * P], identity=ident[:])
+
+        def group_weights(g):
             w_grouped[g] = prep.tile([P, 2, P, PACK], BF16, name="w_grouped", align_bytes=64)
             for m in range(2):
-                nc.scalar.copy(out=w_grouped[g][:, m, :, :].bitcast(F32), in_=turned[:, m, :, :].rearrange("p u o -> p o u"))
+                nc.scalar.copy(out=w_grouped[g][:, m, :, :].bitcast(F32), in_=w_turned[g][:, m, :, :].rearrange("p u o -> p o u"))
 
         def quantise_weights(g):
             for m in range(2):
@@ -560,13 +562,8 @@ def tile_taylorsoftmaxattention_pa_kernel(tc, x, Wk, bk, Wv, bv, out_0, out_1, o
             if 0 < g < GROUPS - 1:
                 open_chunk(c, psum_acc, "acc")
                 contract(g - 1, c, all_blocks)
-            if step == 2:
-                add_gram(0)
-                add_gram(1)
-            if step > 1:
-                add_gram(step)
-            if step == STEPS - 2:
-                add_gram(STEPS - 1)
+            for summed in {0: (), 1: (), 2: (0, 1), 3: (2, 3), STEPS - 2: ()}.get(step, (step,)):
+                add_gram(summed)
             if e > 1:
                 pack(e)
             if b < STEPS:
@@ -579,17 +576,18 @@ def tile_taylorsoftmaxattention_pa_kernel(tc, x, Wk, bk, Wv, bv, out_0, out_1, o
                 add_squares(a)
                 empty_v(a)
                 turn_v(a)
+            new_weights = c == 3 and g < GROUPS - 2
+            if new_weights:
+                turn_weights(g + 2)
             first_kn(e)
             first_squares(e)
             if b < STEPS:
                 copy_back(b)
                 turn_kn(b)
-            if step == STEPS - 2:
-                collect_gram(g)
+            if new_weights:
+                group_weights(g + 2)
             if 0 < g < GROUPS - 1:
                 collect(g - 1, c, nc.scalar.copy)
-            if c == 1 and g < GROUPS - 2:
-                turn_weights(g + 2)
             if step == 1:
                 normalise(0)
             if step == 2:
@@ -598,6 +596,7 @@ def tile_taylorsoftmaxattention_pa_kernel(tc, x, Wk, bk, Wv, bv, out_0, out_1, o
 
         turn_first_tokens()
         turn_weights(0)
+        group_weights(0)
         turn_biases()
         quantise_first_tokens(0)
         quantise_first_tokens(1)
@@ -612,26 +611,27 @@ def tile_taylorsoftmaxattention_pa_kernel(tc, x, Wk, bk, Wv, bv, out_0, out_1, o
         turn_k(0)
         turn_tokens(3)
         turn_v(0)
-        quantise_tokens(2)
         project_k(1)
         project_v(1)
         add_first_squares()
         make_factor(0)
         start_first_step()
+        quantise_tokens(2)
         empty_k(1)
         turn_k(1)
         square_k(1)
         empty_v(1)
         turn_weights(1)
+        group_weights(1)
         add_squares(1)
         turn_v(1)
         project_k(2)
-        empty_k(2)
         make_factor(1)
         project_v(2)
-        turn_k(2)
         normalise(1)
         turn_back(1)
+        empty_k(2)
+        turn_k(2)
         square_k(2)
         copy_back(1)
         turn_kn(1)
@@ -646,26 +646,26 @@ def tile_taylorsoftmaxattention_pa_kernel(tc, x, Wk, bk, Wv, bv, out_0, out_1, o
                 open_codes(g)
             multiply(step, nc.vector, True, VECTOR_PARTS)
             multiply(step, nc.gpsimd, False, GPSIMD_PARTS)
-            if g > 1 and c == 3:
-                turn_square(g - 2, 0, 1)
             if step == 0:
                 quantise_tokens(3)
             quantise_v(step)
             quantise_pairs(step, slice(0, HALF))
-            if step == 3:
+            if step == 4:
                 quantise_first(0)
             if step > 2:
                 quantise_first(step - 2)
             if step == 0:
                 quantise_weights(1)
-            if c == 2 and g < GROUPS - 2:
-                quantise_weights(g + 2)
+            if c == 0 and 0 < g < GROUPS - 1:
+                quantise_weights(g + 1)
+            if c == 2 and g > 1:
+                turn_square(g - 2, 0, 1)
             quantise_pairs(step, slice(HALF, PAIR_SLOTS))
             prepare(step)
             if 0 < g < GROUPS - 1 and c == 3:
                 first[g - 1] = psum_work.tile([P, 2 * P], F32, name="first", tag="work")
                 contract_first(g - 1)
-            if g > 1 and c == 3:
+            if c == 2 and g > 1:
                 store(g - 2, 0, 1, nc.scalar.copy)
             if g > 1 and c < 2:
                 for span, half in SPANS[3 * c : 3 * c + 3 + c]:
@@ -691,6 +691,9 @@ def tile_taylorsoftmaxattention_pa_kernel(tc, x, Wk, bk, Wv, bv, out_0, out_1, o
                 for span, half in SPANS:
                     lay(g - 1, span, half, nc.scalar.copy)
                 lay_diagonal(g - 1)
+                add_gram(STEPS - 2)
+                add_gram(STEPS - 1)
+                collect_gram(g)
 
         step, g = STEPS - 1, GROUPS - 1
         first[g] = psum_k.tile([P, 2 * P], F32, name="first", tag="k")
@@ -702,8 +705,8 @@ def tile_taylorsoftmaxattention_pa_kernel(tc, x, Wk, bk, Wv, bv, out_0, out_1, o
             contract(g, chunk, range(BLOCKS - 1))
         multiply(step, nc.gpsimd, False, GPSIMD_PARTS)
         multiply(step, nc.vector, True, VECTOR_PARTS)
-        turn_square(g - 2, 0, 1)
-        store(g - 2, 0, 1, nc.scalar.copy)
+        turn_square(g - 1, 0, 1)
+        store(g - 1, 0, 1, nc.scalar.copy)
         quantise_v(step)
         for chunk in range(2):
             quantise_pairs(step, slice(chunk * CHUNK, (chunk + 1) * CHUNK))
@@ -720,17 +723,15 @@ def tile_taylorsoftmaxattention_pa_kernel(tc, x, Wk, bk, Wv, bv, out_0, out_1, o
         for chunk in range(2, CHUNKS):
             quantise_pairs(step, slice(chunk * CHUNK, (chunk + 1) * CHUNK))
             contract(g, chunk, range(BLOCKS - 1, BLOCKS))
-        turn_square(g - 1, 0, 1)
 
         collect_first(g)
         lay_diagonal(g)
         collect(g, 2, nc.vector.tensor_copy)
         collect(g, 3, nc.vector.tensor_copy)
-        lay(g, 4, 0, nc.scalar.copy)
         lay(g, 1, 0, nc.scalar.copy)
+        lay(g, 4, 0, nc.vector.tensor_copy)
         lay(g, 16, 1, nc.vector.tensor_copy)
         lay(g, 16, 2, nc.vector.tensor_copy)
-        store(g - 1, 0, 1, nc.scalar.copy)
         nc.vector.transpose(out=small_turned[:].rearrange("p g s e -> p (g s e)"), in_=small[:].rearrange("p g s d -> p (g s d)"))
         for part in range(4):
             turn_square(g, part, 4)

@@ -526,6 +526,16 @@ def tile_taylorsoftmaxattention_pa_kernel(tc, x, Wk, bk, Wv, bv, out_0, out_1, o
         def lay_diagonal(g):
             nc.scalar.copy(out=square[g][:].rearrange("p (i w) -> p i w", w=DIAG)[:, :, 0], in_=by_square[g][:])
 
+        def finish_small(first_group):
+            groups = slice(first_group, first_group + 2)
+            nc.vector.transpose(
+                out=small_turned[:, groups, :, :].rearrange("p g s e -> p (g s e)"), in_=small[:, groups, :, :].rearrange("p g s d -> p (g s d)")
+            )
+            nc.scalar.copy(out=kv_stage[:, groups, 1:OUT_DIM], in_=small_turned[:, groups, 0, :])
+            nc.sync.dma_start(out=kv_rows[:, groups, :], in_=kv_stage[:, groups, :])
+            nc.scalar.copy(out=vsum_stage[:, groups, 1:OUT_DIM], in_=small_turned[:, groups, 1, :])
+            nc.sync.dma_start(out=vsum_rows[:, groups, :], in_=vsum_stage[0:P:DIM, groups, :])
+
         def turn_square(g, part, parts):
             rows = slice(part * DIM // parts, (part + 1) * DIM // parts)
             if part == 0:
@@ -652,8 +662,6 @@ def tile_taylorsoftmaxattention_pa_kernel(tc, x, Wk, bk, Wv, bv, out_0, out_1, o
             quantise_pairs(step, slice(0, HALF))
             if step == 4:
                 quantise_first(0)
-            if step > 2:
-                quantise_first(step - 2)
             if step == 0:
                 quantise_weights(1)
             if c == 0 and 0 < g < GROUPS - 1:
@@ -661,12 +669,16 @@ def tile_taylorsoftmaxattention_pa_kernel(tc, x, Wk, bk, Wv, bv, out_0, out_1, o
             if c == 2 and g > 1:
                 turn_square(g - 2, 0, 1)
             quantise_pairs(step, slice(HALF, PAIR_SLOTS))
+            if step > 2:
+                quantise_first(step - 2)
             prepare(step)
             if 0 < g < GROUPS - 1 and c == 3:
                 first[g - 1] = psum_work.tile([P, 2 * P], F32, name="first", tag="work")
                 contract_first(g - 1)
             if c == 2 and g > 1:
                 store(g - 2, 0, 1, nc.scalar.copy)
+            if step == STEPS - 3:
+                finish_small(0)
             if g > 1 and c < 2:
                 for span, half in SPANS[3 * c : 3 * c + 3 + c]:
                     lay(g - 2, span, half, nc.scalar.copy)
@@ -708,36 +720,28 @@ def tile_taylorsoftmaxattention_pa_kernel(tc, x, Wk, bk, Wv, bv, out_0, out_1, o
         turn_square(g - 1, 0, 1)
         store(g - 1, 0, 1, nc.scalar.copy)
         quantise_v(step)
-        for chunk in range(2):
-            quantise_pairs(step, slice(chunk * CHUNK, (chunk + 1) * CHUNK))
-            contract(g, chunk, range(BLOCKS - 1, BLOCKS))
-        collect(g, 0, nc.scalar.copy)
-        collect(g, 1, nc.scalar.copy)
-        lay(g, 16, 0, nc.scalar.copy)
-        lay(g, 8, 0, nc.scalar.copy)
-        lay(g, 2, 0, nc.scalar.copy)
         quantise_first(step - 2)
         quantise_first(step - 1)
         quantise_first(step)
         contract_first(g)
-        for chunk in range(2, CHUNKS):
+        for chunk in range(CHUNKS):
             quantise_pairs(step, slice(chunk * CHUNK, (chunk + 1) * CHUNK))
             contract(g, chunk, range(BLOCKS - 1, BLOCKS))
-
         collect_first(g)
+        collect(g, 0, nc.scalar.copy)
+        collect(g, 1, nc.scalar.copy)
+
+        finish_small(g - 1)
+        lay(g, 16, 0, nc.scalar.copy)
         lay_diagonal(g)
+        lay(g, 8, 0, nc.scalar.copy)
         collect(g, 2, nc.vector.tensor_copy)
         collect(g, 3, nc.vector.tensor_copy)
-        lay(g, 1, 0, nc.scalar.copy)
-        lay(g, 4, 0, nc.vector.tensor_copy)
+        for span in [2, 1, 4]:
+            lay(g, span, 0, nc.vector.tensor_copy)
         lay(g, 16, 1, nc.vector.tensor_copy)
         lay(g, 16, 2, nc.vector.tensor_copy)
-        nc.vector.transpose(out=small_turned[:].rearrange("p g s e -> p (g s e)"), in_=small[:].rearrange("p g s d -> p (g s d)"))
         for part in range(4):
             turn_square(g, part, 4)
-        nc.scalar.copy(out=kv_stage[:, :, 1:OUT_DIM], in_=small_turned[:, :, 0, :])
-        nc.sync.dma_start(out=kv_rows, in_=kv_stage[:])
-        nc.scalar.copy(out=vsum_stage[:, :, 1:OUT_DIM], in_=small_turned[:, :, 1, :])
-        nc.sync.dma_start(out=vsum_rows, in_=vsum_stage[0:P:DIM, :, :])
         for part in range(4):
             store(g, part, 4, nc.scalar.copy if part < 2 else nc.vector.tensor_copy)

from contextlib import ExitStack

import concourse.masks as masks
import concourse.mybir as mybir

F32 = mybir.dt.float32
BF16 = mybir.dt.bfloat16
U32 = mybir.dt.uint32
U8 = mybir.dt.uint8
FP8X4 = mybir.dt.float8_e4m3fn_x4
ACT = mybir.ActivationFunctionType
ALU = mybir.AluOpType

P = 128
PACK = 4
K_PASS = P * PACK
TOKENS = 2048
CHANNELS = 512
HEADS = 16
DIM = 32
OUT_DIM = DIM + 1
EPS = 1e-12
SCALE = float(DIM) ** 0.25

GROUP_HEADS = P // DIM
GROUPS = HEADS // GROUP_HEADS
BLOCKS = TOKENS // K_PASS
STEPS = GROUPS * BLOCKS
CELL = GROUP_HEADS * PACK
SPANS = [(16, 0), (16, 1), (16, 2), (8, 0), (4, 0), (2, 0), (1, 0)]
LAY_16 = [slice(0, 6), slice(6, 8), slice(8, 16)]
FIRST_PAIR = {(16, 0): 0, (8, 0): 96, (2, 0): 224, (4, 0): 256, (1, 0): 320, (16, 1): 352}
PAD = slice(336, 352)
ROWS_16 = [slice(0, 6), slice(6, 16)]
PAIRS = DIM * (DIM - 1) // 2
PAIR_SLOTS = 512
CHUNK = 128
CHUNKS = PAIR_SLOTS // CHUNK
HALF = PAIR_SLOTS // 2
VECTOR_PARTS = [(16, 0), (8, 0), (8, 1), (2, 0), (2, 1), (4, 0), (4, 1), (4, 2), (4, 3), (1, 0)]
GPSIMD_PARTS = [(16, 1)]
GRAM_COLS = P + 2
DIAG = DIM + 1

FLOPS = 2 * TOKENS * CHANNELS * 2 * HEADS * DIM + 2 * TOKENS * HEADS * (DIM * DIM * DIM + DIM * DIM)


def tile_taylorsoftmaxattention_pa_kernel(tc, x, Wk, bk, Wv, bv, out_0, out_1, out_2):
    nc = tc.nc

    x_rows = x.rearrange("b (j p) c -> p (b j) c", p=P)
    wk_rows = Wk.rearrange("(g p) c -> p g c", p=P)
    wv_rows = Wv.rearrange("(g p) c -> p g c", p=P)
    kv_mod_rows = out_0.rearrange("b (g h) a w e -> (b g) (h a) (w e)", g=GROUPS)
    kv_rows = out_1.rearrange("b (g h) d e -> (h d) (b g) e", g=GROUPS)
    vsum_rows = out_2.rearrange("b (g h) o e -> (h o) (b g) e", g=GROUPS)

    with ExitStack() as ctx:
        keep = ctx.enter_context(tc.tile_pool(name="keep", bufs=1))
        prep = ctx.enter_context(tc.tile_pool(name="prep", bufs=2))
        ahead = ctx.enter_context(tc.tile_pool(name="ahead", bufs=3))
        prod = ctx.enter_context(tc.tile_pool(name="prod", bufs=2))
        codes = ctx.enter_context(tc.tile_pool(name="codes", bufs=3))
        firsts = ctx.enter_context(tc.tile_pool(name="firsts", bufs=4))
        done = ctx.enter_context(tc.tile_pool(name="done", bufs=2))
        psum_acc = ctx.enter_context(tc.psum_pool(name="psum_acc", bufs=1))
        psum_gram = ctx.enter_context(tc.psum_pool(name="psum_gram", bufs=1))
        psum_k = ctx.enter_context(tc.psum_pool(name="psum_k", bufs=2))
        psum_work = ctx.enter_context(tc.psum_pool(name="psum_work", bufs=4))
        ctx.enter_context(tc.manual_schedule())

        w_raw = keep.tile([P, GROUPS, 2, CHANNELS], BF16)
        x_raw = prod.tile([P, TOKENS // P, CHANNELS], BF16, name="kk_codes", align_bytes=64)
        bias_rows = keep.tile([2 * GROUPS, P], BF16)
        nc.scalar.dma_start(out=bias_rows[0:GROUPS, :], in_=bk.rearrange("(g f) -> g f", g=GROUPS))
        nc.scalar.dma_start(out=bias_rows[GROUPS : 2 * GROUPS, :], in_=bv.rearrange("(g f) -> g f", g=GROUPS))
        for j in range(PACK):
            nc.sync.dma_start(out=x_raw[:, j : j + 1, :], in_=x_rows[:, j : j + 1, :])
        nc.sync.dma_start(out=w_raw[:, 0, 0, :], in_=wk_rows[:, 0, :])
        nc.sync.dma_start(out=w_raw[:, 0, 1, :], in_=wv_rows[:, 0, :])
        for c in range(1, BLOCKS):
            nc.sync.dma_start(out=x_raw[:, PACK * c : PACK * (c + 1), :], in_=x_rows[:, PACK * c : PACK * (c + 1), :])
        nc.sync.dma_start(out=w_raw[:, 1:GROUPS, 0, :], in_=wk_rows[:, 1:GROUPS, :])
        nc.sync.dma_start(out=w_raw[:, 1:GROUPS, 1, :], in_=wv_rows[:, 1:GROUPS, :])
        w_words = w_raw[:].bitcast(F32)
        x_words = x_raw[:].bitcast(F32)

        ident = keep.tile([P, P], F32)
        masks.make_identity(nc, ident[:])
        one = keep.tile([P, 1], F32)
        nc.vector.memset(one[:], 1.0)
        table_warm = keep.tile([P, 1], F32)
        nc.scalar.activation(out=table_warm[:], in_=one[:], func=ACT.Abs_reciprocal_sqrt)
        minus_floor = keep.tile([P, 1], F32)
        nc.vector.memset(minus_floor[:], -EPS * EPS)
        scaled_floor = keep.tile([P, 1], F32)
        nc.vector.memset(scaled_floor[:], EPS * EPS / (SCALE * SCALE))
        bias_square = keep.tile([P, P], F32)
        nc.vector.memset(bias_square[:], 0.0)
        head_marks = keep.tile([P, GROUP_HEADS], F32)
        nc.vector.tensor_reduce(
            out=head_marks[:], in_=ident[:].rearrange("p (h d) -> p h d", h=GROUP_HEADS), op=ALU.add, axis=mybir.AxisListType.X
        )
        ident_by_feature = keep.tile([P, P], F32)
        nc.vector.tensor_copy(
            out=ident_by_feature[:].rearrange("p (d h) -> p d h", h=GROUP_HEADS), in_=ident[:].rearrange("p (h d) -> p d h", h=GROUP_HEADS)
        )

        x_codes = keep.tile([P, TOKENS], U32, align_bytes=64)
        x_scales = keep.tile([P, TOKENS], U8, align_bytes=64)
        w_codes = keep.tile([P, GROUPS, 2 * P], U32, align_bytes=64)
        w_scales = keep.tile([P, GROUPS, 2 * P], U8, align_bytes=64)

        kn_rows = []
        for parity in range(5):
            kn_rows.append(keep.tile([P, PACK, GRAM_COLS], F32, name="kn_rows%d" % parity))
            nc.gpsimd.memset(kn_rows[parity][:, :, P:GRAM_COLS], 1.0)
        kk_bf = keep.tile([P, PAIR_SLOTS, CELL], BF16, align_bytes=64)
        nc.gpsimd.memset(kk_bf[:, PAD, :], 0.0)
        small = keep.tile([P, GROUPS, 2, DIM], F32, align_bytes=64)
        nc.gpsimd.memset(small[:], 0.0)
        small_turned = keep.tile([P, GROUPS, 2, DIM], F32, align_bytes=64)
        kv_stage = keep.tile([P, GROUPS, OUT_DIM], F32)
        vsum_stage = keep.tile([P, GROUPS, OUT_DIM], F32)
        nc.gpsimd.memset(vsum_stage[:], 1.0)
        bias_cols = keep.tile([P, 2 * GROUPS], F32)

        w_turned, w_grouped, x_grouped = {}, {}, {}
        k_squares, k_sums, v_sum_bank, k_feat, v_feat, k_tok, k_rows, v_tok, norms, factor = {}, {}, {}, {}, {}, {}, {}, {}, {}, {}
        kn_turned, kn_feat, kn_tok, packed, first_bf, v_bf = {}, {}, {}, {}, {}, {}
        v_codes, v_scales, first_codes, first_scales, kk_codes, kk_scales = {}, {}, {}, {}, {}, {}
        operands = {}
        acc, first, gram, v_sums, stage, by_pair, by_square, square, turned_square = {}, {}, {}, {}, {}, {}, {}, {}, {}

        def turn_weights(g):
            pool, tag = (psum_k, "k") if g == 0 else (psum_work, "work")
            w_turned[g] = pool.tile([P, 2, 2, P], F32, name="w_turned", tag=tag)
            for m in range(2):
                for u in range(2):
                    nc.tensor.transpose(out=w_turned[g][:, m, u, :], in_=w_words[:, g, m, u * P : (u + 1) * P], identity=ident[:])

        def group_weights(g):
            w_grouped[g] = prep.tile([P, 2, P, PACK], BF16, name="w_grouped", align_bytes=64)
            for m in range(2):
                nc.scalar.copy(out=w_grouped[g][:, m, :, :].bitcast(F32), in_=w_turned[g][:, m, :, :].rearrange("p u o -> p o u"))

        def quantise_weights(g):
            for m in range(2):
                nc.vector.quantize_mx(
                    out=w_codes[:, g, m * P : (m + 1) * P].bitcast(FP8X4),
                    scales=w_scales[:, g, m * P : (m + 1) * P],
                    in_=w_grouped[g][:, m, :, :].rearrange("p o k -> p (o k)"),
                )

        def turn_biases():
            nc.vector.tensor_copy(out=bias_square[0 : 2 * GROUPS, :], in_=bias_rows[:])
            bias_turned = psum_k.tile([P, P], F32, name="bias_turned", tag="k")
            nc.tensor.transpose(out=bias_turned[:], in_=bias_square[:], identity=ident[:])
            nc.scalar.copy(out=bias_cols[:, 0:GROUPS], in_=bias_turned[:, 0:GROUPS])
            nc.scalar.mul(out=bias_cols[:, GROUPS : 2 * GROUPS], in_=bias_turned[:, GROUPS : 2 * GROUPS], mul=1.0 / TOKENS)

        def turn_first_tokens():
            x_grouped[0] = ahead.tile([P, K_PASS, PACK], BF16, name="x_grouped", align_bytes=64)
            pairs = x_grouped[0][:].bitcast(F32).rearrange("p (j n) u -> p j n u", j=PACK)
            for j in range(PACK):
                pool, tag = (psum_acc, "acc") if j == 0 else (psum_work, "work")
                turned = pool.tile([P, 2, P], F32, name="x_first_turned", tag=tag)
                for u in range(2):
                    nc.tensor.transpose(out=turned[:, u, :], in_=x_words[:, j, u * P : (u + 1) * P], identity=ident[:])
                copy = nc.vector.tensor_copy if j % 2 == 0 else nc.scalar.copy
                copy(out=pairs[:, j, :, :], in_=turned[:].rearrange("p u n -> p n u"))

        def quantise_first_tokens(half):
            tokens = slice(half * K_PASS // 2, (half + 1) * K_PASS // 2)
            nc.vector.quantize_mx(
                out=x_codes[:, tokens].bitcast(FP8X4),
                scales=x_scales[:, tokens],
                in_=x_grouped[0][:, tokens, :].rearrange("p n k -> p (n k)"),
            )

        def turn_tokens(c):
            x_grouped[c] = ahead.tile([P, K_PASS, PACK], BF16, name="x_grouped", align_bytes=64)
            pairs = x_grouped[c][:].bitcast(F32).rearrange("p (j n) u -> p j n u", j=PACK)
            for half in range(2):
                pool, tag = [(psum_acc, "acc"), (psum_k, "k"), (psum_gram, "gram"), (psum_work, "work"), (psum_acc, "acc"), (psum_k, "k")][2 * c - 2 + half]
                turned = pool.tile([P, 2, 2, P], F32, name="x_turned", tag=tag)
                for j in range(2):
                    for u in range(2):
                        nc.tensor.transpose(
                            out=turned[:, j, u, :],
                            in_=x_words[:, PACK * c + 2 * half + j, u * P : (u + 1) * P],
                            identity=ident[:],
                        )
                nc.vector.tensor_copy(out=pairs[:, 2 * half : 2 * half + 2, :, :], in_=turned[:].rearrange("p j u n -> p j n u"))

        def quantise_tokens(c):
            block = slice(c * K_PASS, (c + 1) * K_PASS)
            nc.vector.quantize_mx(
                out=x_codes[:, block].bitcast(FP8X4),
                scales=x_scales[:, block],
                in_=x_grouped[c][:].rearrange("p n k -> p (n k)"),
            )

        def project(sums, m, step):
            g, c = divmod(step, BLOCKS)
            block = slice(c * K_PASS, (c + 1) * K_PASS)
            nc.tensor.matmul_mx(
                out=sums,
                lhsT=w_codes[:, g, m * P : (m + 1) * P].bitcast(FP8X4),
                lhsT_scale=w_scales[:, g, m * P : (m + 1) * P],
                rhs=x_codes[:, block].bitcast(FP8X4),
                rhs_scale=x_scales[:, block],
                start=True,
                stop=True,
            )

        def project_k(step):
            k_sums[step] = psum_work.tile([P, K_PASS], F32, name="k_sums", tag="work")
            project(k_sums[step][:], 0, step)

        def project_v(step):
            v_sum_bank[step] = psum_work.tile([P, K_PASS], F32, name="v_sum_bank", tag="work")
            project(v_sum_bank[step][:], 1, step)

        def empty_k(step):
            g = step // BLOCKS
            k_feat[step] = prep.tile([P, K_PASS], F32, name="k_feat")
            nc.scalar.activation(
                out=k_feat[step][:].rearrange("p (u e n) -> p u e n", u=2, e=2),
                in_=k_sums[step][:].rearrange("p (u n e) -> p u e n", u=2, e=2),
                func=ACT.Identity,
                bias=bias_cols[:, g : g + 1],
                scale=1.0,
            )

        def square_k(step):
            g = step // BLOCKS
            k_squares[step] = prep.tile([P, K_PASS], F32, name="k_squares")
            nc.scalar.activation(
                out=k_squares[step][:].rearrange("p (u e n) -> p u e n", u=2, e=2),
                in_=k_sums[step][:].rearrange("p (u n e) -> p u e n", u=2, e=2),
                func=ACT.Square,
                bias=bias_cols[:, g : g + 1],
                scale=1.0,
            )

        def add_squares(step):
            bank = psum_work.tile([P, PACK, P], F32, name="bank", tag="work")
            v_tok[step] = bank[:, 0:2, :]
            norms[step] = bank[:, 2, 0:CELL].rearrange("p (t h) -> p t h", h=GROUP_HEADS)
            for t in range(PACK):
                nc.tensor.matmul(
                    out=norms[step][:, t, :],
                    lhsT=k_squares[step][:, t * P : (t + 1) * P],
                    rhs=head_marks[:],
                    start=True,
                    stop=True,
                )

        def empty_v(step):
            g, c = divmod(step, BLOCKS)
            if c == 0:
                v_sums[g] = ahead.tile([P, BLOCKS], F32, name="v_sums")
            v_feat[step] = prep.tile([P, K_PASS], BF16, name="v_feat")
            nc.scalar.activation(
                out=v_feat[step][:],
                in_=v_sum_bank[step][:],
                func=ACT.Identity,
                bias=bias_cols[:, GROUPS + g : GROUPS + g + 1],
                scale=1.0 / TOKENS,
                accum_out=v_sums[g][:, c : c + 1],
            )

        def turn_k(step):
            if step == 0:
                k_tok[step] = psum_k.tile([P, P, PACK], F32, name="k_tok", tag="k")
                for t in range(PACK):
                    nc.tensor.transpose(out=k_tok[step][:, :, t], in_=k_feat[step][:, t * P : (t + 1) * P], identity=ident_by_feature[:])
                k_rows[step] = k_tok[step][:].rearrange("p (d h) t -> p t h d", h=GROUP_HEADS)
                return
            k_tok[step] = psum_work.tile([P, PACK, P], F32, name="k_tok", tag="work")
            for t in range(PACK):
                nc.tensor.transpose(out=k_tok[step][:, t, :], in_=k_feat[step][:, t * P : (t + 1) * P], identity=ident[:])
            k_rows[step] = k_tok[step][:].rearrange("p t (h d) -> p t h d", h=GROUP_HEADS)

        def turn_v(step):
            if step == 0:
                first_bank = psum_work.tile([P, 2, P], F32, name="first_bank", tag="work")
                v_tok[0] = first_bank[:]
            v_words = v_feat[step][:].bitcast(F32)
            for u in range(2):
                nc.tensor.transpose(out=v_tok[step][:, u, :], in_=v_words[:, u * P : (u + 1) * P], identity=ident[:])

        def add_first_squares():
            squares = ahead.tile([P, CELL, DIM], F32, name="packed")
            norms_by_cell = keep.tile([P, CELL], F32)
            k_cells = by_cell(k_tok[0])
            for x in range(CELL):
                nc.scalar.activation(out=squares[:, x, :], in_=k_cells[:, :, x], func=ACT.Square, accum_out=norms_by_cell[:, x : x + 1])
            norms[0] = norms_by_cell[:].rearrange("p (h t) -> p t h", h=GROUP_HEADS)

        def make_factor(step):
            above_floor = prep.tile([P, CELL], F32)
            nc.scalar.activation(
                out=above_floor[:].rearrange("p (h t) -> p t h", h=GROUP_HEADS),
                in_=norms[step],
                func=ACT.Relu,
                bias=minus_floor[:],
                scale=1.0,
            )
            v_bf[step] = ahead.tile([P, P, PACK], BF16, name="v_bf", align_bytes=64)
            nc.scalar.copy(out=v_bf[step][:].bitcast(F32), in_=v_tok[step].rearrange("p u f -> p f u"))
            factor[step] = ahead.tile([P, CELL], F32, name="factor")
            nc.scalar.activation(
                out=factor[step][:],
                in_=above_floor[:],
                func=ACT.Abs_reciprocal_sqrt,
                bias=scaled_floor[:],
                scale=1.0 / (SCALE * SCALE),
            )

        def by_cell(tile):
            return tile[:].rearrange("p (d h) t -> p d (h t)", h=GROUP_HEADS)

        def start_first_step():
            packed[0] = ahead.tile([P, DIM, CELL], F32, name="packed")
            nc.vector.tensor_copy(out=packed[0][:], in_=by_cell(k_tok[0]))
            k_rows[0] = packed[0][:].rearrange("p d (h t) -> p t h d", h=GROUP_HEADS)
            factor_squared = keep.tile([P, CELL], F32)
            nc.scalar.activation(out=factor_squared[:], in_=factor[0][:], func=ACT.Square)
            w_packed = ahead.tile([P, DIM, CELL], F32, name="packed")
            nc.vector.tensor_tensor(
                out=w_packed[:],
                in0=by_cell(k_tok[0]),
                in1=factor_squared[:].unsqueeze(1).to_broadcast([P, DIM, CELL]),
                op=ALU.mult,
            )
            operands[0] = by_cell(k_tok[0]), packed[0][:], w_packed[:]

        def turn_back(step):
            kn_turned[step] = psum_work.tile([P, PACK, P], F32, name="kn_turned", tag="work")
            for t in range(PACK):
                nc.tensor.transpose(out=kn_turned[step][:, t, :], in_=kn_rows[step % 5][:, t, 0:P], identity=ident[:])

        def copy_back(step):
            kn_feat[step] = prep.tile([P, PACK, P], F32, name="kn_feat")
            nc.scalar.copy(out=kn_feat[step][:], in_=kn_turned[step][:])

        def turn_kn(step):
            kn_tok[step] = psum_k.tile([P, P, PACK], F32, name="kn_tok", tag="k")
            for t in range(PACK):
                nc.tensor.transpose(out=kn_tok[step][:, :, t], in_=kn_feat[step][:, t, :], identity=ident_by_feature[:])

        def pack(step):
            packed[step] = ahead.tile([P, DIM, CELL], F32, name="packed")
            nc.scalar.copy(out=packed[step][:], in_=by_cell(kn_tok[step]))
            operands[step] = by_cell(kn_tok[step]), packed[step][:], packed[step][:]

        def normalise(step):
            rows = kn_rows[step % 5]
            for t in range(PACK):
                for h in range(GROUP_HEADS):
                    nc.scalar.activation(
                        out=rows[:, t, h * DIM : (h + 1) * DIM],
                        in_=k_rows[step][:, t, h, :],
                        func=ACT.Copy,
                        scale=factor[step][:, h * PACK + t : h * PACK + t + 1],
                    )

        def first_operands(step):
            if step == 0:
                kn = kn_rows[0][:, :, 0:P].rearrange("p t (h d) -> p d h t", h=GROUP_HEADS)
                return kn, first_bf[step][:].rearrange("p s d (h t) -> p s d h t", h=GROUP_HEADS)
            return packed[step][:], first_bf[step][:]

        def first_kn(step):
            first_bf[step] = firsts.tile([P, 2, DIM, CELL], BF16, name="first_bf", align_bytes=64)
            kn, cells = first_operands(step)
            nc.scalar.copy(out=cells[:, 0], in_=kn)

        def first_squares(step):
            kn, cells = first_operands(step)
            nc.scalar.activation(out=cells[:, 1], in_=kn, func=ACT.Square)

        def add_gram(step):
            g, c = divmod(step, BLOCKS)
            rows = kn_rows[step % 5]
            if c == 0:
                gram[g] = psum_gram.tile([P, GRAM_COLS], F32, name="gram", tag="gram")
            for t in range(PACK):
                nc.tensor.matmul(
                    out=gram[g][:],
                    lhsT=rows[:, t, 0:P],
                    rhs=rows[:, t, :],
                    start=(c == 0 and t == 0),
                    stop=(c == BLOCKS - 1 and t == PACK - 1),
                )

        def collect_gram(g):
            stage[g] = ahead.tile([P, DIM, OUT_DIM], F32, name="stage")
            for h in range(GROUP_HEADS):
                rows = slice(h * DIM, (h + 1) * DIM)
                nc.scalar.mul(out=stage[g][rows, :, 0], in_=gram[g][rows, h * DIM : (h + 1) * DIM], mul=1.0 / TOKENS)
            nc.scalar.mul(out=kv_stage[:, g, 0:1], in_=gram[g][:, P : P + 1], mul=1.0 / TOKENS)

        def multiply(step, engine, engine_reads_psum, parts):
            w = operands[step][2]
            k = operands[step][0 if engine_reads_psum else 1]
            for span, part in parts:
                if span == 16:
                    rows = ROWS_16[part]
                    shape = [P, rows.stop - rows.start, 16, CELL]
                    slot = FIRST_PAIR[16, part]
                    left = k[:, rows, :].unsqueeze(2)
                    right = w[:, 16:32, :].unsqueeze(1)
                elif span == 8:
                    shape = [P, span, span, CELL]
                    slot = FIRST_PAIR[span, 0] + part * span * span
                    low = part * 2 * span
                    left = k[:, low : low + span, :].unsqueeze(2)
                    right = w[:, low + span : low + 2 * span, :].unsqueeze(1)
                else:
                    shape = [P, DIM // (2 * span), span, CELL]
                    slot = FIRST_PAIR[span, 0] + part * (DIM // 2)
                    left = k.rearrange("p (b r) x -> p b r x", r=2 * span)[:, :, part, :].unsqueeze(2)
                    right = w.rearrange("p (b r) x -> p b r x", r=2 * span)[:, :, span : 2 * span, :]
                out = kk_bf[:, slot : slot + shape[1] * span, :].rearrange("p (a j) x -> p a j x", j=span)
                engine.tensor_tensor(out=out, in0=left.to_broadcast(shape), in1=right.to_broadcast(shape), op=ALU.mult)

        def open_codes(g):
            v_codes[g] = codes.tile([P, BLOCKS, P], U32, name="v_codes", align_bytes=64)
            v_scales[g] = codes.tile([P, BLOCKS, P], U8, name="v_scales", align_bytes=64)
            first_codes[g] = codes.tile([P, BLOCKS, 2 * P], U32, name="first_codes", align_bytes=64)
            first_scales[g] = codes.tile([P, BLOCKS, 2 * P], U8, name="first_scales", align_bytes=64)
            kk_codes[g] = prod.tile([P, BLOCKS, PAIR_SLOTS * GROUP_HEADS], U32, name="kk_codes", align_bytes=64)
            kk_scales[g] = prod.tile([P, BLOCKS, PAIR_SLOTS * GROUP_HEADS], U8, name="kk_scales", align_bytes=64)

        def quantise_v(step):
            g, c = divmod(step, BLOCKS)
            nc.vector.quantize_mx(
                out=v_codes[g][:, c, :].bitcast(FP8X4), scales=v_scales[g][:, c, :], in_=v_bf[step][:].rearrange("p f t -> p (f t)")
            )

        def quantise_first(step):
            g, c = divmod(step, BLOCKS)
            nc.vector.quantize_mx(
                out=first_codes[g][:, c, :].bitcast(FP8X4),
                scales=first_scales[g][:, c, :],
                in_=first_bf[step][:].rearrange("p s d x -> p (s d x)"),
            )

        def quantise_pairs(step, pairs):
            g, c = divmod(step, BLOCKS)
            columns = slice(pairs.start * GROUP_HEADS, pairs.stop * GROUP_HEADS)
            nc.vector.quantize_mx(
                out=kk_codes[g][:, c, columns].bitcast(FP8X4),
                scales=kk_scales[g][:, c, columns],
                in_=kk_bf[:, pairs, :].rearrange("p q x -> p (q x)"),
            )

        def contract_first(g):
            for b in range(BLOCKS):
                nc.tensor.matmul_mx(
                    out=first[g][:],
                    lhsT=v_codes[g][:, b, :].bitcast(FP8X4),
                    lhsT_scale=v_scales[g][:, b, :],
                    rhs=first_codes[g][:, b, :].bitcast(FP8X4),
                    rhs_scale=first_scales[g][:, b, :],
                    start=(b == 0),
                    stop=(b == BLOCKS - 1),
                )

        def contract(g, chunk, blocks):
            columns = slice(chunk * CHUNK * GROUP_HEADS, (chunk + 1) * CHUNK * GROUP_HEADS)
            for b in blocks:
                nc.tensor.matmul_mx(
                    out=acc[chunk][:],
                    lhsT=v_codes[g][:, b, :].bitcast(FP8X4),
                    lhsT_scale=v_scales[g][:, b, :],
                    rhs=kk_codes[g][:, b, columns].bitcast(FP8X4),
                    rhs_scale=kk_scales[g][:, b, columns],
                    start=(b == 0),
                    stop=(b == BLOCKS - 1),
                )

        def collect_first(g):
            by_square[g] = done.tile([P, DIM], F32, name="by_square")
            sums = first[g][:].rearrange("p (s i m) -> p s m i", s=2, m=GROUP_HEADS)
            for h in range(GROUP_HEADS):
                rows = slice(h * DIM, (h + 1) * DIM)
                nc.scalar.copy(out=small[rows, g, 0, :], in_=sums[rows, 0, h, :])
                nc.scalar.copy(out=by_square[g][rows, :], in_=sums[rows, 1, h, :])
            total = done.tile([P, BLOCKS], F32)
            nc.scalar.activation(out=total[:], in_=v_sums[g][:], func=ACT.Copy, accum_out=small[:, g, 1, 0:1])

        def collect(g, chunk, copy):
            if chunk == 0:
                by_pair[g] = done.tile([P, PAIR_SLOTS], F32, name="by_pair")
            sums = acc[chunk][:].rearrange("p (q m) -> p m q", m=GROUP_HEADS)
            for h in range(GROUP_HEADS):
                rows = slice(h * DIM, (h + 1) * DIM)
                copy(out=by_pair[g][rows, chunk * CHUNK : (chunk + 1) * CHUNK], in_=sums[rows, h, :])

        def lay(g, span, half, copy):
            if (span, half) == (16, 0):
                square[g] = done.tile([P, DIM * DIAG], F32, name="square", align_bytes=64)
            if span == 16:
                rows = LAY_16[half]
                part = 0 if rows.start < ROWS_16[1].start else 1
                pair = FIRST_PAIR[16, part] + 16 * (rows.start - ROWS_16[part].start)
                count = rows.stop - rows.start
                sums = by_pair[g][:, pair : pair + 16 * count].rearrange("p (i j) -> p i j", i=count)
                cells = square[g][:].rearrange("p (i r) -> p i r", r=DIM)
                copy(out=cells[:, rows, 16:32], in_=sums)
                copy(out=cells[:, 16:32, rows], in_=sums.rearrange("p i j -> p j i"))
                return
            spans = DIM // (2 * span)
            order = "p (b i j) -> p b i j" if span >= 8 else "p (i b j) -> p b i j"
            sums = by_pair[g][:, FIRST_PAIR[span, 0] : FIRST_PAIR[span, 0] + DIM // 2 * span].rearrange(order, b=spans, i=span)
            cells = square[g][:].rearrange("p (b w) -> p b w", b=spans)
            upper = cells[:, :, span : span + span * DIM].rearrange("p b (i r) -> p b i r", r=DIM)[:, :, :, 0:span]
            lower = cells[:, :, span * DIM : 2 * span * DIM].rearrange("p b (j r) -> p b j r", r=DIM)[:, :, :, 0:span]
            copy(out=upper, in_=sums)
            copy(out=lower, in_=sums.rearrange("p b i j -> p b j i"))

        def lay_diagonal(g):
            nc.scalar.copy(out=square[g][:].rearrange("p (i w) -> p i w", w=DIAG)[:, :, 0], in_=by_square[g][:])

        def finish_small(first_group):
            groups = slice(first_group, first_group + 2)
            nc.vector.transpose(
                out=small_turned[:, groups, :, :].rearrange("p g s e -> p (g s e)"), in_=small[:, groups, :, :].rearrange("p g s d -> p (g s d)")
            )
            nc.scalar.copy(out=kv_stage[:, groups, 1:OUT_DIM], in_=small_turned[:, groups, 0, :])
            nc.sync.dma_start(out=kv_rows[:, groups, :], in_=kv_stage[:, groups, :])
            nc.scalar.copy(out=vsum_stage[:, groups, 1:OUT_DIM], in_=small_turned[:, groups, 1, :])
            nc.sync.dma_start(out=vsum_rows[:, groups, :], in_=vsum_stage[0:P:DIM, groups, :])

        def turn_square(g, part, parts):
            rows = slice(part * DIM // parts, (part + 1) * DIM // parts)
            if part == 0:
                turned_square[g] = done.tile([P, DIM, DIM], F32, name="turned_square", align_bytes=64)
            nc.vector.transpose(
                out=turned_square[g][:, rows, :].rearrange("p w e -> p (w e)"), in_=square[g][:, rows.start * DIM : rows.stop * DIM]
            )

        def store(g, part, parts, copy):
            rows = slice(part * DIM // parts, (part + 1) * DIM // parts)
            copy(out=stage[g][:, rows, 1:OUT_DIM], in_=turned_square[g][:, rows, :])
            nc.sync.dma_start(
                out=kv_mod_rows[g][:, rows.start * OUT_DIM : rows.stop * OUT_DIM], in_=stage[g][:, rows, :].rearrange("p w e -> p (w e)")
            )

        all_blocks = range(BLOCKS)

        def open_chunk(chunk, pool, tag):
            acc[chunk] = pool.tile([P, CHUNK * GROUP_HEADS], F32, name="acc", tag=tag)

        def prepare(step):
            a, b, e = step + 3, step + 2, step + 1
            g, c = divmod(step, BLOCKS)
            if a < STEPS:
                project_k(a)
            if b < STEPS:
                make_factor(b)
            if g > 1 and c == 0:
                collect_first(g - 2)
            if g > 0 and c == 0:
                collect_gram(g - 1)
            if a < STEPS:
                project_v(a)
            if 0 < g < GROUPS - 1:
                open_chunk(c, psum_acc, "acc")
                contract(g - 1, c, all_blocks)
            for summed in {0: (), 1: (), 2: (0, 1), 3: (2, 3), STEPS - 2: ()}.get(step, (step,)):
                add_gram(summed)
            if e > 1:
                pack(e)
            if b < STEPS:
                normalise(b)
                turn_back(b)
            if a < STEPS:
                empty_k(a)
                turn_k(a)
                square_k(a)
                add_squares(a)
                empty_v(a)
                turn_v(a)
            new_weights = c == 3 and g < GROUPS - 2
            if new_weights:
                turn_weights(g + 2)
            first_kn(e)
            first_squares(e)
            if b < STEPS:
                copy_back(b)
                turn_kn(b)
            if new_weights:
                group_weights(g + 2)
            if 0 < g < GROUPS - 1:
                collect(g - 1, c, nc.scalar.copy)
            if step == 1:
                normalise(0)
            if step == 2:
                first_kn(0)
                first_squares(0)

        turn_first_tokens()
        turn_weights(0)
        group_weights(0)
        turn_biases()
        quantise_first_tokens(0)
        quantise_first_tokens(1)
        quantise_weights(0)
        turn_tokens(1)
        project_k(0)
        project_v(0)
        empty_k(0)
        empty_v(0)
        turn_tokens(2)
        quantise_tokens(1)
        turn_k(0)
        turn_tokens(3)
        turn_v(0)
        project_k(1)
        project_v(1)
        add_first_squares()
        make_factor(0)
        start_first_step()
        quantise_tokens(2)
        empty_k(1)
        turn_k(1)
        square_k(1)
        empty_v(1)
        turn_weights(1)
        group_weights(1)
        add_squares(1)
        turn_v(1)
        project_k(2)
        make_factor(1)
        project_v(2)
        normalise(1)
        turn_back(1)
        empty_k(2)
        turn_k(2)
        square_k(2)
        copy_back(1)
        turn_kn(1)
        add_squares(2)
        empty_v(2)
        turn_v(2)
        pack(1)

        for step in range(STEPS - 1):
            g, c = divmod(step, BLOCKS)
            if c == 0:
                open_codes(g)
            multiply(step, nc.vector, True, VECTOR_PARTS)
            multiply(step, nc.gpsimd, False, GPSIMD_PARTS)
            if step == 0:
                quantise_tokens(3)
            quantise_v(step)
            quantise_pairs(step, slice(0, HALF))
            if step == 4:
                quantise_first(0)
            if step == 0:
                quantise_weights(1)
            if c == 0 and 0 < g < GROUPS - 1:
                quantise_weights(g + 1)
            if c == 2 and g > 1:
                turn_square(g - 2, 0, 1)
            quantise_pairs(step, slice(HALF, PAIR_SLOTS))
            if step > 2:
                quantise_first(step - 2)
            prepare(step)
            if 0 < g < GROUPS - 1 and c == 3:
                first[g - 1] = psum_work.tile([P, 2 * P], F32, name="first", tag="work")
                contract_first(g - 1)
            if c == 2 and g > 1:
                store(g - 2, 0, 1, nc.scalar.copy)
            if step == STEPS - 3:
                finish_small(0)
            if g > 1 and c < 2:
                for span, half in SPANS[3 * c : 3 * c + 3 + c]:
                    lay(g - 2, span, half, nc.scalar.copy)
            if g > 1 and c == 1:
                lay_diagonal(g - 2)
            if step == STEPS - 4:
                open_chunk(0, psum_acc, "acc")
                contract(g - 1, 0, all_blocks)
                collect(g - 1, 0, nc.scalar.copy)
            if step == STEPS - 3:
                for chunk in (1, 2):
                    open_chunk(chunk, psum_work, "work")
                    contract(g - 1, chunk, all_blocks)
                    collect(g - 1, chunk, nc.scalar.copy)
            if step == STEPS - 2:
                first[g - 1] = psum_acc.tile([P, 2 * P], F32, name="first", tag="acc")
                contract_first(g - 1)
                open_chunk(3, psum_work, "work")
                contract(g - 1, 3, all_blocks)
                collect_first(g - 1)
                collect(g - 1, 3, nc.scalar.copy)
                for span, half in SPANS:
                    lay(g - 1, span, half, nc.scalar.copy)
                lay_diagonal(g - 1)
                add_gram(STEPS - 2)
                add_gram(STEPS - 1)
                collect_gram(g)

        step, g = STEPS - 1, GROUPS - 1
        first[g] = psum_k.tile([P, 2 * P], F32, name="first", tag="k")
        for chunk in range(CHUNKS):
            if chunk == 0:
                open_chunk(chunk, psum_acc, "acc")
            else:
                open_chunk(chunk, psum_work, "work")
            contract(g, chunk, range(BLOCKS - 1))
        multiply(step, nc.gpsimd, False, GPSIMD_PARTS)
        multiply(step, nc.vector, True, VECTOR_PARTS)
        turn_square(g - 1, 0, 1)
        store(g - 1, 0, 1, nc.scalar.copy)
        quantise_v(step)
        quantise_first(step - 2)
        quantise_first(step - 1)
        quantise_first(step)
        contract_first(g)
        for chunk in range(CHUNKS):
            quantise_pairs(step, slice(chunk * CHUNK, (chunk + 1) * CHUNK))
            contract(g, chunk, range(BLOCKS - 1, BLOCKS))
        collect_first(g)
        collect(g, 0, nc.scalar.copy)
        collect(g, 1, nc.scalar.copy)

        finish_small(g - 1)
        lay(g, 16, 0, nc.scalar.copy)
        lay_diagonal(g)
        lay(g, 8, 0, nc.scalar.copy)
        collect(g, 2, nc.vector.tensor_copy)
        collect(g, 3, nc.vector.tensor_copy)
        for span in [2, 1, 4]:
            lay(g, span, 0, nc.vector.tensor_copy)
        lay(g, 16, 1, nc.vector.tensor_copy)
        lay(g, 16, 2, nc.vector.tensor_copy)
        for part in range(4):
            turn_square(g, part, 4)
        for part in range(4):
            store(g, part, 4, nc.scalar.copy if part < 2 else nc.vector.tensor_copy)
